import numpy as np
import ml_dtypes


def mxq(x, axis, fmt="e4m3"):
    dtype, down = {"e4m3": (ml_dtypes.float8_e4m3fn, 7), "e5m2": (ml_dtypes.float8_e5m2, 14)}[fmt]
    v = np.moveaxis(np.asarray(x, np.float32).astype(ml_dtypes.bfloat16).astype(np.float64), axis, -1)
    blocks = v.reshape(v.shape[:-1] + (-1, 32))
    amax = np.abs(blocks).max(-1, keepdims=True)
    byte = np.maximum(np.where(amax > 0, np.frexp(amax)[1] - 1 + 127, 0) - down, 1)
    scale = np.exp2(byte - 127.0)
    codes = (blocks / scale).astype(np.float32).astype(dtype).astype(np.float64)
    return np.moveaxis((codes * scale).reshape(v.shape), -1, axis)


WIDE = False


def mx_kscale(k):
    if not WIDE:
        return np.ones(k)
    levels = np.array([18, -18])
    if k % 512:
        return np.exp2(np.random.permutation(np.resize(levels, k // 32))).repeat(32)
    a = np.empty((k // 512, 16))
    for p in range(k // 512):
        a[p, :8] = np.random.permutation(np.resize(levels, 8))
        for g in range(8):
            far = levels[np.abs(levels - a[p, g]) >= 10]
            a[p, g + 8] = far[np.random.randint(len(far))]
    return np.exp2(a.ravel()).repeat(32)


BF16 = ml_dtypes.bfloat16


def bf(x):
    return np.asarray(x, np.float32).astype(BF16)


def f64(x):
    return np.asarray(x).astype(np.float64)


B, T, P, F, G, R, C, O = 256, 8, 1024, 512, 512, 128, 4, 10
N = B * T


def setup_inputs():
    s = np.repeat(mx_kscale(N)[::T], T)[:, None]
    u = mx_kscale(F)
    v = mx_kscale(G)
    r0 = np.concatenate([np.full(P + F, 1.0 / np.sqrt(P + F)), [0.1]])[:, None]
    r1 = np.concatenate([np.full(G, 1.5 / np.sqrt(G)), [0.1]])[:, None]
    p0 = bf(np.random.standard_normal((N, P)))
    x0 = bf(np.maximum(np.random.standard_normal((N, F)), 0.0) * 0.9)
    col0 = bf(np.array([float(np.random.randint(1, C))]))
    w0_0 = bf(np.random.standard_normal((P + F + 1, G)) * r0)
    b0 = bf(np.random.standard_normal(G) * 0.2)
    w1_0 = bf(np.random.standard_normal((G + 1, F)) * r1)
    b1 = bf(np.random.standard_normal(F) * 0.2)
    c, w0, w1 = f64(col0), f64(w0_0), f64(w1_0)
    a = np.concatenate([f64(p0), f64(x0)], axis=1) @ w0[:P + F] + c * w0[P + F] + f64(b0)
    h = np.roll(np.maximum(a, 0.0).reshape(B, T * G), -R, axis=1).reshape(N, G)
    y = h @ w1[:G] + c * w1[G] + f64(b1)
    gy = np.random.standard_normal((N, F)) * 2.0 * np.exp2(np.random.randint(-6, 1, (N, 1))) / s * u
    return {"primary_input": bf(f64(p0) * s).reshape(B, T * P),
            "prev": bf(f64(x0) * s).reshape(B, T * F),
            "col": bf(f64(col0) * s.min()),
            "W0": bf(w0 / v),
            "b0": b0,
            "W1": bf(w1 * np.concatenate([np.roll(v, -R), [1.0]])[:, None] / u),
            "b1": b1,
            "a": np.asarray(a.reshape(B, T, G), np.float32),
            "y": np.asarray(y.reshape(B, T, F), np.float32),
            "grad_out": bf(np.roll(gy.reshape(B, T * F), R, axis=1))}


def reference(primary_input, prev, col, W0, b0, W1, b1, a, y, grad_out):
    w0, w1, c = f64(W0), f64(W1), f64(col)
    inp = np.concatenate([f64(primary_input).reshape(N, P), f64(prev).reshape(N, F)], axis=1)
    dy = np.roll(f64(grad_out), -R, axis=1).reshape(N, F) * (f64(y).reshape(N, F) > 0.0)
    dh = mxq(dy, 1, "e5m2") @ mxq(w1[:G], 1, "e4m3").T
    da = np.roll(dh.reshape(B, T * G), R, axis=1).reshape(N, G) * (f64(a).reshape(N, G) > 0.0)
    dp = mxq(da, 1, "e5m2") @ mxq(w0[:P], 1, "e4m3").T
    dw = mxq(inp, 0, "e4m3").T @ mxq(da, 0, "e5m2")
    last = c * da.sum(axis=0)
    return dp.reshape(B, T * P), np.concatenate([dw, last[None, :]], axis=0)

@@ -1,0 +1,450 @@
+from contextlib import ExitStack
+
+import concourse.mybir as mybir
+from concourse.masks import make_identity
+
+B, T, P_IN, F, G = 256, 8, 1024, 512, 512
+N = B * T
+C_OUT = P_IN + F
+FLOPS = 2 * N * F * G + 2 * N * G * P_IN + 2 * N * C_OUT * G
+BYTES = 2 * (N * P_IN + N * F + 1 + P_IN * G + G * F + N * F) + 4 * (N * G + N * F) + 4 * (N * P_IN + (C_OUT + 1) * G)
+
+F32 = mybir.dt.float32
+BF16 = mybir.dt.bfloat16
+U32 = mybir.dt.uint32
+U8 = mybir.dt.uint8
+E4 = mybir.dt.float8_e4m3fn_x4
+E5 = mybir.dt.float8_e5m2_x4
+ALU = mybir.AluOpType
+
+PART = 128
+PACK = 4
+GROUP = PART * PACK
+GROUPS = N // GROUP
+ROLL = 128
+W = (8, 8, 3, 2, 1, 1, 1, 2)
+
+
+def tile_capsuleneuralnetwork_pa_v_kernel(
+    tc, primary_input, prev, col, W0, b0, W1, b1, a, y, grad_out, out_0, out_1
+):
+    nc = tc.nc
+
+    p_dram = primary_input.rearrange("b (t w) -> (b t) w", t=T).rearrange("(g p j) w -> g p j w", p=PART, j=PACK)
+    x_dram = prev.rearrange("b (t w) -> (b t) w", t=T).rearrange("(g p j) w -> g p j w", p=PART, j=PACK)
+    a_dram = a.rearrange("b t w -> (b t) w").rearrange("(g p j) w -> g p j w", p=PART, j=PACK)
+    y_dram = y.rearrange("b t w -> (b t) w").rearrange("(g p j) w -> g p j w", p=PART, j=PACK)
+    o_dram = out_0.rearrange("b (t w) -> (b t) w", t=T).rearrange("(g p j) w -> g p j w", p=PART, j=PACK)
+    gr_rows = grad_out.rearrange("b (h w) -> (b h) w", h=2)
+    gr_half = grad_out.rearrange("(g b) (h w) -> h b g w", b=PART // 2, h=2)
+
+    with ExitStack() as ctx:
+        pool = ctx.enter_context(tc.tile_pool(name="pool", bufs=1))
+        psum = ctx.enter_context(tc.psum_pool(name="psum", bufs=1))
+
+        def bank(tag):
+            return psum.tile([PART, 512], F32, name=tag, tag=tag, bufs={"tp": 2, "dh": 3, "acc": 2, "c": 1}[tag])
+
+        ident = pool.tile([PART, PART], F32, name="ident")
+        swap = pool.tile([PART, PART], F32, name="swap")
+        make_identity(nc, ident[:])
+        for h in range(2):
+            nc.gpsimd.tensor_copy(
+                out=swap[:].rearrange("p (b h) -> p b h", h=2)[:, :, h],
+                in_=ident[:].rearrange("p (b h) -> p b h", h=2)[:, :, 1 - h],
+            )
+        col_b = pool.tile([PART, 1], BF16, name="col_b")
+        nc.gpsimd.dma_start(out=col_b[:], in_=col.partition_broadcast(PART))
+
+        q_all = pool.tile([PART, GROUPS, 4 * F], BF16, name="q_all")
+        w1_codes = pool.tile([PART, G], U32, name="w1_codes", align_bytes=64)
+        w1_scales = pool.tile([PART, G], U8, name="w1_scales", align_bytes=64)
+        w0_codes = pool.tile([PART, P_IN], U32, name="w0_codes", align_bytes=64)
+        w0_scales = pool.tile([PART, P_IN], U8, name="w0_scales", align_bytes=64)
+
+        ctx.enter_context(tc.manual_schedule())
+
+        y_t, a_t, p_t, x_t = {}, {}, {}, {}
+
+        def load_y(g):
+            y_t[g] = pool.tile([PART, PACK, F], F32, name="y_sb", tag="y_sb", bufs=2)
+            pieces = ((0, 2), (2, 4)) if g == 0 else ((0, 4),)
+            nc.sync.dma_start(out=q_all[:, g, 0 : 4 * F - ROLL], in_=gr_rows[g * PART : (g + 1) * PART, ROLL : 4 * F])
+            for lo, hi in pieces:
+                nc.sync.dma_start(out=y_t[g][:, lo:hi, :], in_=y_dram[g][:, lo:hi, :])
+
+        def load_a(g):
+            a_t[g] = pool.tile([PART, PACK, G], F32, name="a_sb", tag="a_sb", bufs=2)
+            nc.sync.dma_start(out=a_t[g][:], in_=a_dram[g])
+
+        def load_p(g):
+            p_t[g] = pool.tile([PART, PACK, P_IN], BF16, name="p_sb", tag="p_sb", bufs=4)
+            nc.sync.dma_start(out=p_t[g][:], in_=p_dram[g])
+
+        def load_x(g):
+            x_t[g] = pool.tile([PART, PACK, F], BF16, name="x_sb", tag="x_sb", bufs=3)
+            nc.sync.dma_start(out=x_t[g][:], in_=x_dram[g])
+
+        def transpose_pair(words, grouped, first, engine):
+            tp = bank("tp")
+            for i in range(2):
+                for u in range(2):
+                    nc.tensor.transpose(tp[:, (2 * i + u) * 128 : (2 * i + u + 1) * 128], words(i, u), ident[:])
+            dst = grouped.rearrange("p n k -> p (n k)").bitcast(F32)[:, 2 * first : 2 * first + 512]
+            engine(
+                out=dst.rearrange("p (t r u) -> p t r u", t=2, u=2),
+                in_=tp[:].rearrange("p (t u r) -> p t r u", t=2, u=2),
+            )
+
+        load_x(0)
+        w1_raw = pool.tile([PART, PACK, F], BF16, name="w1_raw", tag="x_sb", bufs=3)
+        nc.sync.dma_start(out=w1_raw[:], in_=W1[0:G, :].rearrange("(m t) k -> m t k", t=PACK))
+        for h in range(2):
+            nc.scalar.dma_start(out=q_all[h:PART:2, :, 4 * F - ROLL : 4 * F], in_=gr_half[1 - h][:, :, 0:ROLL])
+        load_x(1)
+        load_y(0)
+        load_p(0)
+        load_a(0)
+        w0_raw = pool.tile([PART, 2, PACK, G], BF16, name="w0_raw", tag="p_sb", bufs=4)
+        nc.sync.dma_start(out=w0_raw[:], in_=W0[0:P_IN, :].rearrange("(n m t) k -> m n t k", n=2, t=PACK))
+        load_y(1)
+        load_a(1)
+
+        def stage_tile():
+            return pool.tile([PART, 512, PACK], BF16, name="stage", tag="stage", bufs=4, align_bytes=64)
+
+        ic, isc, staged = {}, {}, {}
+
+        def interleave(g, c, copy):
+            src = x_t[g][:] if c == 2 else p_t[g][:, :, 512 * c : 512 * (c + 1)]
+            staged[g, c] = stage_tile()
+            copy(
+                out=staged[g, c][:].rearrange("p (c i) t -> p c t i", i=4),
+                in_=src.rearrange("p t (c i) -> p c t i", i=4),
+            )
+
+        def quantize_chunk(g, c):
+            ic[g, c] = pool.tile([PART, 512], U32, name="ic", tag="ic", bufs=12, align_bytes=64)
+            isc[g, c] = pool.tile([PART, 512], U8, name="isc", tag="isc", bufs=12, align_bytes=64)
+            nc.vector.quantize_mx(
+                out=ic[g, c][:].bitcast(E4), scales=isc[g, c][:], in_=staged[g, c][:].rearrange("p n k -> p (n k)")
+            )
+
+        vcopy, scopy = nc.vector.tensor_copy, nc.scalar.copy
+        ac, asc, dgc, dgs, dyg, dyc, dys, dh, da, dag = ({} for i in range(10))
+        c_bank = bank("c")
+
+        ob_t = {}
+
+        def dp_tile(g, j, engines):
+            if j % 2 == 0:
+                ob_t[0] = pool.tile([PART, 2, P_IN], F32, name="ob", tag="ob", bufs=4)
+            ob = ob_t[0][:, j % 2, :]
+            for n in range(2):
+                acc = bank("acc")
+                nc.tensor.matmul_mx(
+                    out=acc[:],
+                    lhsT=dgc[g][:, 128 * j : 128 * (j + 1)].bitcast(E5),
+                    lhsT_scale=dgs[g][:, 128 * j : 128 * (j + 1)],
+                    rhs=w0_codes[:, 512 * n : 512 * (n + 1)].bitcast(E4),
+                    rhs_scale=w0_scales[:, 512 * n : 512 * (n + 1)],
+                    start=True,
+                    stop=True,
+                )
+                engines[n](
+                    out=ob[:, 512 * n : 512 * (n + 1)].rearrange("p (m t) -> p m t", t=4),
+                    in_=acc[:].rearrange("p (t m) -> p m t", t=4),
+                )
+            if j % 2:
+                nc.sync.dma_start(out=o_dram[g][:, j - 1 : j + 1, :], in_=ob_t[0][:])
+
+        def warm(n):
+            for k in range(n):
+                spare = bank("acc")
+                nc.tensor.matmul(out=spare[:, 0:PART], lhsT=ident[:], rhs=ident[:], start=True, stop=True)
+
+        def dy_half(g, i):
+            if i == 0:
+                dyg[g, 0] = pool.tile([PART, PACK * F], BF16, name="dy", tag="dy", bufs=1)
+            cols = slice(1024 * i, 1024 * (i + 1))
+            nc.vector.scalar_tensor_tensor(
+                out=dyg[g, 0][:, cols],
+                in0=y_t[g][:].rearrange("p j w -> p (j w)")[:, cols],
+                scalar=0.0,
+                in1=q_all[:, g, cols],
+                op0=ALU.is_gt,
+                op1=ALU.mult,
+            )
+
+        def dy_transposes(g):
+            dyg[g, 1] = pool.tile([PART, 640, PACK], BF16, name="dyg", tag="dyg", bufs=1, align_bytes=64)
+            dyw = dyg[g, 0][:].bitcast(F32)
+
+            def words(j, u):
+                return dyw[:, 256 * j + u : 256 * (j + 1) : 2]
+
+            for s in range(2):
+                transpose_pair(lambda i, u: words(2 * s + i, u), dyg[g, 1][:], 256 * s, scopy)
+                if g == 0 and s == 0:
+                    warm(W[7])
+            tp = bank("tp")
+            for u in range(2):
+                nc.tensor.transpose(tp[:, 128 * u : 128 * (u + 1)], words(3, u), swap[:])
+            scopy(
+                out=dyg[g, 1][:].rearrange("p n k -> p (n k)").bitcast(F32)[:, 1024:1280].rearrange("p (r u) -> p r u", u=2),
+                in_=tp[:, 0:256].rearrange("p (u r) -> p r u", u=2),
+            )
+
+        def dy_quantize(g):
+            dyc[g] = pool.tile([PART, 640], U32, name="dyc", tag="dyc", bufs=2, align_bytes=64)
+            dys[g] = pool.tile([PART, 640], U8, name="dys", tag="dys", bufs=2, align_bytes=64)
+            for lo, hi in ((0, 512), (512, 640)):
+                nc.vector.quantize_mx(
+                    out=dyc[g][:, lo:hi].bitcast(E5),
+                    scales=dys[g][:, lo:hi],
+                    in_=dyg[g, 1][:, lo:hi, :].rearrange("p n k -> p (n k)"),
+                )
+
+        def dh_tile(g, s):
+            dh[g, s] = bank("dh")
+            nc.tensor.matmul_mx(
+                out=dh[g, s][:],
+                lhsT=dyc[g][:, 128 * s : 128 * (s + 1)].bitcast(E5),
+                lhsT_scale=dys[g][:, 128 * s : 128 * (s + 1)],
+                rhs=w1_codes[:].bitcast(E4),
+                rhs_scale=w1_scales[:],
+                start=True,
+                stop=True,
+            )
+
+        def mask(g, j, s, lo, hi, src):
+            nc.vector.scalar_tensor_tensor(
+                out=da[g][:, j, :].rearrange("p (t m) -> p t m", t=4)[:, :, lo:hi],
+                in0=a_t[g][:, j, :].rearrange("p (m t) -> p t m", t=4)[:, :, lo:hi],
+                scalar=0.0,
+                in1=dh[g, s][:].rearrange("p (t m) -> p t m", t=4)[:, :, src : src + hi - lo],
+                op0=ALU.is_gt,
+                op1=ALU.mult,
+            )
+
+        def da_transposes(g, j):
+            if j == 0:
+                dag[g] = pool.tile([PART, GROUP, PACK], BF16, name="dag", tag="dag", bufs=1, align_bytes=64)
+            tp = bank("tp")
+            for t in range(4):
+                nc.tensor.transpose(tp[:, 128 * t : 128 * (t + 1)], da[g][:, j, 128 * t : 128 * (t + 1)], ident[:])
+            for t in range(4):
+                nc.tensor.matmul(
+                    out=c_bank[:, 128 * t : 128 * (t + 1)],
+                    lhsT=da[g][:, j, 128 * t : 128 * (t + 1)],
+                    rhs=ident[:],
+                    is_transpose=True,
+                    start=(g == 0 and j == 0 and t == 0),
+                    stop=(g == 3 and j == 3 and t == 3),
+                )
+            scopy(out=dag[g][:, 128 * j : 128 * (j + 1), :], in_=tp[:].rearrange("p (t n) -> p n t", t=4))
+
+        interleave(0, 2, vcopy)
+        load_x(2)
+        w1_g = stage_tile()
+        warm(W[0])
+        w1_words = w1_raw[:].rearrange("p t k -> p (t k)").bitcast(F32)
+        for s in range(2):
+            transpose_pair(
+                lambda i, u: w1_words[:, 256 * (2 * s + i) + u : 256 * (2 * s + i + 1) : 2], w1_g[:], 256 * s, scopy
+            )
+        warm(W[1])
+        quantize_chunk(0, 2)
+        nc.vector.quantize_mx(
+            out=w1_codes[:].bitcast(E4), scales=w1_scales[:], in_=w1_g[:].rearrange("p n k -> p (n k)")
+        )
+        interleave(1, 2, vcopy)
+        dy_half(0, 0)
+        dy_half(0, 1)
+        dy_transposes(0)
+        warm(W[2])
+        load_y(2)
+        quantize_chunk(1, 2)
+        interleave(0, 0, vcopy)
+        dy_quantize(0)
+        interleave(0, 1, vcopy)
+        for s in (4, 0, 1):
+            dh_tile(0, s)
+
+        w0_g = {}
+        w0_words = w0_raw[:].rearrange("p n t k -> p (n t k)").bitcast(F32)
+
+        def w0_transposes(s):
+            if s % 2 == 0:
+                w0_g[s // 2] = stage_tile()
+            transpose_pair(
+                lambda i, u: w0_words[:, 256 * (2 * s + i) + u : 256 * (2 * s + i + 1) : 2],
+                w0_g[s // 2][:], 256 * (s % 2), scopy,
+            )
+
+        def w0_quantize(n):
+            nc.vector.quantize_mx(
+                out=w0_codes[:, 512 * n : 512 * (n + 1)].bitcast(E4),
+                scales=w0_scales[:, 512 * n : 512 * (n + 1)],
+                in_=w0_g[n][:].rearrange("p n k -> p (n k)"),
+            )
+
+        def dp_index(k):
+            if k >= 0:
+                dp_tile(k // 4, k % 4, (scopy, scopy))
+
+        at = {}
+
+        def da_cast(g):
+            at[0] = pool.tile([PART, G, PACK], BF16, name="at", tag="at", bufs=1, align_bytes=64)
+            vcopy(
+                out=at[0][:].rearrange("p (c i) j -> p c j i", i=4),
+                in_=da[g][:].rearrange("p j (c i) -> p c j i", i=4),
+            )
+
+        def da_quantize(g):
+            ac[g] = pool.tile([PART, G], U32, name="ac", tag="ac", bufs=GROUPS, align_bytes=64)
+            asc[g] = pool.tile([PART, G], U8, name="asc", tag="asc", bufs=GROUPS, align_bytes=64)
+            dgc[g] = pool.tile([PART, GROUP], U32, name="dgc", tag="dgc", bufs=2, align_bytes=64)
+            dgs[g] = pool.tile([PART, GROUP], U8, name="dgs", tag="dgs", bufs=2, align_bytes=64)
+            nc.vector.quantize_mx(out=dgc[g][:].bitcast(E5), scales=dgs[g][:], in_=dag[g][:].rearrange("p n k -> p (n k)"))
+            nc.vector.quantize_mx(out=ac[g][:].bitcast(E5), scales=asc[g][:], in_=at[0][:].rearrange("p n k -> p (n k)"))
+
+        for g in range(GROUPS):
+            da[g] = pool.tile([PART, PACK, G], F32, name="da", tag="da", bufs=1)
+            mask(g, 0, 4, 0, 32, 96)
+            mask(g, 0, 0, 32, 128, 0)
+            dh_tile(g, 2)
+            mask(g, 1, 0, 0, 32, 96)
+            mask(g, 1, 1, 32, 128, 0)
+            dh_tile(g, 3)
+            mask(g, 2, 1, 0, 32, 96)
+            mask(g, 2, 2, 32, 128, 0)
+            mask(g, 3, 2, 0, 32, 96)
+            mask(g, 3, 3, 32, 128, 0)
+            da_transposes(g, 0)
+            da_transposes(g, 1)
+            if g == 0:
+                warm(W[3])
+            dp_index(4 * g - 2)
+            da_transposes(g, 2)
+            da_transposes(g, 3)
+            if g == 0:
+                warm(W[4])
+            dp_index(4 * g - 1)
+            if g == 0:
+                load_a(2)
+                load_x(3)
+                for s in range(4):
+                    w0_transposes(s)
+                    warm(W[5])
+                da_cast(0)
+                quantize_chunk(0, 0)
+                quantize_chunk(0, 1)
+                da_quantize(0)
+            if g == 1:
+                load_a(3)
+                load_p(1)
+            if g == 2:
+                load_p(2)
+                load_p(3)
+            if g < 3:
+                dy_half(g + 1, 0)
+                dy_half(g + 1, 1)
+                dy_transposes(g + 1)
+            if g == 0:
+                load_y(3)
+                warm(W[6])
+                w0_quantize(0)
+                w0_quantize(1)
+            else:
+                da_cast(g)
+                if g == 2:
+                    quantize_chunk(2, 2)
+                if g == 3:
+                    quantize_chunk(3, 2)
+                    interleave(1, 0, vcopy)
+                da_quantize(g)
+            if g < 3:
+                dp_index(4 * g)
+                dy_quantize(g + 1)
+                if g > 0:
+                    interleave(g + 1, 2, vcopy)
+                for s in (4, 0, 1):
+                    dh_tile(g + 1, s)
+                dp_index(4 * g + 1)
+
+        seq = ["tp", "dh", "dh", "dh", "tp", "tp", "acc", "acc", "dh", "dh", "dh", "tp"]
+        dw_bank = {}
+
+        def dw_pass(i, g):
+            c, r = divmod(i, 4)
+            if g == 0:
+                dw_bank[i] = bank(seq[i])
+            nc.tensor.matmul_mx(
+                out=dw_bank[i][:],
+                lhsT=ic[g, c][:, 128 * r : 128 * (r + 1)].bitcast(E4),
+                lhsT_scale=isc[g, c][:, 128 * r : 128 * (r + 1)],
+                rhs=ac[g][:].bitcast(E5),
+                rhs_scale=asc[g][:],
+                start=(g == 0),
+                stop=(g == GROUPS - 1),
+            )
+
+        def dw_out(i, copy):
+            if i % 4 == 0:
+                ob_t[1] = pool.tile([PART, 4, G], F32, name="wb", tag="ob", bufs=4)
+            wb = ob_t[1][:, i % 4, :]
+            copy(out=wb.rearrange("p (m t) -> p m t", t=4), in_=dw_bank[i][:].rearrange("p (t m) -> p m t", t=4))
+            nc.sync.dma_start(out=out_1[128 * i : 128 * (i + 1), :], in_=wb)
+
+        interleave(3, 0, scopy)
+        for i in range(8, 12):
+            for g in range(3):
+                dw_pass(i, g)
+        interleave(2, 0, vcopy)
+        quantize_chunk(1, 0)
+        dp_index(12)
+        for i in range(8, 12):
+            dw_pass(i, 3)
+        dp_index(13)
+        interleave(1, 1, vcopy)
+        quantize_chunk(2, 0)
+        quantize_chunk(3, 0)
+        dw_out(8, scopy)
+        dw_out(9, scopy)
+        dw_out(10, vcopy)
+        dw_out(11, vcopy)
+        for i in range(4):
+            for g in range(4):
+                dw_pass(i, g)
+            if i < 2:
+                dp_index(14 + i)
+        interleave(2, 1, vcopy)
+        interleave(3, 1, scopy)
+        red = pool.tile([PART, 4], F32, name="red")
+        red_col = pool.tile([PART, 4], F32, name="red_col")
+        nc.vector.tensor_reduce(
+            out=red[:], in_=c_bank[:].rearrange("p (t n) -> p t n", t=4), axis=mybir.AxisListType.X, op=ALU.add
+        )
+        quantize_chunk(1, 1)
+        nc.vector.tensor_scalar(out=red_col[:], in0=red[:], scalar1=col_b[:, 0:1], scalar2=None, op0=ALU.mult)
+        last_bank = bank("c")
+        for t in range(4):
+            nc.tensor.transpose(
+                last_bank[:, 128 * t : 128 * (t + 1)], red_col[:, t : t + 1].to_broadcast([PART, PART]), ident[:]
+            )
+        quantize_chunk(2, 1)
+        dw_out(0, vcopy)
+        quantize_chunk(3, 1)
+        dw_out(1, scopy)
+        dw_out(2, vcopy)
+        dw_out(3, scopy)
+        row = pool.tile([1, G], F32, name="row")
+        scopy(out=row[:].rearrange("p (m t) -> p m t", t=4), in_=last_bank[0:1, :].rearrange("p (t m) -> p m t", t=4))
+        nc.sync.dma_start(out=out_1[C_OUT : C_OUT + 1, :], in_=row[:])
+        for g in range(4):
+            for i in range(4, 8):
+                dw_pass(i, g)
+        for i in range(4, 8):
+            dw_out(i, scopy if i % 2 == 0 else vcopy)

@@ -22,7 +22,6 @@ PACK = 4
 GROUP = PART * PACK
 GROUPS = N // GROUP
 ROLL = 128
-W = (8, 8, 3, 2, 1, 1, 1, 2)
 
 
 def tile_capsuleneuralnetwork_pa_v_kernel(
@@ -158,11 +157,6 @@ def tile_capsuleneuralnetwork_pa_v_kernel(
             if j % 2:
                 nc.sync.dma_start(out=o_dram[g][:, j - 1 : j + 1, :], in_=ob_t[0][:])
 
-        def warm(n):
-            for k in range(n):
-                spare = bank("acc")
-                nc.tensor.matmul(out=spare[:, 0:PART], lhsT=ident[:], rhs=ident[:], start=True, stop=True)
-
         def dy_half(g, i):
             if i == 0:
                 dyg[g, 0] = pool.tile([PART, PACK * F], BF16, name="dy", tag="dy", bufs=1)
@@ -185,8 +179,6 @@ def tile_capsuleneuralnetwork_pa_v_kernel(
 
             for s in range(2):
                 transpose_pair(lambda i, u: words(2 * s + i, u), dyg[g, 1][:], 256 * s, scopy)
-                if g == 0 and s == 0:
-                    warm(W[7])
             tp = bank("tp")
             for u in range(2):
                 nc.tensor.transpose(tp[:, 128 * u : 128 * (u + 1)], words(3, u), swap[:])
@@ -247,13 +239,11 @@ def tile_capsuleneuralnetwork_pa_v_kernel(
         interleave(0, 2, vcopy)
         load_x(2)
         w1_g = stage_tile()
-        warm(W[0])
         w1_words = w1_raw[:].rearrange("p t k -> p (t k)").bitcast(F32)
         for s in range(2):
             transpose_pair(
                 lambda i, u: w1_words[:, 256 * (2 * s + i) + u : 256 * (2 * s + i + 1) : 2], w1_g[:], 256 * s, scopy
             )
-        warm(W[1])
         quantize_chunk(0, 2)
         nc.vector.quantize_mx(
             out=w1_codes[:].bitcast(E4), scales=w1_scales[:], in_=w1_g[:].rearrange("p n k -> p (n k)")
@@ -262,7 +252,6 @@ def tile_capsuleneuralnetwork_pa_v_kernel(
         dy_half(0, 0)
         dy_half(0, 1)
         dy_transposes(0)
-        warm(W[2])
         load_y(2)
         quantize_chunk(1, 2)
         interleave(0, 0, vcopy)
@@ -324,20 +313,15 @@ def tile_capsuleneuralnetwork_pa_v_kernel(
             mask(g, 3, 3, 32, 128, 0)
             da_transposes(g, 0)
             da_transposes(g, 1)
-            if g == 0:
-                warm(W[3])
             dp_index(4 * g - 2)
             da_transposes(g, 2)
             da_transposes(g, 3)
-            if g == 0:
-                warm(W[4])
             dp_index(4 * g - 1)
             if g == 0:
                 load_a(2)
                 load_x(3)
                 for s in range(4):
                     w0_transposes(s)
-                    warm(W[5])
                 da_cast(0)
                 quantize_chunk(0, 0)
                 quantize_chunk(0, 1)
@@ -354,7 +338,6 @@ def tile_capsuleneuralnetwork_pa_v_kernel(
                 dy_transposes(g + 1)
             if g == 0:
                 load_y(3)
-                warm(W[6])
                 w0_quantize(0)
                 w0_quantize(1)
             else:

@@ -5,9 +5,9 @@ from concourse.masks import make_identity
 
 B, T, P_IN, F, G = 256, 8, 1024, 512, 512
 N = B * T
-C_OUT = P_IN + F
-FLOPS = 2 * N * F * G + 2 * N * G * P_IN + 2 * N * C_OUT * G
-BYTES = 2 * (N * P_IN + N * F + 1 + P_IN * G + G * F + N * F) + 4 * (N * G + N * F) + 4 * (N * P_IN + (C_OUT + 1) * G)
+C_IN = P_IN + F
+FLOPS = 2 * N * F * G + 2 * N * G * P_IN + 2 * N * C_IN * G
+BYTES = 2 * (N * P_IN + N * F + 1 + P_IN * G + G * F + N * F) + 4 * (N * G + N * F) + 4 * (N * P_IN + (C_IN + 1) * G)
 
 F32 = mybir.dt.float32
 BF16 = mybir.dt.bfloat16
@@ -19,21 +19,27 @@ ALU = mybir.AluOpType
 
 PART = 128
 PACK = 4
-GROUP = PART * PACK
-GROUPS = N // GROUP
+PASS = PART * PACK
+GROUPS = N // PASS
 ROLL = 128
+ROW = PACK * F
+LAST = GROUPS - 1
 
 
 def tile_capsuleneuralnetwork_pa_v_kernel(
     tc, primary_input, prev, col, W0, b0, W1, b1, a, y, grad_out, out_0, out_1
 ):
     nc = tc.nc
+    vcopy, scopy = nc.vector.tensor_copy, nc.scalar.copy
 
-    p_dram = primary_input.rearrange("b (t w) -> (b t) w", t=T).rearrange("(g p j) w -> g p j w", p=PART, j=PACK)
-    x_dram = prev.rearrange("b (t w) -> (b t) w", t=T).rearrange("(g p j) w -> g p j w", p=PART, j=PACK)
-    a_dram = a.rearrange("b t w -> (b t) w").rearrange("(g p j) w -> g p j w", p=PART, j=PACK)
-    y_dram = y.rearrange("b t w -> (b t) w").rearrange("(g p j) w -> g p j w", p=PART, j=PACK)
-    o_dram = out_0.rearrange("b (t w) -> (b t) w", t=T).rearrange("(g p j) w -> g p j w", p=PART, j=PACK)
+    def by_group(rows):
+        return rows.rearrange("(g p j) w -> g p j w", p=PART, j=PACK)
+
+    p_dram = by_group(primary_input.rearrange("b (t w) -> (b t) w", t=T))
+    x_dram = by_group(prev.rearrange("b (t w) -> (b t) w", t=T))
+    a_dram = by_group(a.rearrange("b t w -> (b t) w"))
+    y_dram = by_group(y.rearrange("b t w -> (b t) w"))
+    o_dram = by_group(out_0.rearrange("b (t w) -> (b t) w", t=T))
     gr_rows = grad_out.rearrange("b (h w) -> (b h) w", h=2)
     gr_half = grad_out.rearrange("(g b) (h w) -> h b g w", b=PART // 2, h=2)
 
@@ -41,393 +47,449 @@ def tile_capsuleneuralnetwork_pa_v_kernel(
         pool = ctx.enter_context(tc.tile_pool(name="pool", bufs=1))
         psum = ctx.enter_context(tc.psum_pool(name="psum", bufs=1))
 
-        def bank(tag):
-            return psum.tile([PART, 512], F32, name=tag, tag=tag, bufs={"tp": 2, "dh": 3, "acc": 2, "c": 1}[tag])
+        rings = {"vector": [0, 1, 2], "scalar": [3, 4, 5, 6]}
+
+        def bank(which):
+            if which in rings:
+                ring = rings[which]
+                which = ring[0]
+                ring.remove(which)
+                ring.append(which)
+            return psum.tile([PART, 512], F32, name="bank%d" % which, tag="bank%d" % which, bufs=1)
+
+        def mx_pair(name, width, bufs):
+            codes = pool.tile([PART, width], U32, name=name + "_c", tag=name + "_c", bufs=bufs, align_bytes=64)
+            scales = pool.tile([PART, width], U8, name=name + "_s", tag=name + "_s", bufs=bufs, align_bytes=64)
+            return codes, scales
+
+        def quantize(pair, fmt, src, lo=0):
+            width = src.shape[1] // PACK
+            nc.vector.quantize_mx(out=pair[0][:, lo : lo + width].bitcast(fmt), scales=pair[1][:, lo : lo + width], in_=src)
+
+        def mx_pass(out, lhs, lhs_fmt, m0, rhs, rhs_fmt, n0, start=True, stop=True):
+            nc.tensor.matmul_mx(
+                out=out[:],
+                lhsT=lhs[0][:, m0 : m0 + PART].bitcast(lhs_fmt),
+                lhsT_scale=lhs[1][:, m0 : m0 + PART],
+                rhs=rhs[0][:, n0 : n0 + 512].bitcast(rhs_fmt),
+                rhs_scale=rhs[1][:, n0 : n0 + 512],
+                start=start,
+                stop=stop,
+            )
 
         ident = pool.tile([PART, PART], F32, name="ident")
-        swap = pool.tile([PART, PART], F32, name="swap")
         make_identity(nc, ident[:])
-        for h in range(2):
-            nc.gpsimd.tensor_copy(
-                out=swap[:].rearrange("p (b h) -> p b h", h=2)[:, :, h],
-                in_=ident[:].rearrange("p (b h) -> p b h", h=2)[:, :, 1 - h],
-            )
         col_b = pool.tile([PART, 1], BF16, name="col_b")
-        nc.gpsimd.dma_start(out=col_b[:], in_=col.partition_broadcast(PART))
-
-        q_all = pool.tile([PART, GROUPS, 4 * F], BF16, name="q_all")
-        w1_codes = pool.tile([PART, G], U32, name="w1_codes", align_bytes=64)
-        w1_scales = pool.tile([PART, G], U8, name="w1_scales", align_bytes=64)
-        w0_codes = pool.tile([PART, P_IN], U32, name="w0_codes", align_bytes=64)
-        w0_scales = pool.tile([PART, P_IN], U8, name="w0_scales", align_bytes=64)
 
         ctx.enter_context(tc.manual_schedule())
 
+        q_all = pool.tile([PART, GROUPS, ROW], BF16, name="q_all", tag="wide_q")
         y_t, a_t, p_t, x_t = {}, {}, {}, {}
 
-        def load_y(g):
-            y_t[g] = pool.tile([PART, PACK, F], F32, name="y_sb", tag="y_sb", bufs=2)
-            pieces = ((0, 2), (2, 4)) if g == 0 else ((0, 4),)
-            nc.sync.dma_start(out=q_all[:, g, 0 : 4 * F - ROLL], in_=gr_rows[g * PART : (g + 1) * PART, ROLL : 4 * F])
-            for lo, hi in pieces:
-                nc.sync.dma_start(out=y_t[g][:, lo:hi, :], in_=y_dram[g][:, lo:hi, :])
+        def load_qy(g, lo=0, hi=ROW):
+            if lo == 0:
+                y_t[g] = pool.tile([PART, ROW], F32, name="y_sb", tag="ring_y", bufs=2)
+            q_hi = min(hi, ROW - ROLL)
+            nc.sync.dma_start(out=q_all[:, g, lo:q_hi], in_=gr_rows[g * PART : (g + 1) * PART, ROLL + lo : ROLL + q_hi])
+            nc.sync.dma_start(out=y_t[g][:, lo:hi], in_=y_dram[g].rearrange("p j w -> p (j w)")[:, lo:hi])
 
-        def load_a(g):
-            a_t[g] = pool.tile([PART, PACK, G], F32, name="a_sb", tag="a_sb", bufs=2)
-            nc.sync.dma_start(out=a_t[g][:], in_=a_dram[g])
+        def load_a(g, lo=0, hi=ROW):
+            if lo == 0:
+                a_t[g] = pool.tile([PART, ROW], F32, name="a_sb", tag="ring_a", bufs=2)
+            nc.sync.dma_start(out=a_t[g][:, lo:hi], in_=a_dram[g].rearrange("p j w -> p (j w)")[:, lo:hi])
 
         def load_p(g):
-            p_t[g] = pool.tile([PART, PACK, P_IN], BF16, name="p_sb", tag="p_sb", bufs=4)
+            p_t[g] = pool.tile([PART, PACK, P_IN], BF16, name="p_sb", tag="ring_p" if g < 2 else "ring_y", bufs=2)
             nc.sync.dma_start(out=p_t[g][:], in_=p_dram[g])
 
         def load_x(g):
-            x_t[g] = pool.tile([PART, PACK, F], BF16, name="x_sb", tag="x_sb", bufs=3)
+            x_t[g] = pool.tile([PART, PACK, F], BF16, name="x_sb", tag="x_sb", bufs=GROUPS)
             nc.sync.dma_start(out=x_t[g][:], in_=x_dram[g])
 
-        def transpose_pair(words, grouped, first, engine):
-            tp = bank("tp")
+        def stage_tile():
+            return pool.tile([PART, ROW], BF16, name="stage", tag="stage", bufs=4, align_bytes=64)
+
+        def word_transposes(words, first):
+            tp = bank("scalar")
             for i in range(2):
                 for u in range(2):
-                    nc.tensor.transpose(tp[:, (2 * i + u) * 128 : (2 * i + u + 1) * 128], words(i, u), ident[:])
-            dst = grouped.rearrange("p n k -> p (n k)").bitcast(F32)[:, 2 * first : 2 * first + 512]
-            engine(
-                out=dst.rearrange("p (t r u) -> p t r u", t=2, u=2),
-                in_=tp[:].rearrange("p (t u r) -> p t r u", t=2, u=2),
-            )
+                    lo = 256 * (first + i)
+                    nc.tensor.transpose(tp[:, (2 * i + u) * PART : (2 * i + u + 1) * PART], words[:, lo + u : lo + 256 : 2], ident[:])
+            return tp
 
-        load_x(0)
-        w1_raw = pool.tile([PART, PACK, F], BF16, name="w1_raw", tag="x_sb", bufs=3)
-        nc.sync.dma_start(out=w1_raw[:], in_=W1[0:G, :].rearrange("(m t) k -> m t k", t=PACK))
-        for h in range(2):
-            nc.scalar.dma_start(out=q_all[h:PART:2, :, 4 * F - ROLL : 4 * F], in_=gr_half[1 - h][:, :, 0:ROLL])
-        load_x(1)
-        load_y(0)
-        load_p(0)
-        load_a(0)
-        w0_raw = pool.tile([PART, 2, PACK, G], BF16, name="w0_raw", tag="p_sb", bufs=4)
-        nc.sync.dma_start(out=w0_raw[:], in_=W0[0:P_IN, :].rearrange("(n m t) k -> m n t k", n=2, t=PACK))
-        load_y(1)
-        load_a(1)
-
-        def stage_tile():
-            return pool.tile([PART, 512, PACK], BF16, name="stage", tag="stage", bufs=4, align_bytes=64)
-
-        ic, isc, staged = {}, {}, {}
-
-        def interleave(g, c, copy):
-            src = x_t[g][:] if c == 2 else p_t[g][:, :, 512 * c : 512 * (c + 1)]
-            staged[g, c] = stage_tile()
-            copy(
-                out=staged[g, c][:].rearrange("p (c i) t -> p c t i", i=4),
-                in_=src.rearrange("p t (c i) -> p c t i", i=4),
-            )
-
-        def quantize_chunk(g, c):
-            ic[g, c] = pool.tile([PART, 512], U32, name="ic", tag="ic", bufs=12, align_bytes=64)
-            isc[g, c] = pool.tile([PART, 512], U8, name="isc", tag="isc", bufs=12, align_bytes=64)
-            nc.vector.quantize_mx(
-                out=ic[g, c][:].bitcast(E4), scales=isc[g, c][:], in_=staged[g, c][:].rearrange("p n k -> p (n k)")
-            )
-
-        vcopy, scopy = nc.vector.tensor_copy, nc.scalar.copy
-        ac, asc, dgc, dgs, dyg, dyc, dys, dh, da, dag = ({} for i in range(10))
-        c_bank = bank("c")
-
-        ob_t = {}
-
-        def dp_tile(g, j, engines):
-            if j % 2 == 0:
-                ob_t[0] = pool.tile([PART, 2, P_IN], F32, name="ob", tag="ob", bufs=4)
-            ob = ob_t[0][:, j % 2, :]
-            for n in range(2):
-                acc = bank("acc")
-                nc.tensor.matmul_mx(
-                    out=acc[:],
-                    lhsT=dgc[g][:, 128 * j : 128 * (j + 1)].bitcast(E5),
-                    lhsT_scale=dgs[g][:, 128 * j : 128 * (j + 1)],
-                    rhs=w0_codes[:, 512 * n : 512 * (n + 1)].bitcast(E4),
-                    rhs_scale=w0_scales[:, 512 * n : 512 * (n + 1)],
-                    start=True,
-                    stop=True,
-                )
-                engines[n](
-                    out=ob[:, 512 * n : 512 * (n + 1)].rearrange("p (m t) -> p m t", t=4),
-                    in_=acc[:].rearrange("p (t m) -> p m t", t=4),
-                )
-            if j % 2:
-                nc.sync.dma_start(out=o_dram[g][:, j - 1 : j + 1, :], in_=ob_t[0][:])
-
-        def dy_half(g, i):
-            if i == 0:
-                dyg[g, 0] = pool.tile([PART, PACK * F], BF16, name="dy", tag="dy", bufs=1)
-            cols = slice(1024 * i, 1024 * (i + 1))
-            nc.vector.scalar_tensor_tensor(
-                out=dyg[g, 0][:, cols],
-                in0=y_t[g][:].rearrange("p j w -> p (j w)")[:, cols],
-                scalar=0.0,
-                in1=q_all[:, g, cols],
-                op0=ALU.is_gt,
-                op1=ALU.mult,
-            )
-
-        def dy_transposes(g):
-            dyg[g, 1] = pool.tile([PART, 640, PACK], BF16, name="dyg", tag="dyg", bufs=1, align_bytes=64)
-            dyw = dyg[g, 0][:].bitcast(F32)
-
-            def words(j, u):
-                return dyw[:, 256 * j + u : 256 * (j + 1) : 2]
-
-            for s in range(2):
-                transpose_pair(lambda i, u: words(2 * s + i, u), dyg[g, 1][:], 256 * s, scopy)
-            tp = bank("tp")
-            for u in range(2):
-                nc.tensor.transpose(tp[:, 128 * u : 128 * (u + 1)], words(3, u), swap[:])
+        def weight_half(raw_words, staged, s):
+            tp = word_transposes(raw_words, 2 * s)
             scopy(
-                out=dyg[g, 1][:].rearrange("p n k -> p (n k)").bitcast(F32)[:, 1024:1280].rearrange("p (r u) -> p r u", u=2),
-                in_=tp[:, 0:256].rearrange("p (u r) -> p r u", u=2),
+                out=staged[:].bitcast(F32).rearrange("p (m w) -> p m w", w=8)[:, :, 4 * s : 4 * s + 4],
+                in_=tp[:].rearrange("p (w m) -> p m w", w=4),
             )
 
-        def dy_quantize(g):
-            dyc[g] = pool.tile([PART, 640], U32, name="dyc", tag="dyc", bufs=2, align_bytes=64)
-            dys[g] = pool.tile([PART, 640], U8, name="dys", tag="dys", bufs=2, align_bytes=64)
-            for lo, hi in ((0, 512), (512, 640)):
-                nc.vector.quantize_mx(
-                    out=dyc[g][:, lo:hi].bitcast(E5),
-                    scales=dys[g][:, lo:hi],
-                    in_=dyg[g, 1][:, lo:hi, :].rearrange("p n k -> p (n k)"),
+        dy, dyg, dyw, dyq, dywq, dh = ({} for i in range(6))
+
+        def dy_mask(g, s):
+            if s == 0:
+                dy[g] = pool.tile([PART, ROW], BF16, name="dy", tag="dy", bufs=1)
+            cols = slice(1024 * s, 1024 * (s + 1))
+            nc.vector.scalar_tensor_tensor(
+                out=dy[g][:, cols], in0=y_t[g][:, cols], scalar=0.0, in1=q_all[:, g, cols], op0=ALU.is_gt, op1=ALU.mult
+            )
+
+        def dy_turn(g, s):
+            if s == 0:
+                dyg[g] = pool.tile([PART, ROW], BF16, name="dyg", tag="dyg", bufs=1, align_bytes=64)
+            tp = word_transposes(dy[g][:].bitcast(F32), 2 * s)
+            scopy(
+                out=dyg[g][:].bitcast(F32)[:, 512 * s : 512 * (s + 1)].rearrange("p (i r u) -> p i r u", i=2, u=2),
+                in_=tp[:].rearrange("p (i u r) -> p i r u", i=2, u=2),
+            )
+            if s == 1:
+                dyw[g] = pool.tile([PART, PASS], BF16, name="dyw", tag="dyw", bufs=1, align_bytes=64)
+                scopy(
+                    out=dyw[g][:].bitcast(F32).rearrange("p (b h u) -> p b h u", h=2, u=2),
+                    in_=tp[:, 256:512].rearrange("p (u b h) -> p b h u", u=2, h=2)[:, :, ::-1, :],
                 )
 
-        def dh_tile(g, s):
-            dh[g, s] = bank("dh")
-            nc.tensor.matmul_mx(
-                out=dh[g, s][:],
-                lhsT=dyc[g][:, 128 * s : 128 * (s + 1)].bitcast(E5),
-                lhsT_scale=dys[g][:, 128 * s : 128 * (s + 1)],
-                rhs=w1_codes[:].bitcast(E4),
-                rhs_scale=w1_scales[:],
-                start=True,
-                stop=True,
-            )
+        def dy_quantize(g, lo=0, hi=ROW):
+            if lo == 0:
+                dyq[g] = mx_pair("dyq", PASS, 2)
+            quantize(dyq[g], E5, dyg[g][:, lo:hi], lo // PACK)
+            if hi == ROW:
+                dywq[g] = mx_pair("dywq", PART, 2)
+                quantize(dywq[g], E5, dyw[g][:])
 
-        def mask(g, j, s, lo, hi, src):
+        def dh_pass(g, s):
+            dh[g, s] = bank("vector")
+            if s < 0:
+                mx_pass(dh[g, s], dywq[g], E5, 0, w1q, E4, 0)
+            else:
+                mx_pass(dh[g, s], dyq[g], E5, PART * s, w1q, E4, 0)
+
+        da, at, atq, dag, dagq, ob = ({} for i in range(6))
+
+        def da_mask(g, s):
+            if s == (0 if g == 0 else -1):
+                da[g] = pool.tile([PART, ROW], F32, name="da", tag="da", bufs=2)
+            lo, hi = max(0, G * s + ROLL), min(ROW, G * (s + 1) + ROLL)
+            src = lo - (G * s + ROLL)
             nc.vector.scalar_tensor_tensor(
-                out=da[g][:, j, :].rearrange("p (t m) -> p t m", t=4)[:, :, lo:hi],
-                in0=a_t[g][:, j, :].rearrange("p (m t) -> p t m", t=4)[:, :, lo:hi],
-                scalar=0.0,
-                in1=dh[g, s][:].rearrange("p (t m) -> p t m", t=4)[:, :, src : src + hi - lo],
-                op0=ALU.is_gt,
-                op1=ALU.mult,
+                out=da[g][:, lo:hi], in0=a_t[g][:, lo:hi], scalar=0.0, in1=dh[g, s][:, src : src + hi - lo],
+                op0=ALU.is_gt, op1=ALU.mult,
             )
 
-        def da_transposes(g, j):
-            if j == 0:
-                dag[g] = pool.tile([PART, GROUP, PACK], BF16, name="dag", tag="dag", bufs=1, align_bytes=64)
-            tp = bank("tp")
-            for t in range(4):
-                nc.tensor.transpose(tp[:, 128 * t : 128 * (t + 1)], da[g][:, j, 128 * t : 128 * (t + 1)], ident[:])
-            for t in range(4):
+        def da_sums(g, j):
+            for t in range(PACK):
                 nc.tensor.matmul(
-                    out=c_bank[:, 128 * t : 128 * (t + 1)],
-                    lhsT=da[g][:, j, 128 * t : 128 * (t + 1)],
+                    out=sum_bank[:, PART * t : PART * (t + 1)],
+                    lhsT=da[g][:, G * j + PART * t : G * j + PART * (t + 1)],
                     rhs=ident[:],
                     is_transpose=True,
-                    start=(g == 0 and j == 0 and t == 0),
-                    stop=(g == 3 and j == 3 and t == 3),
+                    start=(g == 0 and j == 1 and t == 0),
+                    stop=(g == LAST and j == PACK - 1 and t == PACK - 1),
                 )
-            scopy(out=dag[g][:, 128 * j : 128 * (j + 1), :], in_=tp[:].rearrange("p (t n) -> p n t", t=4))
-
-        interleave(0, 2, vcopy)
-        load_x(2)
-        w1_g = stage_tile()
-        w1_words = w1_raw[:].rearrange("p t k -> p (t k)").bitcast(F32)
-        for s in range(2):
-            transpose_pair(
-                lambda i, u: w1_words[:, 256 * (2 * s + i) + u : 256 * (2 * s + i + 1) : 2], w1_g[:], 256 * s, scopy
-            )
-        quantize_chunk(0, 2)
-        nc.vector.quantize_mx(
-            out=w1_codes[:].bitcast(E4), scales=w1_scales[:], in_=w1_g[:].rearrange("p n k -> p (n k)")
-        )
-        interleave(1, 2, vcopy)
-        dy_half(0, 0)
-        dy_half(0, 1)
-        dy_transposes(0)
-        load_y(2)
-        quantize_chunk(1, 2)
-        interleave(0, 0, vcopy)
-        dy_quantize(0)
-        interleave(0, 1, vcopy)
-        for s in (4, 0, 1):
-            dh_tile(0, s)
-
-        w0_g = {}
-        w0_words = w0_raw[:].rearrange("p n t k -> p (n t k)").bitcast(F32)
-
-        def w0_transposes(s):
-            if s % 2 == 0:
-                w0_g[s // 2] = stage_tile()
-            transpose_pair(
-                lambda i, u: w0_words[:, 256 * (2 * s + i) + u : 256 * (2 * s + i + 1) : 2],
-                w0_g[s // 2][:], 256 * (s % 2), scopy,
-            )
-
-        def w0_quantize(n):
-            nc.vector.quantize_mx(
-                out=w0_codes[:, 512 * n : 512 * (n + 1)].bitcast(E4),
-                scales=w0_scales[:, 512 * n : 512 * (n + 1)],
-                in_=w0_g[n][:].rearrange("p n k -> p (n k)"),
-            )
-
-        def dp_index(k):
-            if k >= 0:
-                dp_tile(k // 4, k % 4, (scopy, scopy))
-
-        at = {}
 
         def da_cast(g):
-            at[0] = pool.tile([PART, G, PACK], BF16, name="at", tag="at", bufs=1, align_bytes=64)
+            at[g] = pool.tile([PART, ROW], BF16, name="at", tag="at", bufs=1, align_bytes=64)
             vcopy(
-                out=at[0][:].rearrange("p (c i) j -> p c j i", i=4),
-                in_=da[g][:].rearrange("p j (c i) -> p c j i", i=4),
+                out=at[g][:].rearrange("p (t m j) -> p m j t", t=PACK, j=PACK),
+                in_=da[g][:].rearrange("p (j m t) -> p m j t", j=PACK, t=PACK),
             )
 
-        def da_quantize(g):
-            ac[g] = pool.tile([PART, G], U32, name="ac", tag="ac", bufs=GROUPS, align_bytes=64)
-            asc[g] = pool.tile([PART, G], U8, name="asc", tag="asc", bufs=GROUPS, align_bytes=64)
-            dgc[g] = pool.tile([PART, GROUP], U32, name="dgc", tag="dgc", bufs=2, align_bytes=64)
-            dgs[g] = pool.tile([PART, GROUP], U8, name="dgs", tag="dgs", bufs=2, align_bytes=64)
-            nc.vector.quantize_mx(out=dgc[g][:].bitcast(E5), scales=dgs[g][:], in_=dag[g][:].rearrange("p n k -> p (n k)"))
-            nc.vector.quantize_mx(out=ac[g][:].bitcast(E5), scales=asc[g][:], in_=at[0][:].rearrange("p n k -> p (n k)"))
+        def at_quantize(g):
+            atq[g] = mx_pair("atq", G, GROUPS)
+            quantize(atq[g], E5, at[g][:])
 
-        for g in range(GROUPS):
-            da[g] = pool.tile([PART, PACK, G], F32, name="da", tag="da", bufs=1)
-            mask(g, 0, 4, 0, 32, 96)
-            mask(g, 0, 0, 32, 128, 0)
-            dh_tile(g, 2)
-            mask(g, 1, 0, 0, 32, 96)
-            mask(g, 1, 1, 32, 128, 0)
-            dh_tile(g, 3)
-            mask(g, 2, 1, 0, 32, 96)
-            mask(g, 2, 2, 32, 128, 0)
-            mask(g, 3, 2, 0, 32, 96)
-            mask(g, 3, 3, 32, 128, 0)
-            da_transposes(g, 0)
-            da_transposes(g, 1)
-            dp_index(4 * g - 2)
-            da_transposes(g, 2)
-            da_transposes(g, 3)
-            dp_index(4 * g - 1)
-            if g == 0:
-                load_a(2)
-                load_x(3)
-                for s in range(4):
-                    w0_transposes(s)
-                da_cast(0)
-                quantize_chunk(0, 0)
-                quantize_chunk(0, 1)
-                da_quantize(0)
-            if g == 1:
-                load_a(3)
-                load_p(1)
-            if g == 2:
-                load_p(2)
-                load_p(3)
-            if g < 3:
-                dy_half(g + 1, 0)
-                dy_half(g + 1, 1)
-                dy_transposes(g + 1)
-            if g == 0:
-                load_y(3)
-                w0_quantize(0)
-                w0_quantize(1)
-            else:
-                da_cast(g)
-                if g == 2:
-                    quantize_chunk(2, 2)
-                if g == 3:
-                    quantize_chunk(3, 2)
-                    interleave(1, 0, vcopy)
-                da_quantize(g)
-            if g < 3:
-                dp_index(4 * g)
-                dy_quantize(g + 1)
-                if g > 0:
-                    interleave(g + 1, 2, vcopy)
-                for s in (4, 0, 1):
-                    dh_tile(g + 1, s)
-                dp_index(4 * g + 1)
-
-        seq = ["tp", "dh", "dh", "dh", "tp", "tp", "acc", "acc", "dh", "dh", "dh", "tp"]
-        dw_bank = {}
-
-        def dw_pass(i, g):
-            c, r = divmod(i, 4)
-            if g == 0:
-                dw_bank[i] = bank(seq[i])
-            nc.tensor.matmul_mx(
-                out=dw_bank[i][:],
-                lhsT=ic[g, c][:, 128 * r : 128 * (r + 1)].bitcast(E4),
-                lhsT_scale=isc[g, c][:, 128 * r : 128 * (r + 1)],
-                rhs=ac[g][:].bitcast(E5),
-                rhs_scale=asc[g][:],
-                start=(g == 0),
-                stop=(g == GROUPS - 1),
+        def da_turn(g, u):
+            if u == 0:
+                dag[g] = pool.tile([PART, ROW], BF16, name="dag", tag="dag", bufs=1, align_bytes=64)
+            words = at[g][:].bitcast(F32)
+            tp = bank("scalar")
+            for t in range(PACK):
+                nc.tensor.transpose(tp[:, PART * t : PART * (t + 1)], words[:, 256 * t + u : 256 * (t + 1) : 2], ident[:])
+            scopy(
+                out=dag[g][:, 1024 * u : 1024 * (u + 1)].rearrange("p (e r t) -> p e r t", e=2, t=PACK),
+                in_=tp[:].bitcast(BF16).rearrange("p (t r e) -> p e r t", t=PACK, e=2),
             )
 
-        def dw_out(i, copy):
-            if i % 4 == 0:
-                ob_t[1] = pool.tile([PART, 4, G], F32, name="wb", tag="ob", bufs=4)
-            wb = ob_t[1][:, i % 4, :]
-            copy(out=wb.rearrange("p (m t) -> p m t", t=4), in_=dw_bank[i][:].rearrange("p (t m) -> p m t", t=4))
-            nc.sync.dma_start(out=out_1[128 * i : 128 * (i + 1), :], in_=wb)
+        def dag_quantize(g):
+            dagq[g] = mx_pair("dagq", PASS, 2)
+            quantize(dagq[g], E5, dag[g][:])
 
-        interleave(3, 0, scopy)
-        for i in range(8, 12):
-            for g in range(3):
-                dw_pass(i, g)
-        interleave(2, 0, vcopy)
-        quantize_chunk(1, 0)
-        dp_index(12)
-        for i in range(8, 12):
-            dw_pass(i, 3)
-        dp_index(13)
-        interleave(1, 1, vcopy)
-        quantize_chunk(2, 0)
-        quantize_chunk(3, 0)
-        dw_out(8, scopy)
-        dw_out(9, scopy)
-        dw_out(10, vcopy)
-        dw_out(11, vcopy)
-        for i in range(4):
-            for g in range(4):
-                dw_pass(i, g)
-            if i < 2:
-                dp_index(14 + i)
-        interleave(2, 1, vcopy)
-        interleave(3, 1, scopy)
-        red = pool.tile([PART, 4], F32, name="red")
-        red_col = pool.tile([PART, 4], F32, name="red_col")
-        nc.vector.tensor_reduce(
-            out=red[:], in_=c_bank[:].rearrange("p (t n) -> p t n", t=4), axis=mybir.AxisListType.X, op=ALU.add
+        def dp_tile(g, i, copy=scopy):
+            if g < 0:
+                return
+            j, n = divmod(i, 2)
+            if i == 0:
+                ob[g] = pool.tile([PART, PACK, P_IN], F32, name="ob", tag="wide_q" if g == LAST else "wide_%d" % g)
+            acc = bank("scalar")
+            mx_pass(acc, dagq[g], E5, PART * j, w0q, E4, 512 * n)
+            copy(out=ob[g][:, j, 512 * n : 512 * (n + 1)], in_=acc[:])
+
+        def store_dp(g, s):
+            nc.sync.dma_start(out=o_dram[g][:, 2 * s : 2 * s + 2, :], in_=ob[g][:, 2 * s : 2 * s + 2, :])
+
+        staged, inq = {}, {}
+
+        def interleave(g, c, copy, lo=0, hi=512):
+            src = x_t[g][:, :, lo:hi] if c == 2 else p_t[g][:, :, 512 * c + lo : 512 * c + hi]
+            if lo == 0:
+                staged[g, c] = stage_tile()
+            copy(
+                out=staged[g, c][:, PACK * lo : PACK * hi].rearrange("p (c i j) -> p c j i", i=4, j=PACK),
+                in_=src.rearrange("p j (c i) -> p c j i", i=4),
+            )
+
+        def inp_quantize(g, c, lo=0, hi=512):
+            if lo == 0:
+                inq[g, c] = mx_pair("inq", 512, 8)
+            quantize(inq[g, c], E4, staged[g, c][:, PACK * lo : PACK * hi], lo)
+
+        dw, wb = {}, {}
+
+        def dw_pass(c, r, g, tag):
+            if g == 0:
+                dw[c, r] = bank(tag)
+            mx_pass(dw[c, r], inq[g, c], E4, PART * r, atq[g], E5, 0, start=(g == 0), stop=(g == LAST))
+
+        def dw_out(c, r, copy):
+            if r == 0:
+                wb[c] = pool.tile([PART, PACK, G], F32, name="wb", tag={2: "da", 0: "da", 1: "wide_0"}[c], bufs={2: 2, 0: 2, 1: 1}[c])
+            copy(
+                out=wb[c][:, r, :].rearrange("p (m t) -> p m t", t=PACK), in_=dw[c, r][:].rearrange("p (t m) -> p m t", t=PACK)
+            )
+
+        def store_dw(c, lo, hi):
+            rows = out_1[512 * c : 512 * (c + 1), :].rearrange("(r p) w -> p r w", p=PART)
+            nc.sync.dma_start(out=rows[:, lo:hi, :], in_=wb[c][:, lo:hi, :])
+
+        for h in range(2):
+            nc.scalar.dma_start(out=q_all[h:PART:2, :, ROW - ROLL : ROW], in_=gr_half[1 - h][:, :, 0:ROLL])
+        w1_raw = stage_tile()
+        nc.sync.dma_start(out=w1_raw[:], in_=W1[0:G, :].rearrange("(m t) k -> m (t k)", t=PACK))
+        load_qy(0, 0, 1024)
+        load_qy(0, 1024, ROW)
+        w0_raw = pool.tile([PART, 2 * ROW], BF16, name="w0_raw", tag="wide_2")
+        nc.sync.dma_start(
+            out=w0_raw[:].rearrange("p (n w) -> p n w", n=2), in_=W0[0:P_IN, :].rearrange("(n m t) k -> m n (t k)", n=2, t=PACK)
         )
-        quantize_chunk(1, 1)
+        load_a(0, 0, 1024 + ROLL)
+        load_a(0, 1024 + ROLL, ROW)
+        load_qy(1)
+        load_x(0)
+        load_a(1)
+        load_x(1)
+
+        sum_bank = bank(7)
+        w1q = mx_pair("w1q", G, 1)
+        w0q = mx_pair("w0q", P_IN, 1)
+        w0_words = w0_raw[:].bitcast(F32)
+        w0_staged = {}
+
+        def w0_half(i):
+            n, s = divmod(i, 2)
+            if s == 0:
+                w0_staged[n] = stage_tile()
+            weight_half(w0_words[:, 1024 * n : 1024 * (n + 1)], w0_staged[n], s)
+
+        w1_staged = stage_tile()
+        for s in range(2):
+            weight_half(w1_raw[:].bitcast(F32), w1_staged, s)
+        dy_mask(0, 0)
+        dy_turn(0, 0)
+        quantize(w1q, E4, w1_staged[:])
+        dy_mask(0, 1)
+        load_qy(2)
+        dy_quantize(0, 0, 1024)
+        dy_turn(0, 1)
+        dh_pass(0, 0)
+        dh_pass(0, 1)
+        w0_half(0)
+        da_mask(0, 0)
+        dy_quantize(0, 1024, ROW)
+        dh_pass(0, 2)
+        da_mask(0, 1)
+        dh_pass(0, 3)
+        dh_pass(0, -1)
+        for s in (2, 3, -1):
+            da_mask(0, s)
+        load_x(2)
+        load_a(2)
+        for i in range(1, 4):
+            w0_half(i)
+        da_cast(0)
+        da_turn(0, 0)
+        da_turn(0, 1)
+        dy_mask(1, 0)
+        dy_turn(1, 0)
+        dy_mask(1, 1)
+        load_qy(3)
+        dy_turn(1, 1)
+        quantize(w0q, E4, w0_staged[0][:])
+        quantize(w0q, E4, w0_staged[1][:], 512)
+        dag_quantize(0)
+        dp_tile(0, 0)
+        dp_tile(0, 1)
+        dy_quantize(1)
+        at_quantize(0)
+
+        def group_head(g, fill):
+            for s in (-1, 0, 1):
+                dh_pass(g, s)
+            if g > 1:
+                da_turn(g - 1, 1)
+            else:
+                dp_tile(0, 2)
+                dp_tile(0, 3)
+            da_mask(g, -1)
+            dh_pass(g, 2)
+            da_mask(g, 0)
+            dh_pass(g, 3)
+            fill[0]()
+            for s in (1, 2, 3):
+                da_mask(g, s)
+            fill[1]()
+
+        def sums(g, slots):
+            for j in slots:
+                da_sums(g, j)
+
+        def tiles(g, which):
+            for i in which:
+                dp_tile(g, i)
+
+        group_head(1, (lambda: sums(0, (1, 0)), lambda: interleave(0, 2, scopy)))
+        load_a(3)
+        load_x(3)
+        nc.sync.dma_start(out=col_b[:], in_=col.partition_broadcast(PART))
+        load_p(0)
+        load_p(1)
+        load_p(2)
+        tiles(0, (4,))
+        sums(0, (2, 3))
+        dy_mask(2, 0)
+        tiles(0, (5,))
+        dy_turn(2, 0)
+        tiles(0, (6,))
+        dy_mask(2, 1)
+        sums(1, (0,))
+        dy_turn(2, 1)
+        tiles(0, (7,))
+        da_cast(1)
+        sums(1, (1, 2))
+        da_turn(1, 0)
+        interleave(1, 2, scopy)
+        inp_quantize(0, 2)
+        dy_quantize(2)
+        at_quantize(1)
+        group_head(2, (lambda: sums(1, (3,)), lambda: interleave(2, 2, scopy)))
+        sums(2, (0, 1))
+        dy_mask(3, 0)
+        dag_quantize(1)
+        dy_turn(3, 0)
+        tiles(1, (0, 1))
+        dy_mask(3, 1)
+        load_p(3)
+        store_dp(0, 0)
+        store_dp(0, 1)
+        sums(2, (2,))
+        dy_turn(3, 1)
+        tiles(1, (2,))
+        da_cast(2)
+        sums(2, (3,))
+        tiles(1, (3,))
+        da_turn(2, 0)
+        tiles(1, (4,))
+        inp_quantize(1, 2)
+        dy_quantize(3)
+        at_quantize(2)
+        group_head(3, (lambda: tiles(1, (5, 6)), lambda: sums(3, (0, 1))))
+        tiles(1, (7,))
+        store_dp(1, 0)
+        store_dp(1, 1)
+        held = rings["vector"]
+        red = pool.tile([PART, PACK], F32, name="red")
+        red_col = pool.tile([PART, PACK], F32, name="red_col")
+        dag_quantize(2)
+        da_cast(LAST)
+        inp_quantize(2, 2)
+        sums(3, (2, 3))
+        tiles(2, (0, 1, 2))
+        at_quantize(LAST)
+        interleave(3, 2, vcopy)
+        nc.vector.tensor_reduce(
+            out=red[:], in_=sum_bank[:].rearrange("p (t n) -> p t n", t=PACK), axis=mybir.AxisListType.X, op=ALU.add
+        )
+        inp_quantize(3, 2)
         nc.vector.tensor_scalar(out=red_col[:], in0=red[:], scalar1=col_b[:, 0:1], scalar2=None, op0=ALU.mult)
-        last_bank = bank("c")
-        for t in range(4):
-            nc.tensor.transpose(
-                last_bank[:, 128 * t : 128 * (t + 1)], red_col[:, t : t + 1].to_broadcast([PART, PART]), ident[:]
-            )
-        quantize_chunk(2, 1)
-        dw_out(0, vcopy)
-        quantize_chunk(3, 1)
-        dw_out(1, scopy)
-        dw_out(2, vcopy)
-        dw_out(3, scopy)
+        interleave(0, 0, vcopy)
+        tiles(2, (3,))
+        store_dp(2, 0)
+        da_turn(LAST, 0)
+        da_turn(LAST, 1)
+        for r in range(3):
+            tiles(2, (4 + r,))
+            for g in range(LAST):
+                dw_pass(2, r, g, held[r])
+        tiles(2, (7,))
+        store_dp(2, 1)
+        for r in range(3):
+            dw_pass(2, r, LAST, held[r])
+        inp_quantize(0, 0)
+        dag_quantize(LAST)
+        interleave(1, 0, vcopy)
+        last_bank = bank(7)
+        for t in range(PACK):
+            nc.tensor.transpose(last_bank[:, PART * t : PART * (t + 1)], red_col[:, t : t + 1].to_broadcast([PART, PART]), ident[:])
         row = pool.tile([1, G], F32, name="row")
-        scopy(out=row[:].rearrange("p (m t) -> p m t", t=4), in_=last_bank[0:1, :].rearrange("p (t m) -> p m t", t=4))
-        nc.sync.dma_start(out=out_1[C_OUT : C_OUT + 1, :], in_=row[:])
-        for g in range(4):
-            for i in range(4, 8):
-                dw_pass(i, g)
-        for i in range(4, 8):
-            dw_out(i, scopy if i % 2 == 0 else vcopy)
+        dw_out(2, 0, scopy)
+        dw_out(2, 1, scopy)
+        scopy(out=row[:], in_=last_bank[0:1, :])
+        dw_out(2, 2, scopy)
+        store_dw(2, 0, 3)
+        nc.sync.dma_start(out=out_1[C_IN : C_IN + 1, :], in_=row[:])
+        tiles(LAST, (0, 1, 2, 3))
+        store_dp(LAST, 0)
+        interleave(2, 0, vcopy)
+        inp_quantize(1, 0)
+        for r in range(2):
+            dw_pass(0, r, 0, held[r])
+        for g in range(GROUPS):
+            dw_pass(2, 3, g, 7)
+        dw_pass(0, 2, 0, held[2])
+        tiles(LAST, (4, 5))
+        for r in range(3):
+            dw_pass(0, r, 1, held[r])
+        tiles(LAST, (6, 7))
+        store_dp(LAST, 1)
+        dw_out(2, 3, scopy)
+        store_dw(2, 3, 4)
+        interleave(3, 0, vcopy)
+        inp_quantize(2, 0)
+        interleave(0, 1, vcopy)
+        inp_quantize(3, 0)
+        interleave(2, 1, scopy)
+        for r in range(3):
+            dw_pass(0, r, 2, held[r])
+        for g in range(LAST):
+            dw_pass(0, 3, g, 7)
+        for r in range(4):
+            dw_pass(0, r, LAST, None)
+        for r in range(4):
+            dw_out(0, r, scopy)
+            if r % 2:
+                store_dw(0, r - 1, r + 1)
+        interleave(1, 1, vcopy)
+        inp_quantize(0, 1)
+        interleave(3, 1, vcopy, 0, 256)
+        inp_quantize(1, 1)
+        interleave(3, 1, vcopy, 256, 512)
+        inp_quantize(2, 1)
+        inp_quantize(3, 1, 0, 256)
+        inp_quantize(3, 1, 256, 512)
+        for g in range(2):
+            for r in range(4):
+                dw_pass(1, r, g, rings["scalar"][r])
+        for r in range(4):
+            dw_pass(1, r, 2, None)
+            dw_pass(1, r, 3, None)
+            dw_out(1, r, vcopy if r % 2 else scopy)
+            store_dw(1, r, r + 1)

@@ -49,13 +49,13 @@ def tile_capsuleneuralnetwork_pa_v_kernel(
 
         rings = {"vector": [0, 1, 2], "scalar": [3, 4, 5, 6]}
 
-        def bank(which):
+        def bank(which, dtype=F32):
             if which in rings:
                 ring = rings[which]
                 which = ring[0]
                 ring.remove(which)
                 ring.append(which)
-            return psum.tile([PART, 512], F32, name="bank%d" % which, tag="bank%d" % which, bufs=1)
+            return psum.tile([PART, 512 if dtype == F32 else 1024], dtype, name="bank%d" % which, tag="bank%d" % which, bufs=1)
 
         def mx_pair(name, width, bufs):
             codes = pool.tile([PART, width], U32, name=name + "_c", tag=name + "_c", bufs=bufs, align_bytes=64)
@@ -79,6 +79,8 @@ def tile_capsuleneuralnetwork_pa_v_kernel(
 
         ident = pool.tile([PART, PART], F32, name="ident")
         make_identity(nc, ident[:])
+        ident_bf = pool.tile([PART, PART], BF16, name="ident_bf")
+        make_identity(nc, ident_bf[:])
         col_b = pool.tile([PART, 1], BF16, name="col_b")
 
         ctx.enter_context(tc.manual_schedule())
@@ -201,13 +203,19 @@ def tile_capsuleneuralnetwork_pa_v_kernel(
         def da_turn(g, u):
             if u == 0:
                 dag[g] = pool.tile([PART, ROW], BF16, name="dag", tag="dag", bufs=1, align_bytes=64)
-            words = at[g][:].bitcast(F32)
-            tp = bank("scalar")
-            for t in range(PACK):
-                nc.tensor.transpose(tp[:, PART * t : PART * (t + 1)], words[:, 256 * t + u : 256 * (t + 1) : 2], ident[:])
+            tp = bank("scalar", BF16)
+            for e in range(2):
+                for t in range(PACK):
+                    nc.tensor.matmul(
+                        out=tp[:, PART * (PACK * e + t) : PART * (PACK * e + t + 1)],
+                        lhsT=at[g][:, 512 * t + 2 * u + e : 512 * (t + 1) : PACK],
+                        rhs=ident_bf[:],
+                        start=True,
+                        stop=True,
+                    )
             scopy(
                 out=dag[g][:, 1024 * u : 1024 * (u + 1)].rearrange("p (e r t) -> p e r t", e=2, t=PACK),
-                in_=tp[:].bitcast(BF16).rearrange("p (t r e) -> p e r t", t=PACK, e=2),
+                in_=tp[:].rearrange("p (e t r) -> p e r t", t=PACK, e=2),
             )
 
         def dag_quantize(g):

@@ -24,6 +24,8 @@ GROUPS = N // PASS
 ROLL = 128
 ROW = PACK * F
 LAST = GROUPS - 1
+WRAP = -1
+X_CHUNK = 2
 
 
 def tile_capsuleneuralnetwork_pa_v_kernel(
@@ -47,15 +49,17 @@ def tile_capsuleneuralnetwork_pa_v_kernel(
         pool = ctx.enter_context(tc.tile_pool(name="pool", bufs=1))
         psum = ctx.enter_context(tc.psum_pool(name="psum", bufs=1))
 
-        rings = {"vector": [0, 1, 2], "scalar": [3, 4, 5, 6]}
+        free_banks = list(range(8))
+        filled = {}
 
-        def bank(which, dtype=F32):
-            if which in rings:
-                ring = rings[which]
-                which = ring[0]
-                ring.remove(which)
-                ring.append(which)
-            return psum.tile([PART, 512 if dtype == F32 else 1024], dtype, name="bank%d" % which, tag="bank%d" % which, bufs=1)
+        def take_bank(key, dtype=F32):
+            k = free_banks.pop(0)
+            tile = psum.tile([PART, 512 if dtype == F32 else 1024], dtype, name="bank%d" % k, tag="bank%d" % k, bufs=1)
+            filled[key] = (k, tile)
+            return tile
+
+        def give_bank(key):
+            free_banks.append(filled.pop(key)[0])
 
         def mx_pair(name, width, bufs):
             codes = pool.tile([PART, width], U32, name=name + "_c", tag=name + "_c", bufs=bufs, align_bytes=64)
@@ -88,12 +92,12 @@ def tile_capsuleneuralnetwork_pa_v_kernel(
         q_all = pool.tile([PART, GROUPS, ROW], BF16, name="q_all", tag="wide_q")
         y_t, a_t, p_t, x_t = {}, {}, {}, {}
 
-        def load_qy(g, lo=0, hi=ROW):
+        def load_qy(g, lo=0, hi=PACK):
             if lo == 0:
                 y_t[g] = pool.tile([PART, ROW], F32, name="y_sb", tag="ring_y", bufs=2)
-            q_hi = min(hi, ROW - ROLL)
-            nc.sync.dma_start(out=q_all[:, g, lo:q_hi], in_=gr_rows[g * PART : (g + 1) * PART, ROLL + lo : ROLL + q_hi])
-            nc.sync.dma_start(out=y_t[g][:, lo:hi], in_=y_dram[g].rearrange("p j w -> p (j w)")[:, lo:hi])
+            q_hi = min(F * hi, ROW - ROLL)
+            nc.sync.dma_start(out=q_all[:, g, F * lo : q_hi], in_=gr_rows[g * PART : (g + 1) * PART, ROLL + F * lo : ROLL + q_hi])
+            nc.sync.dma_start(out=y_t[g][:, F * lo : F * hi], in_=y_dram[g].rearrange("p j w -> p (j w)")[:, F * lo : F * hi])
 
         def load_a(g, lo=0, hi=ROW):
             if lo == 0:
@@ -111,83 +115,91 @@ def tile_capsuleneuralnetwork_pa_v_kernel(
         def stage_tile():
             return pool.tile([PART, ROW], BF16, name="stage", tag="stage", bufs=4, align_bytes=64)
 
-        def word_transposes(words, first):
-            tp = bank("scalar")
-            for i in range(2):
+        def word_transposes(key, words, first, count):
+            tp = take_bank(key)
+            for i in range(count):
                 for u in range(2):
                     lo = 256 * (first + i)
                     nc.tensor.transpose(tp[:, (2 * i + u) * PART : (2 * i + u + 1) * PART], words[:, lo + u : lo + 256 : 2], ident[:])
-            return tp
 
-        def weight_half(raw_words, staged, s):
-            tp = word_transposes(raw_words, 2 * s)
+        def weight_turn(raw, staged, s):
+            word_transposes("w", raw.bitcast(F32), 2 * s, 2)
             scopy(
                 out=staged[:].bitcast(F32).rearrange("p (m w) -> p m w", w=8)[:, :, 4 * s : 4 * s + 4],
-                in_=tp[:].rearrange("p (w m) -> p m w", w=4),
+                in_=filled["w"][1][:].rearrange("p (w m) -> p m w", w=4),
             )
+            give_bank("w")
 
-        dy, dyg, dyw, dyq, dywq, dh = ({} for i in range(6))
+        dy, dyg, dyw, dyq, dywq = ({} for i in range(5))
 
-        def dy_mask(g, s):
-            if s == 0:
-                dy[g] = pool.tile([PART, ROW], BF16, name="dy", tag="dy", bufs=1)
-            cols = slice(1024 * s, 1024 * (s + 1))
+        def dy_mask(g, lo, hi):
+            if lo == 0:
+                dy[g] = pool.tile([PART, ROW], BF16, name="dy", tag="dy", bufs=2)
+            cols = slice(F * lo, F * hi)
             nc.vector.scalar_tensor_tensor(
                 out=dy[g][:, cols], in0=y_t[g][:, cols], scalar=0.0, in1=q_all[:, g, cols], op0=ALU.is_gt, op1=ALU.mult
             )
 
-        def dy_turn(g, s):
-            if s == 0:
+        def dy_turn(g, lo, hi):
+            word_transposes(("dy", lo), dy[g][:].bitcast(F32), lo, hi - lo)
+
+        def dy_out(g, lo, hi):
+            if lo == 0:
                 dyg[g] = pool.tile([PART, ROW], BF16, name="dyg", tag="dyg", bufs=1, align_bytes=64)
-            tp = word_transposes(dy[g][:].bitcast(F32), 2 * s)
+            n = hi - lo
+            tp = filled["dy", lo][1]
             scopy(
-                out=dyg[g][:].bitcast(F32)[:, 512 * s : 512 * (s + 1)].rearrange("p (i r u) -> p i r u", i=2, u=2),
-                in_=tp[:].rearrange("p (i u r) -> p i r u", i=2, u=2),
+                out=dyg[g][:].bitcast(F32)[:, 256 * lo : 256 * hi].rearrange("p (i r u) -> p i r u", i=n, u=2),
+                in_=tp[:, 0 : 256 * n].rearrange("p (i u r) -> p i r u", i=n, u=2),
             )
-            if s == 1:
+            if hi == PACK:
                 dyw[g] = pool.tile([PART, PASS], BF16, name="dyw", tag="dyw", bufs=1, align_bytes=64)
                 scopy(
                     out=dyw[g][:].bitcast(F32).rearrange("p (b h u) -> p b h u", h=2, u=2),
-                    in_=tp[:, 256:512].rearrange("p (u b h) -> p b h u", u=2, h=2)[:, :, ::-1, :],
+                    in_=tp[:, 256 * (n - 1) : 256 * n].rearrange("p (u b h) -> p b h u", u=2, h=2)[:, :, ::-1, :],
                 )
+            give_bank(("dy", lo))
 
-        def dy_quantize(g, lo=0, hi=ROW):
+        def dy_quantize(g, lo, hi):
             if lo == 0:
                 dyq[g] = mx_pair("dyq", PASS, 2)
-            quantize(dyq[g], E5, dyg[g][:, lo:hi], lo // PACK)
-            if hi == ROW:
-                dywq[g] = mx_pair("dywq", PART, 2)
-                quantize(dywq[g], E5, dyw[g][:])
+            quantize(dyq[g], E5, dyg[g][:, F * lo : F * hi], PART * lo)
+
+        def dyw_quantize(g):
+            dywq[g] = mx_pair("dywq", PART, 2)
+            quantize(dywq[g], E5, dyw[g][:])
 
         def dh_pass(g, s):
-            dh[g, s] = bank("vector")
-            if s < 0:
-                mx_pass(dh[g, s], dywq[g], E5, 0, w1q, E4, 0)
+            out = take_bank(("dh", s))
+            if s == WRAP:
+                mx_pass(out, dywq[g], E5, 0, w1q, E4, 0)
             else:
-                mx_pass(dh[g, s], dyq[g], E5, PART * s, w1q, E4, 0)
+                mx_pass(out, dyq[g], E5, PART * s, w1q, E4, 0)
 
         da, at, atq, dag, dagq, ob = ({} for i in range(6))
 
         def da_mask(g, s):
-            if s == (0 if g == 0 else -1):
+            if g not in da:
                 da[g] = pool.tile([PART, ROW], F32, name="da", tag="da", bufs=2)
             lo, hi = max(0, G * s + ROLL), min(ROW, G * (s + 1) + ROLL)
             src = lo - (G * s + ROLL)
             nc.vector.scalar_tensor_tensor(
-                out=da[g][:, lo:hi], in0=a_t[g][:, lo:hi], scalar=0.0, in1=dh[g, s][:, src : src + hi - lo],
+                out=da[g][:, lo:hi], in0=a_t[g][:, lo:hi], scalar=0.0, in1=filled["dh", s][1][:, src : src + hi - lo],
                 op0=ALU.is_gt, op1=ALU.mult,
             )
+            give_bank(("dh", s))
 
-        def da_sums(g, j):
-            for t in range(PACK):
-                nc.tensor.matmul(
-                    out=sum_bank[:, PART * t : PART * (t + 1)],
-                    lhsT=da[g][:, G * j + PART * t : G * j + PART * (t + 1)],
-                    rhs=ident[:],
-                    is_transpose=True,
-                    start=(g == 0 and j == 1 and t == 0),
-                    stop=(g == LAST and j == PACK - 1 and t == PACK - 1),
-                )
+        def da_sums(g, slots):
+            for j in slots:
+                for t in range(PACK):
+                    nc.tensor.matmul(
+                        out=sum_bank[:, PART * t : PART * (t + 1)],
+                        lhsT=da[g][:, G * j + PART * t : G * j + PART * (t + 1)],
+                        rhs=ident[:],
+                        is_transpose=True,
+                        start=(g == 0 and j == 0 and t == 0),
+                        stop=(g == LAST and j == PACK - 1 and t == PACK - 1),
+                    )
 
         def da_cast(g):
             at[g] = pool.tile([PART, ROW], BF16, name="at", tag="at", bufs=1, align_bytes=64)
@@ -201,9 +213,7 @@ def tile_capsuleneuralnetwork_pa_v_kernel(
             quantize(atq[g], E5, at[g][:])
 
         def da_turn(g, u):
-            if u == 0:
-                dag[g] = pool.tile([PART, ROW], BF16, name="dag", tag="dag", bufs=1, align_bytes=64)
-            tp = bank("scalar", BF16)
+            tp = take_bank(("da", u), BF16)
             for e in range(2):
                 for t in range(PACK):
                     nc.tensor.matmul(
@@ -213,32 +223,44 @@ def tile_capsuleneuralnetwork_pa_v_kernel(
                         start=True,
                         stop=True,
                     )
+
+        def da_out(g, u):
+            if u == 0:
+                dag[g] = pool.tile([PART, ROW], BF16, name="dag", tag="dag", bufs=1, align_bytes=64)
             scopy(
                 out=dag[g][:, 1024 * u : 1024 * (u + 1)].rearrange("p (e r t) -> p e r t", e=2, t=PACK),
-                in_=tp[:].rearrange("p (e t r) -> p e r t", t=PACK, e=2),
+                in_=filled["da", u][1][:].rearrange("p (e t r) -> p e r t", t=PACK, e=2),
             )
+            give_bank(("da", u))
 
-        def dag_quantize(g):
-            dagq[g] = mx_pair("dagq", PASS, 2)
-            quantize(dagq[g], E5, dag[g][:])
+        def dag_quantize(g, lo=0, hi=2):
+            if lo == 0:
+                dagq[g] = mx_pair("dagq", PASS, 2)
+            quantize(dagq[g], E5, dag[g][:, 1024 * lo : 1024 * hi], 256 * lo)
 
-        def dp_tile(g, i, copy=scopy):
-            if g < 0:
-                return
+        def dp_pass(g, i):
             j, n = divmod(i, 2)
-            if i == 0:
+            mx_pass(take_bank(("dp", i)), dagq[g], E5, PART * j, w0q, E4, 512 * n)
+
+        def dp_out(g, i, copy=scopy):
+            j, n = divmod(i, 2)
+            if g not in ob:
                 ob[g] = pool.tile([PART, PACK, P_IN], F32, name="ob", tag="wide_q" if g == LAST else "wide_%d" % g)
-            acc = bank("scalar")
-            mx_pass(acc, dagq[g], E5, PART * j, w0q, E4, 512 * n)
-            copy(out=ob[g][:, j, 512 * n : 512 * (n + 1)], in_=acc[:])
+            copy(out=ob[g][:, j, 512 * n : 512 * (n + 1)], in_=filled["dp", i][1][:])
+            give_bank(("dp", i))
+
+        def dp_tiles(g, which):
+            for i in which:
+                dp_pass(g, i)
+                dp_out(g, i)
 
         def store_dp(g, s):
             nc.sync.dma_start(out=o_dram[g][:, 2 * s : 2 * s + 2, :], in_=ob[g][:, 2 * s : 2 * s + 2, :])
 
-        staged, inq = {}, {}
+        staged, inq, wb = {}, {}, {}
 
         def interleave(g, c, copy, lo=0, hi=512):
-            src = x_t[g][:, :, lo:hi] if c == 2 else p_t[g][:, :, 512 * c + lo : 512 * c + hi]
+            src = x_t[g][:, :, lo:hi] if c == X_CHUNK else p_t[g][:, :, 512 * c + lo : 512 * c + hi]
             if lo == 0:
                 staged[g, c] = stage_tile()
             copy(
@@ -251,19 +273,19 @@ def tile_capsuleneuralnetwork_pa_v_kernel(
                 inq[g, c] = mx_pair("inq", 512, 8)
             quantize(inq[g, c], E4, staged[g, c][:, PACK * lo : PACK * hi], lo)
 
-        dw, wb = {}, {}
-
-        def dw_pass(c, r, g, tag):
+        def dw_pass(c, r, g):
             if g == 0:
-                dw[c, r] = bank(tag)
-            mx_pass(dw[c, r], inq[g, c], E4, PART * r, atq[g], E5, 0, start=(g == 0), stop=(g == LAST))
+                take_bank(("dw", c, r))
+            mx_pass(filled["dw", c, r][1], inq[g, c], E4, PART * r, atq[g], E5, 0, start=(g == 0), stop=(g == LAST))
 
-        def dw_out(c, r, copy):
-            if r == 0:
-                wb[c] = pool.tile([PART, PACK, G], F32, name="wb", tag={2: "da", 0: "da", 1: "wide_0"}[c], bufs={2: 2, 0: 2, 1: 1}[c])
+        def dw_out(c, r, copy=scopy):
+            if c not in wb:
+                wb[c] = pool.tile([PART, PACK, G], F32, name="wb", tag="wide_0" if c == 1 else "da", bufs=1 if c == 1 else 2)
             copy(
-                out=wb[c][:, r, :].rearrange("p (m t) -> p m t", t=PACK), in_=dw[c, r][:].rearrange("p (t m) -> p m t", t=PACK)
+                out=wb[c][:, r, :].rearrange("p (m t) -> p m t", t=PACK),
+                in_=filled["dw", c, r][1][:].rearrange("p (t m) -> p m t", t=PACK),
             )
+            give_bank(("dw", c, r))
 
         def store_dw(c, lo, hi):
             rows = out_1[512 * c : 512 * (c + 1), :].rearrange("(r p) w -> p r w", p=PART)
@@ -273,231 +295,173 @@ def tile_capsuleneuralnetwork_pa_v_kernel(
             nc.scalar.dma_start(out=q_all[h:PART:2, :, ROW - ROLL : ROW], in_=gr_half[1 - h][:, :, 0:ROLL])
         w1_raw = stage_tile()
         nc.sync.dma_start(out=w1_raw[:], in_=W1[0:G, :].rearrange("(m t) k -> m (t k)", t=PACK))
-        load_qy(0, 0, 1024)
-        load_qy(0, 1024, ROW)
+        load_qy(0, 0, 2)
+        load_qy(0, 2, 4)
+        load_qy(1, 0, 2)
+        load_qy(1, 2, 4)
+        load_a(0, 0, 1024 + ROLL)
+        load_a(0, 1024 + ROLL, ROW)
+
+        sum_bank = take_bank("sum")
+        w1q = mx_pair("w1q", G, 1)
+        w0q = mx_pair("w0q", P_IN, 1)
+        w1_staged = stage_tile()
         w0_raw = pool.tile([PART, 2 * ROW], BF16, name="w0_raw", tag="wide_2")
+        w0_staged = [stage_tile(), stage_tile()]
+
+        def w0_turn(i):
+            n, s = divmod(i, 2)
+            weight_turn(w0_raw[:, ROW * n : ROW * (n + 1)], w0_staged[n], s)
+
+        def dy_half(g, s):
+            dy_mask(g, 2 * s, 2 * s + 2)
+            dy_turn(g, 2 * s, 2 * s + 2)
+            dy_out(g, 2 * s, 2 * s + 2)
+
+        for s in range(2):
+            weight_turn(w1_raw[:], w1_staged, s)
+        dy_half(0, 0)
+        quantize(w1q, E4, w1_staged[:])
+        dy_half(0, 1)
+        load_qy(2)
+        load_a(1)
         nc.sync.dma_start(
             out=w0_raw[:].rearrange("p (n w) -> p n w", n=2), in_=W0[0:P_IN, :].rearrange("(n m t) k -> m n (t k)", n=2, t=PACK)
         )
-        load_a(0, 0, 1024 + ROLL)
-        load_a(0, 1024 + ROLL, ROW)
-        load_qy(1)
-        load_x(0)
-        load_a(1)
-        load_x(1)
-
-        sum_bank = bank(7)
-        w1q = mx_pair("w1q", G, 1)
-        w0q = mx_pair("w0q", P_IN, 1)
-        w0_words = w0_raw[:].bitcast(F32)
-        w0_staged = {}
-
-        def w0_half(i):
-            n, s = divmod(i, 2)
-            if s == 0:
-                w0_staged[n] = stage_tile()
-            weight_half(w0_words[:, 1024 * n : 1024 * (n + 1)], w0_staged[n], s)
-
-        w1_staged = stage_tile()
-        for s in range(2):
-            weight_half(w1_raw[:].bitcast(F32), w1_staged, s)
-        dy_mask(0, 0)
-        dy_turn(0, 0)
-        quantize(w1q, E4, w1_staged[:])
-        dy_mask(0, 1)
-        load_qy(2)
-        dy_quantize(0, 0, 1024)
-        dy_turn(0, 1)
-        dh_pass(0, 0)
-        dh_pass(0, 1)
-        w0_half(0)
-        da_mask(0, 0)
-        dy_quantize(0, 1024, ROW)
-        dh_pass(0, 2)
-        da_mask(0, 1)
-        dh_pass(0, 3)
-        dh_pass(0, -1)
-        for s in (2, 3, -1):
-            da_mask(0, s)
-        load_x(2)
-        load_a(2)
-        for i in range(1, 4):
-            w0_half(i)
-        da_cast(0)
-        da_turn(0, 0)
-        da_turn(0, 1)
-        dy_mask(1, 0)
-        dy_turn(1, 0)
-        dy_mask(1, 1)
+        dy_mask(1, 0, 2)
+        dy_quantize(0, 0, 4)
+        dyw_quantize(0)
+        dy_turn(1, 0, 2)
+        dy_out(1, 0, 2)
+        for s in range(3):
+            dh_pass(0, s)
+        dy_half(1, 1)
         load_qy(3)
-        dy_turn(1, 1)
-        quantize(w0q, E4, w0_staged[0][:])
-        quantize(w0q, E4, w0_staged[1][:], 512)
-        dag_quantize(0)
-        dp_tile(0, 0)
-        dp_tile(0, 1)
-        dy_quantize(1)
-        at_quantize(0)
 
-        def group_head(g, fill):
-            for s in (-1, 0, 1):
-                dh_pass(g, s)
-            if g > 1:
-                da_turn(g - 1, 1)
-            else:
-                dp_tile(0, 2)
-                dp_tile(0, 3)
-            da_mask(g, -1)
-            dh_pass(g, 2)
+        for g in range(GROUPS):
+            if g >= 2:
+                dp_tiles(g - 2, (0, 1))
             da_mask(g, 0)
             dh_pass(g, 3)
-            fill[0]()
-            for s in (1, 2, 3):
+            if g >= 2:
+                dp_tiles(g - 2, (2,))
+            da_mask(g, 1)
+            dh_pass(g, WRAP)
+            if g >= 2:
+                dp_tiles(g - 2, (3, 4, 5, 6, 7))
+            for s in (2, 3, WRAP):
                 da_mask(g, s)
-            fill[1]()
+            if g == 0:
+                load_a(2)
+            if g == 1:
+                load_a(3)
+                for k in range(GROUPS):
+                    load_x(k)
+                nc.sync.dma_start(out=col_b[:], in_=col.partition_broadcast(PART))
+                load_p(0)
+                load_p(1)
+                load_p(2)
+                for i in range(4):
+                    w0_turn(i)
+            if g < LAST:
+                dy_quantize(g + 1, 0, 4)
+            da_cast(g)
+            if g > 0:
+                dag_quantize(g - 1)
+            da_sums(g, (0, 1))
+            if g == 2:
+                store_dp(0, 0)
+                store_dp(0, 1)
+            for u in range(2):
+                da_turn(g, u)
+                da_out(g, u)
+            da_sums(g, (2, 3))
+            if g < LAST:
+                dyw_quantize(g + 1)
+            if g == 1:
+                quantize(w0q, E4, w0_staged[0][:])
+                quantize(w0q, E4, w0_staged[1][:], 512)
+            if g < 2:
+                dy_half(g + 2, 0)
+            if g == 2:
+                interleave(0, X_CHUNK, vcopy)
+            if g < LAST:
+                dh_pass(g + 1, 0)
+                dh_pass(g + 1, 1)
+            if g < 2:
+                dy_half(g + 2, 1)
+            if g == 1:
+                load_p(3)
+            if g < LAST:
+                dh_pass(g + 1, 2)
+            at_quantize(g)
+            if g == 2:
+                inp_quantize(0, X_CHUNK)
 
-        def sums(g, slots):
-            for j in slots:
-                da_sums(g, j)
-
-        def tiles(g, which):
-            for i in which:
-                dp_tile(g, i)
-
-        group_head(1, (lambda: sums(0, (1, 0)), lambda: interleave(0, 2, scopy)))
-        load_a(3)
-        load_x(3)
-        nc.sync.dma_start(out=col_b[:], in_=col.partition_broadcast(PART))
-        load_p(0)
-        load_p(1)
-        load_p(2)
-        tiles(0, (4,))
-        sums(0, (2, 3))
-        dy_mask(2, 0)
-        tiles(0, (5,))
-        dy_turn(2, 0)
-        tiles(0, (6,))
-        dy_mask(2, 1)
-        sums(1, (0,))
-        dy_turn(2, 1)
-        tiles(0, (7,))
-        da_cast(1)
-        sums(1, (1, 2))
-        da_turn(1, 0)
-        interleave(1, 2, scopy)
-        inp_quantize(0, 2)
-        dy_quantize(2)
-        at_quantize(1)
-        group_head(2, (lambda: sums(1, (3,)), lambda: interleave(2, 2, scopy)))
-        sums(2, (0, 1))
-        dy_mask(3, 0)
-        dag_quantize(1)
-        dy_turn(3, 0)
-        tiles(1, (0, 1))
-        dy_mask(3, 1)
-        load_p(3)
-        store_dp(0, 0)
-        store_dp(0, 1)
-        sums(2, (2,))
-        dy_turn(3, 1)
-        tiles(1, (2,))
-        da_cast(2)
-        sums(2, (3,))
-        tiles(1, (3,))
-        da_turn(2, 0)
-        tiles(1, (4,))
-        inp_quantize(1, 2)
-        dy_quantize(3)
-        at_quantize(2)
-        group_head(3, (lambda: tiles(1, (5, 6)), lambda: sums(3, (0, 1))))
-        tiles(1, (7,))
         store_dp(1, 0)
         store_dp(1, 1)
-        held = rings["vector"]
+        interleave(1, X_CHUNK, vcopy)
         red = pool.tile([PART, PACK], F32, name="red")
         red_col = pool.tile([PART, PACK], F32, name="red_col")
-        dag_quantize(2)
-        da_cast(LAST)
-        inp_quantize(2, 2)
-        sums(3, (2, 3))
-        tiles(2, (0, 1, 2))
-        at_quantize(LAST)
-        interleave(3, 2, vcopy)
         nc.vector.tensor_reduce(
             out=red[:], in_=sum_bank[:].rearrange("p (t n) -> p t n", t=PACK), axis=mybir.AxisListType.X, op=ALU.add
         )
-        inp_quantize(3, 2)
+        give_bank("sum")
+        inp_quantize(1, X_CHUNK)
         nc.vector.tensor_scalar(out=red_col[:], in0=red[:], scalar1=col_b[:, 0:1], scalar2=None, op0=ALU.mult)
-        interleave(0, 0, vcopy)
-        tiles(2, (3,))
-        store_dp(2, 0)
-        da_turn(LAST, 0)
-        da_turn(LAST, 1)
-        for r in range(3):
-            tiles(2, (4 + r,))
-            for g in range(LAST):
-                dw_pass(2, r, g, held[r])
-        tiles(2, (7,))
-        store_dp(2, 1)
-        for r in range(3):
-            dw_pass(2, r, LAST, held[r])
-        inp_quantize(0, 0)
+        interleave(2, X_CHUNK, vcopy)
         dag_quantize(LAST)
-        interleave(1, 0, vcopy)
-        last_bank = bank(7)
+        inp_quantize(2, X_CHUNK)
+        interleave(3, X_CHUNK, vcopy)
+        interleave(0, 0, vcopy)
+        inp_quantize(3, X_CHUNK)
+        for g in range(2):
+            for r in range(4):
+                dp_tiles(2, (4 * g + r,))
+                dw_pass(X_CHUNK, r, g)
+            store_dp(2, g)
+        last_bank = take_bank("row")
         for t in range(PACK):
             nc.tensor.transpose(last_bank[:, PART * t : PART * (t + 1)], red_col[:, t : t + 1].to_broadcast([PART, PART]), ident[:])
         row = pool.tile([1, G], F32, name="row")
-        dw_out(2, 0, scopy)
-        dw_out(2, 1, scopy)
         scopy(out=row[:], in_=last_bank[0:1, :])
-        dw_out(2, 2, scopy)
-        store_dw(2, 0, 3)
-        nc.sync.dma_start(out=out_1[C_IN : C_IN + 1, :], in_=row[:])
-        tiles(LAST, (0, 1, 2, 3))
-        store_dp(LAST, 0)
-        interleave(2, 0, vcopy)
-        inp_quantize(1, 0)
-        for r in range(2):
-            dw_pass(0, r, 0, held[r])
-        for g in range(GROUPS):
-            dw_pass(2, 3, g, 7)
-        dw_pass(0, 2, 0, held[2])
-        tiles(LAST, (4, 5))
-        for r in range(3):
-            dw_pass(0, r, 1, held[r])
-        tiles(LAST, (6, 7))
-        store_dp(LAST, 1)
-        dw_out(2, 3, scopy)
-        store_dw(2, 3, 4)
-        interleave(3, 0, vcopy)
-        inp_quantize(2, 0)
-        interleave(0, 1, vcopy)
-        inp_quantize(3, 0)
-        interleave(2, 1, scopy)
-        for r in range(3):
-            dw_pass(0, r, 2, held[r])
-        for g in range(LAST):
-            dw_pass(0, 3, g, 7)
-        for r in range(4):
-            dw_pass(0, r, LAST, None)
-        for r in range(4):
-            dw_out(0, r, scopy)
-            if r % 2:
-                store_dw(0, r - 1, r + 1)
-        interleave(1, 1, vcopy)
-        inp_quantize(0, 1)
-        interleave(3, 1, vcopy, 0, 256)
-        inp_quantize(1, 1)
-        interleave(3, 1, vcopy, 256, 512)
-        inp_quantize(2, 1)
-        inp_quantize(3, 1, 0, 256)
-        inp_quantize(3, 1, 256, 512)
+        give_bank("row")
         for g in range(2):
             for r in range(4):
-                dw_pass(1, r, g, rings["scalar"][r])
+                dp_tiles(LAST, (4 * g + r,))
+                dw_pass(X_CHUNK, r, 2 + g)
+            store_dp(LAST, g)
+        for g in range(GROUPS):
+            if g < LAST:
+                interleave(g + 1, 0, vcopy)
+            else:
+                interleave(0, 1, vcopy)
+            inp_quantize(g, 0)
         for r in range(4):
-            dw_pass(1, r, 2, None)
-            dw_pass(1, r, 3, None)
+            dw_pass(0, r, 0)
+            dw_out(X_CHUNK, r)
+        store_dw(X_CHUNK, 0, 4)
+        nc.sync.dma_start(out=out_1[C_IN : C_IN + 1, :], in_=row[:])
+        interleave(1, 1, scopy)
+        for r in range(4):
+            dw_pass(0, r, 1)
+        for r in range(4):
+            dw_pass(0, r, 2)
+            dw_pass(0, r, 3)
+            dw_out(0, r)
+            if r % 2:
+                store_dw(0, r - 1, r + 1)
+        interleave(2, 1, vcopy)
+        inp_quantize(0, 1)
+        interleave(3, 1, vcopy)
+        inp_quantize(1, 1)
+        inp_quantize(2, 1)
+        inp_quantize(3, 1)
+        for g in range(2):
+            for r in range(4):
+                dw_pass(1, r, g)
+        for r in range(4):
+            dw_pass(1, r, 2)
+            dw_pass(1, r, 3)
             dw_out(1, r, vcopy if r % 2 else scopy)
             store_dw(1, r, r + 1)

@@ -25,6 +25,9 @@ ROLL = 128
 ROW = PACK * F
 LAST = GROUPS - 1
 WRAP = -1
+PLAIN_DY = 0
+PLAIN_W1 = False
+PLAIN_W0 = 2
 X_CHUNK = 2
 
 
@@ -109,8 +112,10 @@ def tile_capsuleneuralnetwork_pa_v_kernel(
             nc.sync.dma_start(out=p_t[g][:], in_=p_dram[g])
 
         def load_x(g):
-            x_t[g] = pool.tile([PART, PACK, F], BF16, name="x_sb", tag="x_sb", bufs=GROUPS)
-            nc.sync.dma_start(out=x_t[g][:], in_=x_dram[g])
+            pair = pool.tile([PART, 2, ROW], BF16, name="x_sb", tag="x_sb", bufs=2)
+            nc.sync.dma_start(out=pair[:], in_=x_dram[g : g + 2].rearrange("g p j w -> p g (j w)"))
+            for k in range(2):
+                x_t[g + k] = pair[:, k, :].rearrange("p (j w) -> p j w", j=PACK)
 
         def stage_tile():
             return pool.tile([PART, ROW], BF16, name="stage", tag="stage", bufs=4, align_bytes=64)
@@ -122,12 +127,32 @@ def tile_capsuleneuralnetwork_pa_v_kernel(
                     lo = 256 * (first + i)
                     nc.tensor.transpose(tp[:, (2 * i + u) * PART : (2 * i + u + 1) * PART], words[:, lo + u : lo + 256 : 2], ident[:])
 
-        def weight_turn(raw, staged, s):
-            word_transposes("w", raw.bitcast(F32), 2 * s, 2)
-            scopy(
-                out=staged[:].bitcast(F32).rearrange("p (m w) -> p m w", w=8)[:, :, 4 * s : 4 * s + 4],
-                in_=filled["w"][1][:].rearrange("p (w m) -> p m w", w=4),
-            )
+        def identity_turns(key, rows, first, count):
+            tp = take_bank(key, BF16)
+            for i in range(count):
+                for t in range(PACK):
+                    lo = 512 * (first + i)
+                    nc.tensor.matmul(
+                        out=tp[:, PART * (PACK * i + t) : PART * (PACK * i + t + 1)],
+                        lhsT=rows[:, lo + t : lo + 512 : PACK],
+                        rhs=ident_bf[:],
+                        start=True,
+                        stop=True,
+                    )
+
+        def weight_turn(raw, staged, s, plain):
+            if plain:
+                identity_turns("w", raw, 2 * s, 2)
+                scopy(
+                    out=staged[:].rearrange("p (m w) -> p m w", w=16)[:, :, 8 * s : 8 * s + 8],
+                    in_=filled["w"][1][:].rearrange("p (w m) -> p m w", w=8),
+                )
+            else:
+                word_transposes("w", raw.bitcast(F32), 2 * s, 2)
+                scopy(
+                    out=staged[:].bitcast(F32).rearrange("p (m w) -> p m w", w=8)[:, :, 4 * s : 4 * s + 4],
+                    in_=filled["w"][1][:].rearrange("p (w m) -> p m w", w=4),
+                )
             give_bank("w")
 
         dy, dyg, dyw, dyq, dywq = ({} for i in range(5))
@@ -141,13 +166,29 @@ def tile_capsuleneuralnetwork_pa_v_kernel(
             )
 
         def dy_turn(g, lo, hi):
-            word_transposes(("dy", lo), dy[g][:].bitcast(F32), lo, hi - lo)
+            if g < PLAIN_DY:
+                identity_turns(("dy", lo), dy[g][:], lo, hi - lo)
+            else:
+                word_transposes(("dy", lo), dy[g][:].bitcast(F32), lo, hi - lo)
 
         def dy_out(g, lo, hi):
             if lo == 0:
                 dyg[g] = pool.tile([PART, ROW], BF16, name="dyg", tag="dyg", bufs=1, align_bytes=64)
             n = hi - lo
             tp = filled["dy", lo][1]
+            if g < PLAIN_DY:
+                scopy(
+                    out=dyg[g][:, F * lo : F * hi].rearrange("p (i r t) -> p i r t", i=n, t=PACK),
+                    in_=tp[:, 0 : F * n].rearrange("p (i t r) -> p i r t", i=n, t=PACK),
+                )
+                if hi == PACK:
+                    dyw[g] = pool.tile([PART, PASS], BF16, name="dyw", tag="dyw", bufs=1, align_bytes=64)
+                    scopy(
+                        out=dyw[g][:].rearrange("p (b h t) -> p b h t", h=2, t=PACK),
+                        in_=tp[:, F * (n - 1) : F * n].rearrange("p (t b h) -> p b h t", t=PACK, h=2)[:, :, ::-1, :],
+                    )
+                give_bank(("dy", lo))
+                return
             scopy(
                 out=dyg[g][:].bitcast(F32)[:, 256 * lo : 256 * hi].rearrange("p (i r u) -> p i r u", i=n, u=2),
                 in_=tp[:, 0 : 256 * n].rearrange("p (i u r) -> p i r u", i=n, u=2),
@@ -254,8 +295,8 @@ def tile_capsuleneuralnetwork_pa_v_kernel(
                 dp_pass(g, i)
                 dp_out(g, i)
 
-        def store_dp(g, s):
-            nc.sync.dma_start(out=o_dram[g][:, 2 * s : 2 * s + 2, :], in_=ob[g][:, 2 * s : 2 * s + 2, :])
+        def store_dp(g, lo=0, hi=PACK):
+            nc.sync.dma_start(out=o_dram[g][:, lo:hi, :], in_=ob[g][:, lo:hi, :])
 
         staged, inq, wb = {}, {}, {}
 
@@ -293,6 +334,7 @@ def tile_capsuleneuralnetwork_pa_v_kernel(
 
         for h in range(2):
             nc.scalar.dma_start(out=q_all[h:PART:2, :, ROW - ROLL : ROW], in_=gr_half[1 - h][:, :, 0:ROLL])
+        nc.scalar.dma_start(out=col_b[:], in_=col.partition_broadcast(PART))
         w1_raw = stage_tile()
         nc.sync.dma_start(out=w1_raw[:], in_=W1[0:G, :].rearrange("(m t) k -> m (t k)", t=PACK))
         load_qy(0, 0, 2)
@@ -301,17 +343,20 @@ def tile_capsuleneuralnetwork_pa_v_kernel(
         load_qy(1, 2, 4)
         load_a(0, 0, 1024 + ROLL)
         load_a(0, 1024 + ROLL, ROW)
+        w0_raw = pool.tile([PART, 2 * ROW], BF16, name="w0_raw", tag="wide_2")
+        nc.sync.dma_start(
+            out=w0_raw[:].rearrange("p (n w) -> p n w", n=2), in_=W0[0:P_IN, :].rearrange("(n m t) k -> m n (t k)", n=2, t=PACK)
+        )
 
         sum_bank = take_bank("sum")
         w1q = mx_pair("w1q", G, 1)
         w0q = mx_pair("w0q", P_IN, 1)
         w1_staged = stage_tile()
-        w0_raw = pool.tile([PART, 2 * ROW], BF16, name="w0_raw", tag="wide_2")
         w0_staged = [stage_tile(), stage_tile()]
 
         def w0_turn(i):
             n, s = divmod(i, 2)
-            weight_turn(w0_raw[:, ROW * n : ROW * (n + 1)], w0_staged[n], s)
+            weight_turn(w0_raw[:, ROW * n : ROW * (n + 1)], w0_staged[n], s, i < PLAIN_W0)
 
         def dy_half(g, s):
             dy_mask(g, 2 * s, 2 * s + 2)
@@ -319,15 +364,13 @@ def tile_capsuleneuralnetwork_pa_v_kernel(
             dy_out(g, 2 * s, 2 * s + 2)
 
         for s in range(2):
-            weight_turn(w1_raw[:], w1_staged, s)
+            weight_turn(w1_raw[:], w1_staged, s, PLAIN_W1)
         dy_half(0, 0)
         quantize(w1q, E4, w1_staged[:])
         dy_half(0, 1)
-        load_qy(2)
+        load_qy(2, 0, 2)
+        load_qy(2, 2, 4)
         load_a(1)
-        nc.sync.dma_start(
-            out=w0_raw[:].rearrange("p (n w) -> p n w", n=2), in_=W0[0:P_IN, :].rearrange("(n m t) k -> m n (t k)", n=2, t=PACK)
-        )
         dy_mask(1, 0, 2)
         dy_quantize(0, 0, 4)
         dyw_quantize(0)
@@ -335,102 +378,97 @@ def tile_capsuleneuralnetwork_pa_v_kernel(
         dy_out(1, 0, 2)
         for s in range(3):
             dh_pass(0, s)
-        dy_half(1, 1)
+        dy_mask(1, 2, 4)
         load_qy(3)
 
         for g in range(GROUPS):
-            if g >= 2:
-                dp_tiles(g - 2, (0, 1))
             da_mask(g, 0)
             dh_pass(g, 3)
-            if g >= 2:
-                dp_tiles(g - 2, (2,))
             da_mask(g, 1)
             dh_pass(g, WRAP)
-            if g >= 2:
-                dp_tiles(g - 2, (3, 4, 5, 6, 7))
+            if g == 0:
+                dy_turn(1, 2, 4)
+                dy_out(1, 2, 4)
+            if g >= 1:
+                dag_quantize(g - 1)
+                dp_tiles(g - 1, range(6))
             for s in (2, 3, WRAP):
                 da_mask(g, s)
             if g == 0:
                 load_a(2)
+                load_x(0)
+                for i in range(4):
+                    w0_turn(i)
             if g == 1:
                 load_a(3)
-                for k in range(GROUPS):
-                    load_x(k)
-                nc.sync.dma_start(out=col_b[:], in_=col.partition_broadcast(PART))
+                load_x(2)
                 load_p(0)
                 load_p(1)
                 load_p(2)
-                for i in range(4):
-                    w0_turn(i)
+            if 0 < g < LAST:
+                dyw_quantize(g + 1)
+            da_cast(g)
             if g < LAST:
                 dy_quantize(g + 1, 0, 4)
-            da_cast(g)
-            if g > 0:
-                dag_quantize(g - 1)
-            da_sums(g, (0, 1))
-            if g == 2:
-                store_dp(0, 0)
-                store_dp(0, 1)
+            if g == 0:
+                dyw_quantize(g + 1)
             for u in range(2):
                 da_turn(g, u)
                 da_out(g, u)
-            da_sums(g, (2, 3))
+            if g >= 1:
+                dp_tiles(g - 1, (6, 7))
             if g < LAST:
-                dyw_quantize(g + 1)
-            if g == 1:
-                quantize(w0q, E4, w0_staged[0][:])
-                quantize(w0q, E4, w0_staged[1][:], 512)
+                for s in range(3):
+                    dh_pass(g + 1, s)
+            da_sums(g, (0, 1, 2, 3))
             if g < 2:
                 dy_half(g + 2, 0)
             if g == 2:
                 interleave(0, X_CHUNK, vcopy)
-            if g < LAST:
-                dh_pass(g + 1, 0)
-                dh_pass(g + 1, 1)
             if g < 2:
                 dy_half(g + 2, 1)
             if g == 1:
                 load_p(3)
-            if g < LAST:
-                dh_pass(g + 1, 2)
-            at_quantize(g)
+                store_dp(0)
             if g == 2:
+                store_dp(1)
+            at_quantize(g)
+            if g == 0:
+                quantize(w0q, E4, w0_staged[0][:])
+                quantize(w0q, E4, w0_staged[1][:], 512)
+            if g == 2:
+                interleave(1, X_CHUNK, vcopy)
                 inp_quantize(0, X_CHUNK)
 
-        store_dp(1, 0)
-        store_dp(1, 1)
-        interleave(1, X_CHUNK, vcopy)
+        store_dp(2)
+        inp_quantize(1, X_CHUNK)
+        interleave(2, X_CHUNK, vcopy)
+        for g in range(2):
+            for r in range(4):
+                dw_pass(X_CHUNK, r, g)
+        interleave(0, 0, scopy)
+        interleave(3, X_CHUNK, vcopy)
+        inp_quantize(2, X_CHUNK)
+        dag_quantize(LAST)
         red = pool.tile([PART, PACK], F32, name="red")
         red_col = pool.tile([PART, PACK], F32, name="red_col")
         nc.vector.tensor_reduce(
             out=red[:], in_=sum_bank[:].rearrange("p (t n) -> p t n", t=PACK), axis=mybir.AxisListType.X, op=ALU.add
         )
         give_bank("sum")
-        inp_quantize(1, X_CHUNK)
-        nc.vector.tensor_scalar(out=red_col[:], in0=red[:], scalar1=col_b[:, 0:1], scalar2=None, op0=ALU.mult)
-        interleave(2, X_CHUNK, vcopy)
-        dag_quantize(LAST)
-        inp_quantize(2, X_CHUNK)
-        interleave(3, X_CHUNK, vcopy)
-        interleave(0, 0, vcopy)
         inp_quantize(3, X_CHUNK)
+        nc.vector.tensor_scalar(out=red_col[:], in0=red[:], scalar1=col_b[:, 0:1], scalar2=None, op0=ALU.mult)
         for g in range(2):
             for r in range(4):
-                dp_tiles(2, (4 * g + r,))
-                dw_pass(X_CHUNK, r, g)
-            store_dp(2, g)
+                dp_tiles(LAST, (4 * g + r,))
+                dw_pass(X_CHUNK, r, 2 + g)
+            store_dp(LAST, 2 * g, 2 * g + 2)
         last_bank = take_bank("row")
         for t in range(PACK):
             nc.tensor.transpose(last_bank[:, PART * t : PART * (t + 1)], red_col[:, t : t + 1].to_broadcast([PART, PART]), ident[:])
         row = pool.tile([1, G], F32, name="row")
         scopy(out=row[:], in_=last_bank[0:1, :])
         give_bank("row")
-        for g in range(2):
-            for r in range(4):
-                dp_tiles(LAST, (4 * g + r,))
-                dw_pass(X_CHUNK, r, 2 + g)
-            store_dp(LAST, g)
         for g in range(GROUPS):
             if g < LAST:
                 interleave(g + 1, 0, vcopy)
@@ -442,7 +480,7 @@ def tile_capsuleneuralnetwork_pa_v_kernel(
             dw_out(X_CHUNK, r)
         store_dw(X_CHUNK, 0, 4)
         nc.sync.dma_start(out=out_1[C_IN : C_IN + 1, :], in_=row[:])
-        interleave(1, 1, scopy)
+        interleave(3, 1, scopy)
         for r in range(4):
             dw_pass(0, r, 1)
         for r in range(4):
@@ -451,9 +489,9 @@ def tile_capsuleneuralnetwork_pa_v_kernel(
             dw_out(0, r)
             if r % 2:
                 store_dw(0, r - 1, r + 1)
-        interleave(2, 1, vcopy)
+        interleave(1, 1, vcopy)
         inp_quantize(0, 1)
-        interleave(3, 1, vcopy)
+        interleave(2, 1, vcopy)
         inp_quantize(1, 1)
         inp_quantize(2, 1)
         inp_quantize(3, 1)

@@ -89,15 +89,18 @@ def tile_capsuleneuralnetwork_pa_v_kernel(
         ident_bf = pool.tile([PART, PART], BF16, name="ident_bf")
         make_identity(nc, ident_bf[:])
         col_b = pool.tile([PART, 1], BF16, name="col_b")
+        red_col = pool.tile([PART, PART], F32, name="red_col")
+        nc.gpsimd.memset(red_col[:], 0.0)
 
         ctx.enter_context(tc.manual_schedule())
 
         q_all = pool.tile([PART, GROUPS, ROW], BF16, name="q_all", tag="wide_q")
         y_t, a_t, p_t, x_t = {}, {}, {}, {}
 
+        y_ring = pool.tile([PART, 2 * ROW], F32, name="y_ring", tag="wide_y")
+
         def load_qy(g, lo=0, hi=PACK):
-            if lo == 0:
-                y_t[g] = pool.tile([PART, ROW], F32, name="y_sb", tag="ring_y", bufs=2)
+            y_t[g] = y_ring[:, ROW * (g % 2) : ROW * (g % 2 + 1)]
             q_hi = min(F * hi, ROW - ROLL)
             nc.sync.dma_start(out=q_all[:, g, F * lo : q_hi], in_=gr_rows[g * PART : (g + 1) * PART, ROLL + F * lo : ROLL + q_hi])
             nc.sync.dma_start(out=y_t[g][:, F * lo : F * hi], in_=y_dram[g].rearrange("p j w -> p (j w)")[:, F * lo : F * hi])
@@ -108,14 +111,16 @@ def tile_capsuleneuralnetwork_pa_v_kernel(
             nc.sync.dma_start(out=a_t[g][:, lo:hi], in_=a_dram[g].rearrange("p j w -> p (j w)")[:, lo:hi])
 
         def load_p(g):
-            p_t[g] = pool.tile([PART, PACK, P_IN], BF16, name="p_sb", tag="ring_p" if g < 2 else "ring_y", bufs=2)
-            nc.sync.dma_start(out=p_t[g][:], in_=p_dram[g])
-
-        def load_x(g):
-            pair = pool.tile([PART, 2, ROW], BF16, name="x_sb", tag="x_sb", bufs=2)
-            nc.sync.dma_start(out=pair[:], in_=x_dram[g : g + 2].rearrange("g p j w -> p g (j w)"))
+            pair = pool.tile([PART, 2, PACK * P_IN], BF16, name="p_sb", tag="wide_p" if g < 2 else "wide_y")
+            nc.sync.dma_start(out=pair[:], in_=p_dram[g : g + 2].rearrange("g p j w -> p g (j w)"))
             for k in range(2):
-                x_t[g + k] = pair[:, k, :].rearrange("p (j w) -> p j w", j=PACK)
+                p_t[g + k] = pair[:, k, :].rearrange("p (j w) -> p j w", j=PACK)
+
+        def load_x():
+            x_all = pool.tile([PART, GROUPS, ROW], BF16, name="x_all")
+            nc.sync.dma_start(out=x_all[:], in_=x_dram.rearrange("g p j w -> p g (j w)"))
+            for g in range(GROUPS):
+                x_t[g] = x_all[:, g, :].rearrange("p (j w) -> p j w", j=PACK)
 
         def stage_tile():
             return pool.tile([PART, ROW], BF16, name="stage", tag="stage", bufs=4, align_bytes=64)
@@ -161,15 +166,26 @@ def tile_capsuleneuralnetwork_pa_v_kernel(
             if lo == 0:
                 dy[g] = pool.tile([PART, ROW], BF16, name="dy", tag="dy", bufs=2)
             cols = slice(F * lo, F * hi)
-            nc.vector.scalar_tensor_tensor(
-                out=dy[g][:, cols], in0=y_t[g][:, cols], scalar=0.0, in1=q_all[:, g, cols], op0=ALU.is_gt, op1=ALU.mult
-            )
+            for u in range(2):
+                nc.vector.scalar_tensor_tensor(
+                    out=dy[g][:, cols].rearrange("p (u w e) -> p u w e", u=2, e=2)[:, u],
+                    in0=y_t[g][:, cols].rearrange("p (w u e) -> p u w e", u=2, e=2)[:, u],
+                    scalar=0.0,
+                    in1=q_all[:, g, cols].rearrange("p (w u e) -> p u w e", u=2, e=2)[:, u],
+                    op0=ALU.is_gt,
+                    op1=ALU.mult,
+                )
 
         def dy_turn(g, lo, hi):
             if g < PLAIN_DY:
                 identity_turns(("dy", lo), dy[g][:], lo, hi - lo)
             else:
-                word_transposes(("dy", lo), dy[g][:].bitcast(F32), lo, hi - lo)
+                tp = take_bank(("dy", lo))
+                words = dy[g][:].bitcast(F32)
+                for i in range(2):
+                    for u in range(2):
+                        first = 256 * lo + PART * (2 * u + i)
+                        nc.tensor.transpose(tp[:, (2 * i + u) * PART : (2 * i + u + 1) * PART], words[:, first : first + PART], ident[:])
 
         def dy_out(g, lo, hi):
             if lo == 0:
@@ -390,21 +406,21 @@ def tile_capsuleneuralnetwork_pa_v_kernel(
                 dy_turn(1, 2, 4)
                 dy_out(1, 2, 4)
             if g >= 1:
+                da_sums(g - 1, (0, 1))
                 dag_quantize(g - 1)
-                dp_tiles(g - 1, range(6))
+                dp_tiles(g - 1, range(4))
+                da_sums(g - 1, (2, 3))
+                dp_tiles(g - 1, (4, 5))
             for s in (2, 3, WRAP):
                 da_mask(g, s)
             if g == 0:
                 load_a(2)
-                load_x(0)
+                load_x()
                 for i in range(4):
                     w0_turn(i)
             if g == 1:
                 load_a(3)
-                load_x(2)
                 load_p(0)
-                load_p(1)
-                load_p(2)
             if 0 < g < LAST:
                 dyw_quantize(g + 1)
             da_cast(g)
@@ -420,7 +436,8 @@ def tile_capsuleneuralnetwork_pa_v_kernel(
             if g < LAST:
                 for s in range(3):
                     dh_pass(g + 1, s)
-            da_sums(g, (0, 1, 2, 3))
+            if g == LAST:
+                da_sums(g, (0, 1, 2, 3))
             if g < 2:
                 dy_half(g + 2, 0)
             if g == 2:
@@ -428,7 +445,7 @@ def tile_capsuleneuralnetwork_pa_v_kernel(
             if g < 2:
                 dy_half(g + 2, 1)
             if g == 1:
-                load_p(3)
+                load_p(2)
                 store_dp(0)
             if g == 2:
                 store_dp(1)
@@ -451,23 +468,21 @@ def tile_capsuleneuralnetwork_pa_v_kernel(
         inp_quantize(2, X_CHUNK)
         dag_quantize(LAST)
         red = pool.tile([PART, PACK], F32, name="red")
-        red_col = pool.tile([PART, PACK], F32, name="red_col")
         nc.vector.tensor_reduce(
             out=red[:], in_=sum_bank[:].rearrange("p (t n) -> p t n", t=PACK), axis=mybir.AxisListType.X, op=ALU.add
         )
         give_bank("sum")
         inp_quantize(3, X_CHUNK)
-        nc.vector.tensor_scalar(out=red_col[:], in0=red[:], scalar1=col_b[:, 0:1], scalar2=None, op0=ALU.mult)
+        nc.vector.tensor_scalar(out=red_col[:, 0:PACK], in0=red[:], scalar1=col_b[:, 0:1], scalar2=None, op0=ALU.mult)
         for g in range(2):
             for r in range(4):
                 dp_tiles(LAST, (4 * g + r,))
                 dw_pass(X_CHUNK, r, 2 + g)
             store_dp(LAST, 2 * g, 2 * g + 2)
         last_bank = take_bank("row")
-        for t in range(PACK):
-            nc.tensor.transpose(last_bank[:, PART * t : PART * (t + 1)], red_col[:, t : t + 1].to_broadcast([PART, PART]), ident[:])
-        row = pool.tile([1, G], F32, name="row")
-        scopy(out=row[:], in_=last_bank[0:1, :])
+        nc.tensor.transpose(last_bank[:, 0:PART], red_col[:], ident[:])
+        row = pool.tile([PACK, PART], F32, name="row")
+        scopy(out=row[:], in_=last_bank[0:PACK, 0:PART])
         give_bank("row")
         for g in range(GROUPS):
             if g < LAST:
@@ -479,7 +494,7 @@ def tile_capsuleneuralnetwork_pa_v_kernel(
             dw_pass(0, r, 0)
             dw_out(X_CHUNK, r)
         store_dw(X_CHUNK, 0, 4)
-        nc.sync.dma_start(out=out_1[C_IN : C_IN + 1, :], in_=row[:])
+        nc.sync.dma_start(out=out_1[C_IN : C_IN + 1, :].rearrange("o (t m) -> (o t) m", t=PACK), in_=row[:])
         interleave(3, 1, scopy)
         for r in range(4):
             dw_pass(0, r, 1)

@@ -25,6 +25,7 @@ ROLL = 128
 ROW = PACK * F
 LAST = GROUPS - 1
 WRAP = -1
+LINE = 256
 PLAIN_DY = 0
 PLAIN_W1 = False
 PLAIN_W0 = 2
@@ -65,8 +66,8 @@ def tile_capsuleneuralnetwork_pa_v_kernel(
             free_banks.append(filled.pop(key)[0])
 
         def mx_pair(name, width, bufs):
-            codes = pool.tile([PART, width], U32, name=name + "_c", tag=name + "_c", bufs=bufs, align_bytes=64)
-            scales = pool.tile([PART, width], U8, name=name + "_s", tag=name + "_s", bufs=bufs, align_bytes=64)
+            codes = pool.tile([PART, width], U32, name=name + "_c", tag=name + "_c", bufs=bufs, align_bytes=LINE)
+            scales = pool.tile([PART, width], U8, name=name + "_s", tag=name + "_s", bufs=bufs, align_bytes=LINE)
             return codes, scales
 
         def quantize(pair, fmt, src, lo=0):
@@ -94,10 +95,10 @@ def tile_capsuleneuralnetwork_pa_v_kernel(
 
         ctx.enter_context(tc.manual_schedule())
 
-        q_all = pool.tile([PART, GROUPS, ROW], BF16, name="q_all", tag="wide_q")
+        q_all = pool.tile([PART, GROUPS, ROW], BF16, name="q_all", tag="wide_q", align_bytes=LINE)
         y_t, a_t, p_t, x_t = {}, {}, {}, {}
 
-        y_ring = pool.tile([PART, 2 * ROW], F32, name="y_ring", tag="wide_y")
+        y_ring = pool.tile([PART, 2 * ROW], F32, name="y_ring", tag="wide_y", align_bytes=LINE)
 
         def load_qy(g, lo=0, hi=PACK):
             y_t[g] = y_ring[:, ROW * (g % 2) : ROW * (g % 2 + 1)]
@@ -107,23 +108,23 @@ def tile_capsuleneuralnetwork_pa_v_kernel(
 
         def load_a(g, lo=0, hi=ROW):
             if lo == 0:
-                a_t[g] = pool.tile([PART, ROW], F32, name="a_sb", tag="ring_a", bufs=2)
+                a_t[g] = pool.tile([PART, ROW], F32, name="a_sb", tag="ring_a", bufs=2, align_bytes=LINE)
             nc.sync.dma_start(out=a_t[g][:, lo:hi], in_=a_dram[g].rearrange("p j w -> p (j w)")[:, lo:hi])
 
         def load_p(g):
-            pair = pool.tile([PART, 2, PACK * P_IN], BF16, name="p_sb", tag="wide_p" if g < 2 else "wide_y")
+            pair = pool.tile([PART, 2, PACK * P_IN], BF16, name="p_sb", tag="wide_p" if g < 2 else "wide_y", align_bytes=LINE)
             nc.sync.dma_start(out=pair[:], in_=p_dram[g : g + 2].rearrange("g p j w -> p g (j w)"))
             for k in range(2):
                 p_t[g + k] = pair[:, k, :].rearrange("p (j w) -> p j w", j=PACK)
 
         def load_x():
-            x_all = pool.tile([PART, GROUPS, ROW], BF16, name="x_all")
+            x_all = pool.tile([PART, GROUPS, ROW], BF16, name="x_all", align_bytes=LINE)
             nc.sync.dma_start(out=x_all[:], in_=x_dram.rearrange("g p j w -> p g (j w)"))
             for g in range(GROUPS):
                 x_t[g] = x_all[:, g, :].rearrange("p (j w) -> p j w", j=PACK)
 
         def stage_tile():
-            return pool.tile([PART, ROW], BF16, name="stage", tag="stage", bufs=4, align_bytes=64)
+            return pool.tile([PART, ROW], BF16, name="stage", tag="stage", bufs=4, align_bytes=LINE)
 
         def word_transposes(key, words, first, count):
             tp = take_bank(key)
@@ -166,30 +167,19 @@ def tile_capsuleneuralnetwork_pa_v_kernel(
             if lo == 0:
                 dy[g] = pool.tile([PART, ROW], BF16, name="dy", tag="dy", bufs=2)
             cols = slice(F * lo, F * hi)
-            for u in range(2):
-                nc.vector.scalar_tensor_tensor(
-                    out=dy[g][:, cols].rearrange("p (u w e) -> p u w e", u=2, e=2)[:, u],
-                    in0=y_t[g][:, cols].rearrange("p (w u e) -> p u w e", u=2, e=2)[:, u],
-                    scalar=0.0,
-                    in1=q_all[:, g, cols].rearrange("p (w u e) -> p u w e", u=2, e=2)[:, u],
-                    op0=ALU.is_gt,
-                    op1=ALU.mult,
-                )
+            nc.vector.scalar_tensor_tensor(
+                out=dy[g][:, cols], in0=y_t[g][:, cols], scalar=0.0, in1=q_all[:, g, cols], op0=ALU.is_gt, op1=ALU.mult
+            )
 
         def dy_turn(g, lo, hi):
             if g < PLAIN_DY:
                 identity_turns(("dy", lo), dy[g][:], lo, hi - lo)
             else:
-                tp = take_bank(("dy", lo))
-                words = dy[g][:].bitcast(F32)
-                for i in range(2):
-                    for u in range(2):
-                        first = 256 * lo + PART * (2 * u + i)
-                        nc.tensor.transpose(tp[:, (2 * i + u) * PART : (2 * i + u + 1) * PART], words[:, first : first + PART], ident[:])
+                word_transposes(("dy", lo), dy[g][:].bitcast(F32), lo, hi - lo)
 
         def dy_out(g, lo, hi):
             if lo == 0:
-                dyg[g] = pool.tile([PART, ROW], BF16, name="dyg", tag="dyg", bufs=1, align_bytes=64)
+                dyg[g] = pool.tile([PART, ROW], BF16, name="dyg", tag="dyg", bufs=1, align_bytes=LINE)
             n = hi - lo
             tp = filled["dy", lo][1]
             if g < PLAIN_DY:
@@ -198,7 +188,7 @@ def tile_capsuleneuralnetwork_pa_v_kernel(
                     in_=tp[:, 0 : F * n].rearrange("p (i t r) -> p i r t", i=n, t=PACK),
                 )
                 if hi == PACK:
-                    dyw[g] = pool.tile([PART, PASS], BF16, name="dyw", tag="dyw", bufs=1, align_bytes=64)
+                    dyw[g] = pool.tile([PART, PASS], BF16, name="dyw", tag="dyw", bufs=1, align_bytes=LINE)
                     scopy(
                         out=dyw[g][:].rearrange("p (b h t) -> p b h t", h=2, t=PACK),
                         in_=tp[:, F * (n - 1) : F * n].rearrange("p (t b h) -> p b h t", t=PACK, h=2)[:, :, ::-1, :],
@@ -210,7 +200,7 @@ def tile_capsuleneuralnetwork_pa_v_kernel(
                 in_=tp[:, 0 : 256 * n].rearrange("p (i u r) -> p i r u", i=n, u=2),
             )
             if hi == PACK:
-                dyw[g] = pool.tile([PART, PASS], BF16, name="dyw", tag="dyw", bufs=1, align_bytes=64)
+                dyw[g] = pool.tile([PART, PASS], BF16, name="dyw", tag="dyw", bufs=1, align_bytes=LINE)
                 scopy(
                     out=dyw[g][:].bitcast(F32).rearrange("p (b h u) -> p b h u", h=2, u=2),
                     in_=tp[:, 256 * (n - 1) : 256 * n].rearrange("p (u b h) -> p b h u", u=2, h=2)[:, :, ::-1, :],
@@ -237,7 +227,7 @@ def tile_capsuleneuralnetwork_pa_v_kernel(
 
         def da_mask(g, s):
             if g not in da:
-                da[g] = pool.tile([PART, ROW], F32, name="da", tag="da", bufs=2)
+                da[g] = pool.tile([PART, ROW], F32, name="da", tag="da", bufs=2, align_bytes=LINE)
             lo, hi = max(0, G * s + ROLL), min(ROW, G * (s + 1) + ROLL)
             src = lo - (G * s + ROLL)
             nc.vector.scalar_tensor_tensor(
@@ -259,7 +249,7 @@ def tile_capsuleneuralnetwork_pa_v_kernel(
                     )
 
         def da_cast(g):
-            at[g] = pool.tile([PART, ROW], BF16, name="at", tag="at", bufs=1, align_bytes=64)
+            at[g] = pool.tile([PART, ROW], BF16, name="at", tag="at", bufs=1, align_bytes=LINE)
             vcopy(
                 out=at[g][:].rearrange("p (t m j) -> p m j t", t=PACK, j=PACK),
                 in_=da[g][:].rearrange("p (j m t) -> p m j t", j=PACK, t=PACK),
@@ -283,7 +273,7 @@ def tile_capsuleneuralnetwork_pa_v_kernel(
 
         def da_out(g, u):
             if u == 0:
-                dag[g] = pool.tile([PART, ROW], BF16, name="dag", tag="dag", bufs=1, align_bytes=64)
+                dag[g] = pool.tile([PART, ROW], BF16, name="dag", tag="dag", bufs=1, align_bytes=LINE)
             scopy(
                 out=dag[g][:, 1024 * u : 1024 * (u + 1)].rearrange("p (e r t) -> p e r t", e=2, t=PACK),
                 in_=filled["da", u][1][:].rearrange("p (e t r) -> p e r t", t=PACK, e=2),
@@ -302,7 +292,7 @@ def tile_capsuleneuralnetwork_pa_v_kernel(
         def dp_out(g, i, copy=scopy):
             j, n = divmod(i, 2)
             if g not in ob:
-                ob[g] = pool.tile([PART, PACK, P_IN], F32, name="ob", tag="wide_q" if g == LAST else "wide_%d" % g)
+                ob[g] = pool.tile([PART, PACK, P_IN], F32, name="ob", tag="wide_q" if g == LAST else "wide_%d" % g, align_bytes=LINE)
             copy(out=ob[g][:, j, 512 * n : 512 * (n + 1)], in_=filled["dp", i][1][:])
             give_bank(("dp", i))
 
@@ -337,7 +327,7 @@ def tile_capsuleneuralnetwork_pa_v_kernel(
 
         def dw_out(c, r, copy=scopy):
             if c not in wb:
-                wb[c] = pool.tile([PART, PACK, G], F32, name="wb", tag="wide_0" if c == 1 else "da", bufs=1 if c == 1 else 2)
+                wb[c] = pool.tile([PART, PACK, G], F32, name="wb", tag="wide_0" if c == 1 else "da", bufs=1 if c == 1 else 2, align_bytes=LINE)
             copy(
                 out=wb[c][:, r, :].rearrange("p (m t) -> p m t", t=PACK),
                 in_=filled["dw", c, r][1][:].rearrange("p (t m) -> p m t", t=PACK),
@@ -359,7 +349,7 @@ def tile_capsuleneuralnetwork_pa_v_kernel(
         load_qy(1, 2, 4)
         load_a(0, 0, 1024 + ROLL)
         load_a(0, 1024 + ROLL, ROW)
-        w0_raw = pool.tile([PART, 2 * ROW], BF16, name="w0_raw", tag="wide_2")
+        w0_raw = pool.tile([PART, 2 * ROW], BF16, name="w0_raw", tag="wide_2", align_bytes=LINE)
         nc.sync.dma_start(
             out=w0_raw[:].rearrange("p (n w) -> p n w", n=2), in_=W0[0:P_IN, :].rearrange("(n m t) k -> m n (t k)", n=2, t=PACK)
         )

@@ -398,11 +398,13 @@ def tile_capsuleneuralnetwork_pa_v_kernel(
             if g >= 1:
                 da_sums(g - 1, (0, 1))
                 dag_quantize(g - 1)
-                dp_tiles(g - 1, range(4))
-                da_sums(g - 1, (2, 3))
-                dp_tiles(g - 1, (4, 5))
+                dp_tiles(g - 1, range(2))
             for s in (2, 3, WRAP):
                 da_mask(g, s)
+            if g >= 1:
+                dp_tiles(g - 1, (2, 3))
+                da_sums(g - 1, (2,))
+                dp_tiles(g - 1, (4, 5))
             if g == 0:
                 load_a(2)
                 load_x()
@@ -422,16 +424,21 @@ def tile_capsuleneuralnetwork_pa_v_kernel(
                 da_turn(g, u)
                 da_out(g, u)
             if g >= 1:
-                dp_tiles(g - 1, (6, 7))
+                da_sums(g - 1, (3,))
+                dp_tiles(g - 1, (6,))
             if g < LAST:
-                for s in range(3):
-                    dh_pass(g + 1, s)
-            if g == LAST:
-                da_sums(g, (0, 1, 2, 3))
+                dh_pass(g + 1, 0)
+                dh_pass(g + 1, 1)
             if g < 2:
                 dy_half(g + 2, 0)
             if g == 2:
                 interleave(0, X_CHUNK, vcopy)
+            if g >= 1:
+                dp_tiles(g - 1, (7,))
+            if g < LAST:
+                dh_pass(g + 1, 2)
+            if g == LAST:
+                da_sums(g, (0, 1, 2, 3))
             if g < 2:
                 dy_half(g + 2, 1)
             if g == 1:

@@ -47,7 +47,6 @@ def tile_capsuleneuralnetwork_pa_v_kernel(
     y_dram = by_group(y.rearrange("b t w -> (b t) w"))
     o_dram = by_group(out_0.rearrange("b (t w) -> (b t) w", t=T))
     gr_rows = grad_out.rearrange("b (h w) -> (b h) w", h=2)
-    gr_half = grad_out.rearrange("(g b) (h w) -> h b g w", b=PART // 2, h=2)
 
     with ExitStack() as ctx:
         pool = ctx.enter_context(tc.tile_pool(name="pool", bufs=1))
@@ -89,21 +88,22 @@ def tile_capsuleneuralnetwork_pa_v_kernel(
         make_identity(nc, ident[:])
         ident_bf = pool.tile([PART, PART], BF16, name="ident_bf")
         make_identity(nc, ident_bf[:])
-        col_b = pool.tile([PART, 1], BF16, name="col_b")
-        red_col = pool.tile([PART, PART], F32, name="red_col")
-        nc.gpsimd.memset(red_col[:], 0.0)
+        swap = pool.tile([PART, PART], BF16, name="swap")
+        col_b = pool.tile([PACK, 1], BF16, name="col_b")
+        red = pool.tile([PART, PART], F32, name="red")
+        nc.gpsimd.memset(red[:], 0.0)
 
         ctx.enter_context(tc.manual_schedule())
 
-        q_all = pool.tile([PART, GROUPS, ROW], BF16, name="q_all", tag="wide_q", align_bytes=LINE)
+        q_all = pool.tile([PART, GROUPS, ROW + ROLL], BF16, name="q_all", tag="wide_q", align_bytes=LINE)
         y_t, a_t, p_t, x_t = {}, {}, {}, {}
 
         y_ring = pool.tile([PART, 2 * ROW], F32, name="y_ring", tag="wide_y", align_bytes=LINE)
 
         def load_qy(g, lo=0, hi=PACK):
             y_t[g] = y_ring[:, ROW * (g % 2) : ROW * (g % 2 + 1)]
-            q_hi = min(F * hi, ROW - ROLL)
-            nc.sync.dma_start(out=q_all[:, g, F * lo : q_hi], in_=gr_rows[g * PART : (g + 1) * PART, ROLL + F * lo : ROLL + q_hi])
+            q_lo, q_hi = (F * lo + ROLL if lo else 0), min(F * hi + ROLL, ROW)
+            nc.sync.dma_start(out=q_all[:, g, q_lo:q_hi], in_=gr_rows[g * PART : (g + 1) * PART, q_lo:q_hi])
             nc.sync.dma_start(out=y_t[g][:, F * lo : F * hi], in_=y_dram[g].rearrange("p j w -> p (j w)")[:, F * lo : F * hi])
 
         def load_a(g, lo=0, hi=ROW):
@@ -168,8 +168,14 @@ def tile_capsuleneuralnetwork_pa_v_kernel(
                 dy[g] = pool.tile([PART, ROW], BF16, name="dy", tag="dy", bufs=2)
             cols = slice(F * lo, F * hi)
             nc.vector.scalar_tensor_tensor(
-                out=dy[g][:, cols], in0=y_t[g][:, cols], scalar=0.0, in1=q_all[:, g, cols], op0=ALU.is_gt, op1=ALU.mult
+                out=dy[g][:, cols], in0=y_t[g][:, cols], scalar=0.0, in1=q_all[:, g, F * lo + ROLL : F * hi + ROLL],
+                op0=ALU.is_gt, op1=ALU.mult,
             )
+
+        def q_swap(g):
+            nc.tensor.matmul(out=take_bank("q", BF16)[:, 0:ROLL], lhsT=swap[:], rhs=q_all[:, g, 0:ROLL], start=True, stop=True)
+            scopy(out=q_all[:, g, ROW : ROW + ROLL], in_=filled["q"][1][:, 0:ROLL])
+            give_bank("q")
 
         def dy_turn(g, lo, hi):
             if g < PLAIN_DY:
@@ -338,9 +344,7 @@ def tile_capsuleneuralnetwork_pa_v_kernel(
             rows = out_1[512 * c : 512 * (c + 1), :].rearrange("(r p) w -> p r w", p=PART)
             nc.sync.dma_start(out=rows[:, lo:hi, :], in_=wb[c][:, lo:hi, :])
 
-        for h in range(2):
-            nc.scalar.dma_start(out=q_all[h:PART:2, :, ROW - ROLL : ROW], in_=gr_half[1 - h][:, :, 0:ROLL])
-        nc.scalar.dma_start(out=col_b[:], in_=col.partition_broadcast(PART))
+        vcopy(out=swap[:].rearrange("p (b h) -> p b h", h=2), in_=ident_bf[:].rearrange("p (b h) -> p b h", h=2)[:, :, ::-1])
         w1_raw = stage_tile()
         nc.sync.dma_start(out=w1_raw[:], in_=W1[0:G, :].rearrange("(m t) k -> m (t k)", t=PACK))
         load_qy(0, 0, 2)
@@ -371,12 +375,14 @@ def tile_capsuleneuralnetwork_pa_v_kernel(
 
         for s in range(2):
             weight_turn(w1_raw[:], w1_staged, s, PLAIN_W1)
+        q_swap(0)
         dy_half(0, 0)
         quantize(w1q, E4, w1_staged[:])
         dy_half(0, 1)
         load_qy(2, 0, 2)
         load_qy(2, 2, 4)
         load_a(1)
+        q_swap(1)
         dy_mask(1, 0, 2)
         dy_quantize(0, 0, 4)
         dyw_quantize(0)
@@ -395,6 +401,8 @@ def tile_capsuleneuralnetwork_pa_v_kernel(
             if g == 0:
                 dy_turn(1, 2, 4)
                 dy_out(1, 2, 4)
+            if g == 1:
+                q_swap(3)
             if g >= 1:
                 da_sums(g - 1, (0, 1))
                 dag_quantize(g - 1)
@@ -409,9 +417,12 @@ def tile_capsuleneuralnetwork_pa_v_kernel(
                 load_a(2)
                 load_x()
                 for i in range(4):
+                    if i == 1:
+                        q_swap(2)
                     w0_turn(i)
             if g == 1:
                 load_a(3)
+                nc.sync.dma_start(out=col_b[:], in_=col.partition_broadcast(PACK))
                 load_p(0)
             if 0 < g < LAST:
                 dyw_quantize(g + 1)
@@ -464,24 +475,24 @@ def tile_capsuleneuralnetwork_pa_v_kernel(
         interleave(3, X_CHUNK, vcopy)
         inp_quantize(2, X_CHUNK)
         dag_quantize(LAST)
-        red = pool.tile([PART, PACK], F32, name="red")
         nc.vector.tensor_reduce(
-            out=red[:], in_=sum_bank[:].rearrange("p (t n) -> p t n", t=PACK), axis=mybir.AxisListType.X, op=ALU.add
+            out=red[:, 0:PACK], in_=sum_bank[:].rearrange("p (t n) -> p t n", t=PACK), axis=mybir.AxisListType.X, op=ALU.add
         )
         give_bank("sum")
         inp_quantize(3, X_CHUNK)
-        nc.vector.tensor_scalar(out=red_col[:, 0:PACK], in0=red[:], scalar1=col_b[:, 0:1], scalar2=None, op0=ALU.mult)
+        last_bank = take_bank("row")
+        nc.tensor.transpose(last_bank[:, 0:PART], red[:], ident[:])
+        row = pool.tile([PACK, PART], F32, name="row")
+        interleave(1, 0, vcopy)
+        nc.vector.tensor_scalar(out=row[:], in0=last_bank[0:PACK, 0:PART], scalar1=col_b[:], scalar2=None, op0=ALU.mult)
+        give_bank("row")
+        inp_quantize(0, 0)
         for g in range(2):
             for r in range(4):
                 dp_tiles(LAST, (4 * g + r,))
                 dw_pass(X_CHUNK, r, 2 + g)
             store_dp(LAST, 2 * g, 2 * g + 2)
-        last_bank = take_bank("row")
-        nc.tensor.transpose(last_bank[:, 0:PART], red_col[:], ident[:])
-        row = pool.tile([PACK, PART], F32, name="row")
-        scopy(out=row[:], in_=last_bank[0:PACK, 0:PART])
-        give_bank("row")
-        for g in range(GROUPS):
+        for g in range(1, GROUPS):
             if g < LAST:
                 interleave(g + 1, 0, vcopy)
             else:

@@ -21,15 +21,13 @@ PART = 128
 PACK = 4
 PASS = PART * PACK
 GROUPS = N // PASS
-ROLL = 128
-ROW = PACK * F
 LAST = GROUPS - 1
+ROW = PACK * F
+HALF = ROW // 2
+ROLL = 128
 WRAP = -1
-LINE = 256
-PLAIN_DY = 0
-PLAIN_W1 = False
-PLAIN_W0 = 2
 X_CHUNK = 2
+LINE = 256
 
 
 def tile_capsuleneuralnetwork_pa_v_kernel(
@@ -57,9 +55,12 @@ def tile_capsuleneuralnetwork_pa_v_kernel(
 
         def take_bank(key, dtype=F32):
             k = free_banks.pop(0)
-            tile = psum.tile([PART, 512 if dtype == F32 else 1024], dtype, name="bank%d" % k, tag="bank%d" % k, bufs=1)
+            tile = psum.tile([PART, PASS if dtype == F32 else 2 * PASS], dtype, name="bank%d" % k, tag="bank%d" % k, bufs=1)
             filled[key] = (k, tile)
             return tile
+
+        def bank(key):
+            return filled[key][1]
 
         def give_bank(key):
             free_banks.append(filled.pop(key)[0])
@@ -78,8 +79,8 @@ def tile_capsuleneuralnetwork_pa_v_kernel(
                 out=out[:],
                 lhsT=lhs[0][:, m0 : m0 + PART].bitcast(lhs_fmt),
                 lhsT_scale=lhs[1][:, m0 : m0 + PART],
-                rhs=rhs[0][:, n0 : n0 + 512].bitcast(rhs_fmt),
-                rhs_scale=rhs[1][:, n0 : n0 + 512],
+                rhs=rhs[0][:, n0 : n0 + PASS].bitcast(rhs_fmt),
+                rhs_scale=rhs[1][:, n0 : n0 + PASS],
                 start=start,
                 stop=stop,
             )
@@ -96,23 +97,26 @@ def tile_capsuleneuralnetwork_pa_v_kernel(
         ctx.enter_context(tc.manual_schedule())
 
         q_all = pool.tile([PART, GROUPS, ROW + ROLL], BF16, name="q_all", tag="wide_q", align_bytes=LINE)
+        y_ring = pool.tile([PART, 2 * ROW], F32, name="y_ring", tag="wide_y", align_bytes=LINE)
         y_t, a_t, p_t, x_t = {}, {}, {}, {}
 
-        y_ring = pool.tile([PART, 2 * ROW], F32, name="y_ring", tag="wide_y", align_bytes=LINE)
-
-        def load_qy(g, lo=0, hi=PACK):
+        def load_qy(g, lo=0, hi=ROW):
             y_t[g] = y_ring[:, ROW * (g % 2) : ROW * (g % 2 + 1)]
-            q_lo, q_hi = (F * lo + ROLL if lo else 0), min(F * hi + ROLL, ROW)
+            q_lo, q_hi = (lo + ROLL if lo else 0), min(hi + ROLL, ROW)
             nc.sync.dma_start(out=q_all[:, g, q_lo:q_hi], in_=gr_rows[g * PART : (g + 1) * PART, q_lo:q_hi])
-            nc.sync.dma_start(out=y_t[g][:, F * lo : F * hi], in_=y_dram[g].rearrange("p j w -> p (j w)")[:, F * lo : F * hi])
+            nc.sync.dma_start(out=y_t[g][:, lo:hi], in_=y_dram[g].rearrange("p j w -> p (j w)")[:, lo:hi])
+
+        def load_qy_halves(g):
+            load_qy(g, 0, HALF)
+            load_qy(g, HALF, ROW)
 
         def load_a(g, lo=0, hi=ROW):
             if lo == 0:
                 a_t[g] = pool.tile([PART, ROW], F32, name="a_sb", tag="ring_a", bufs=2, align_bytes=LINE)
             nc.sync.dma_start(out=a_t[g][:, lo:hi], in_=a_dram[g].rearrange("p j w -> p (j w)")[:, lo:hi])
 
-        def load_p(g):
-            pair = pool.tile([PART, 2, PACK * P_IN], BF16, name="p_sb", tag="wide_p" if g < 2 else "wide_y", align_bytes=LINE)
+        def load_p_pair(g):
+            pair = pool.tile([PART, 2, PACK * P_IN], BF16, name="p_sb", tag="wide_p" if g == 0 else "wide_y", align_bytes=LINE)
             nc.sync.dma_start(out=pair[:], in_=p_dram[g : g + 2].rearrange("g p j w -> p g (j w)"))
             for k in range(2):
                 p_t[g + k] = pair[:, k, :].rearrange("p (j w) -> p j w", j=PACK)
@@ -126,121 +130,98 @@ def tile_capsuleneuralnetwork_pa_v_kernel(
         def stage_tile():
             return pool.tile([PART, ROW], BF16, name="stage", tag="stage", bufs=4, align_bytes=LINE)
 
-        def word_transposes(key, words, first, count):
-            tp = take_bank(key)
-            for i in range(count):
+        def word_transposes(key, row, s):
+            words, tp = row.bitcast(F32), take_bank(key)
+            for i in range(2):
+                lo = 2 * PART * (2 * s + i)
                 for u in range(2):
-                    lo = 256 * (first + i)
-                    nc.tensor.transpose(tp[:, (2 * i + u) * PART : (2 * i + u + 1) * PART], words[:, lo + u : lo + 256 : 2], ident[:])
+                    nc.tensor.transpose(tp[:, (2 * i + u) * PART : (2 * i + u + 1) * PART], words[:, lo + u : lo + 2 * PART : 2], ident[:])
 
-        def identity_turns(key, rows, first, count):
+        def identity_matmuls(key, stationaries):
             tp = take_bank(key, BF16)
-            for i in range(count):
-                for t in range(PACK):
-                    lo = 512 * (first + i)
-                    nc.tensor.matmul(
-                        out=tp[:, PART * (PACK * i + t) : PART * (PACK * i + t + 1)],
-                        lhsT=rows[:, lo + t : lo + 512 : PACK],
-                        rhs=ident_bf[:],
-                        start=True,
-                        stop=True,
-                    )
+            for i, lhs in enumerate(stationaries):
+                nc.tensor.matmul(out=tp[:, PART * i : PART * (i + 1)], lhsT=lhs, rhs=ident_bf[:], start=True, stop=True)
 
-        def weight_turn(raw, staged, s, plain):
-            if plain:
-                identity_turns("w", raw, 2 * s, 2)
-                scopy(
-                    out=staged[:].rearrange("p (m w) -> p m w", w=16)[:, :, 8 * s : 8 * s + 8],
-                    in_=filled["w"][1][:].rearrange("p (w m) -> p m w", w=8),
-                )
-            else:
-                word_transposes("w", raw.bitcast(F32), 2 * s, 2)
-                scopy(
-                    out=staged[:].bitcast(F32).rearrange("p (m w) -> p m w", w=8)[:, :, 4 * s : 4 * s + 4],
-                    in_=filled["w"][1][:].rearrange("p (w m) -> p m w", w=4),
-                )
+        def weight_by_words(raw, staged, s):
+            word_transposes("w", raw, s)
+            scopy(
+                out=staged[:].bitcast(F32).rearrange("p (m half w) -> p m half w", half=2, w=PACK)[:, :, s, :],
+                in_=bank("w")[:].rearrange("p (w m) -> p m w", w=PACK),
+            )
+            give_bank("w")
+
+        def weight_by_matmuls(raw, staged, s):
+            slots = raw.rearrange("p (i k) -> p i k", i=PACK)
+            identity_matmuls("w", [slots[:, i, t::PACK] for i in (2 * s, 2 * s + 1) for t in range(PACK)])
+            scopy(
+                out=staged[:].rearrange("p (m half w) -> p m half w", half=2, w=2 * PACK)[:, :, s, :],
+                in_=bank("w")[:].rearrange("p (w m) -> p m w", w=2 * PACK),
+            )
             give_bank("w")
 
         dy, dyg, dyw, dyq, dywq = ({} for i in range(5))
 
-        def dy_mask(g, lo, hi):
-            if lo == 0:
+        def q_swap(g):
+            nc.tensor.matmul(out=take_bank("q", BF16)[:, 0:ROLL], lhsT=swap[:], rhs=q_all[:, g, 0:ROLL], start=True, stop=True)
+            scopy(out=q_all[:, g, ROW : ROW + ROLL], in_=bank("q")[:, 0:ROLL])
+            give_bank("q")
+
+        def dy_mask(g, s):
+            if s == 0:
                 dy[g] = pool.tile([PART, ROW], BF16, name="dy", tag="dy", bufs=2)
-            cols = slice(F * lo, F * hi)
+            lo, hi = HALF * s, HALF * (s + 1)
             nc.vector.scalar_tensor_tensor(
-                out=dy[g][:, cols], in0=y_t[g][:, cols], scalar=0.0, in1=q_all[:, g, F * lo + ROLL : F * hi + ROLL],
+                out=dy[g][:, lo:hi], in0=y_t[g][:, lo:hi], scalar=0.0, in1=q_all[:, g, lo + ROLL : hi + ROLL],
                 op0=ALU.is_gt, op1=ALU.mult,
             )
 
-        def q_swap(g):
-            nc.tensor.matmul(out=take_bank("q", BF16)[:, 0:ROLL], lhsT=swap[:], rhs=q_all[:, g, 0:ROLL], start=True, stop=True)
-            scopy(out=q_all[:, g, ROW : ROW + ROLL], in_=filled["q"][1][:, 0:ROLL])
-            give_bank("q")
-
-        def dy_turn(g, lo, hi):
-            if g < PLAIN_DY:
-                identity_turns(("dy", lo), dy[g][:], lo, hi - lo)
-            else:
-                word_transposes(("dy", lo), dy[g][:].bitcast(F32), lo, hi - lo)
-
-        def dy_out(g, lo, hi):
-            if lo == 0:
+        def dy_turn(g, s):
+            word_transposes("dy", dy[g][:], s)
+            if s == 0:
                 dyg[g] = pool.tile([PART, ROW], BF16, name="dyg", tag="dyg", bufs=1, align_bytes=LINE)
-            n = hi - lo
-            tp = filled["dy", lo][1]
-            if g < PLAIN_DY:
-                scopy(
-                    out=dyg[g][:, F * lo : F * hi].rearrange("p (i r t) -> p i r t", i=n, t=PACK),
-                    in_=tp[:, 0 : F * n].rearrange("p (i t r) -> p i r t", i=n, t=PACK),
-                )
-                if hi == PACK:
-                    dyw[g] = pool.tile([PART, PASS], BF16, name="dyw", tag="dyw", bufs=1, align_bytes=LINE)
-                    scopy(
-                        out=dyw[g][:].rearrange("p (b h t) -> p b h t", h=2, t=PACK),
-                        in_=tp[:, F * (n - 1) : F * n].rearrange("p (t b h) -> p b h t", t=PACK, h=2)[:, :, ::-1, :],
-                    )
-                give_bank(("dy", lo))
-                return
             scopy(
-                out=dyg[g][:].bitcast(F32)[:, 256 * lo : 256 * hi].rearrange("p (i r u) -> p i r u", i=n, u=2),
-                in_=tp[:, 0 : 256 * n].rearrange("p (i u r) -> p i r u", i=n, u=2),
+                out=dyg[g][:].bitcast(F32)[:, PASS * s : PASS * (s + 1)].rearrange("p (i r u) -> p i r u", i=2, u=2),
+                in_=bank("dy")[:].rearrange("p (i u r) -> p i r u", i=2, u=2),
             )
-            if hi == PACK:
+            if s == 1:
                 dyw[g] = pool.tile([PART, PASS], BF16, name="dyw", tag="dyw", bufs=1, align_bytes=LINE)
                 scopy(
                     out=dyw[g][:].bitcast(F32).rearrange("p (b h u) -> p b h u", h=2, u=2),
-                    in_=tp[:, 256 * (n - 1) : 256 * n].rearrange("p (u b h) -> p b h u", u=2, h=2)[:, :, ::-1, :],
+                    in_=bank("dy")[:, 2 * PART : PASS].rearrange("p (u b h) -> p b h u", u=2, h=2)[:, :, ::-1, :],
                 )
-            give_bank(("dy", lo))
+            give_bank("dy")
 
-        def dy_quantize(g, lo, hi):
-            if lo == 0:
-                dyq[g] = mx_pair("dyq", PASS, 2)
-            quantize(dyq[g], E5, dyg[g][:, F * lo : F * hi], PART * lo)
+        def dy_half(g, s):
+            dy_mask(g, s)
+            dy_turn(g, s)
+
+        def dy_quantize(g):
+            dyq[g] = mx_pair("dyq", PASS, 2)
+            quantize(dyq[g], E5, dyg[g][:])
 
         def dyw_quantize(g):
             dywq[g] = mx_pair("dywq", PART, 2)
             quantize(dywq[g], E5, dyw[g][:])
 
-        def dh_pass(g, s):
-            out = take_bank(("dh", s))
-            if s == WRAP:
+        def dh_pass(g, j):
+            out = take_bank(("dh", j))
+            if j == WRAP:
                 mx_pass(out, dywq[g], E5, 0, w1q, E4, 0)
             else:
-                mx_pass(out, dyq[g], E5, PART * s, w1q, E4, 0)
+                mx_pass(out, dyq[g], E5, PART * j, w1q, E4, 0)
 
         da, at, atq, dag, dagq, ob = ({} for i in range(6))
 
-        def da_mask(g, s):
-            if g not in da:
+        def da_mask(g, j):
+            if j == 0:
                 da[g] = pool.tile([PART, ROW], F32, name="da", tag="da", bufs=2, align_bytes=LINE)
-            lo, hi = max(0, G * s + ROLL), min(ROW, G * (s + 1) + ROLL)
-            src = lo - (G * s + ROLL)
+            lo, hi = max(0, G * j + ROLL), min(ROW, G * (j + 1) + ROLL)
+            src = lo - (G * j + ROLL)
             nc.vector.scalar_tensor_tensor(
-                out=da[g][:, lo:hi], in0=a_t[g][:, lo:hi], scalar=0.0, in1=filled["dh", s][1][:, src : src + hi - lo],
+                out=da[g][:, lo:hi], in0=a_t[g][:, lo:hi], scalar=0.0, in1=bank(("dh", j))[:, src : src + hi - lo],
                 op0=ALU.is_gt, op1=ALU.mult,
             )
-            give_bank(("dh", s))
+            give_bank(("dh", j))
 
         def da_sums(g, slots):
             for j in slots:
@@ -254,7 +235,7 @@ def tile_capsuleneuralnetwork_pa_v_kernel(
                         stop=(g == LAST and j == PACK - 1 and t == PACK - 1),
                     )
 
-        def da_cast(g):
+        def da_round(g):
             at[g] = pool.tile([PART, ROW], BF16, name="at", tag="at", bufs=1, align_bytes=LINE)
             vcopy(
                 out=at[g][:].rearrange("p (t m j) -> p m j t", t=PACK, j=PACK),
@@ -265,94 +246,73 @@ def tile_capsuleneuralnetwork_pa_v_kernel(
             atq[g] = mx_pair("atq", G, GROUPS)
             quantize(atq[g], E5, at[g][:])
 
-        def da_turn(g, u):
-            tp = take_bank(("da", u), BF16)
-            for e in range(2):
-                for t in range(PACK):
-                    nc.tensor.matmul(
-                        out=tp[:, PART * (PACK * e + t) : PART * (PACK * e + t + 1)],
-                        lhsT=at[g][:, 512 * t + 2 * u + e : 512 * (t + 1) : PACK],
-                        rhs=ident_bf[:],
-                        start=True,
-                        stop=True,
-                    )
-
-        def da_out(g, u):
-            if u == 0:
+        def da_turn(g, s):
+            planes = at[g][:].rearrange("p (t w) -> p t w", t=PACK)
+            identity_matmuls("da", [planes[:, t, j::PACK] for j in (2 * s, 2 * s + 1) for t in range(PACK)])
+            if s == 0:
                 dag[g] = pool.tile([PART, ROW], BF16, name="dag", tag="dag", bufs=1, align_bytes=LINE)
             scopy(
-                out=dag[g][:, 1024 * u : 1024 * (u + 1)].rearrange("p (e r t) -> p e r t", e=2, t=PACK),
-                in_=filled["da", u][1][:].rearrange("p (e t r) -> p e r t", t=PACK, e=2),
+                out=dag[g][:, HALF * s : HALF * (s + 1)].rearrange("p (i r t) -> p i r t", i=2, t=PACK),
+                in_=bank("da")[:].rearrange("p (i t r) -> p i r t", i=2, t=PACK),
             )
-            give_bank(("da", u))
+            give_bank("da")
 
-        def dag_quantize(g, lo=0, hi=2):
-            if lo == 0:
-                dagq[g] = mx_pair("dagq", PASS, 2)
-            quantize(dagq[g], E5, dag[g][:, 1024 * lo : 1024 * hi], 256 * lo)
+        def dag_quantize(g):
+            dagq[g] = mx_pair("dagq", PASS, 2)
+            quantize(dagq[g], E5, dag[g][:])
 
-        def dp_pass(g, i):
-            j, n = divmod(i, 2)
-            mx_pass(take_bank(("dp", i)), dagq[g], E5, PART * j, w0q, E4, 512 * n)
-
-        def dp_out(g, i, copy=scopy):
-            j, n = divmod(i, 2)
-            if g not in ob:
-                ob[g] = pool.tile([PART, PACK, P_IN], F32, name="ob", tag="wide_q" if g == LAST else "wide_%d" % g, align_bytes=LINE)
-            copy(out=ob[g][:, j, 512 * n : 512 * (n + 1)], in_=filled["dp", i][1][:])
-            give_bank(("dp", i))
-
-        def dp_tiles(g, which):
-            for i in which:
-                dp_pass(g, i)
-                dp_out(g, i)
+        def dp_tiles(g, tiles):
+            for i in tiles:
+                j, n = divmod(i, 2)
+                mx_pass(take_bank("dp"), dagq[g], E5, PART * j, w0q, E4, PASS * n)
+                if i == 0:
+                    ob[g] = pool.tile([PART, PACK, P_IN], F32, name="ob", tag="wide_q" if g == LAST else "wide_%d" % g, align_bytes=LINE)
+                scopy(out=ob[g][:, j, PASS * n : PASS * (n + 1)], in_=bank("dp")[:])
+                give_bank("dp")
 
         def store_dp(g, lo=0, hi=PACK):
             nc.sync.dma_start(out=o_dram[g][:, lo:hi, :], in_=ob[g][:, lo:hi, :])
 
         staged, inq, wb = {}, {}, {}
 
-        def interleave(g, c, copy, lo=0, hi=512):
-            src = x_t[g][:, :, lo:hi] if c == X_CHUNK else p_t[g][:, :, 512 * c + lo : 512 * c + hi]
-            if lo == 0:
+        def interleave(g, c, copy, lo=0, hi=PASS):
+            src = x_t[g][:, :, lo:hi] if c == X_CHUNK else p_t[g][:, :, PASS * c + lo : PASS * c + hi]
+            if (g, c) not in staged:
                 staged[g, c] = stage_tile()
             copy(
-                out=staged[g, c][:, PACK * lo : PACK * hi].rearrange("p (c i j) -> p c j i", i=4, j=PACK),
-                in_=src.rearrange("p j (c i) -> p c j i", i=4),
+                out=staged[g, c][:, PACK * lo : PACK * hi].rearrange("p (c i j) -> p c j i", i=PACK, j=PACK),
+                in_=src.rearrange("p j (c i) -> p c j i", i=PACK),
             )
 
-        def inp_quantize(g, c, lo=0, hi=512):
-            if lo == 0:
-                inq[g, c] = mx_pair("inq", 512, 8)
-            quantize(inq[g, c], E4, staged[g, c][:, PACK * lo : PACK * hi], lo)
+        def inp_quantize(g, c):
+            inq[g, c] = mx_pair("inq", PASS, 2 * GROUPS)
+            quantize(inq[g, c], E4, staged[g, c][:])
 
         def dw_pass(c, r, g):
             if g == 0:
                 take_bank(("dw", c, r))
-            mx_pass(filled["dw", c, r][1], inq[g, c], E4, PART * r, atq[g], E5, 0, start=(g == 0), stop=(g == LAST))
+            mx_pass(bank(("dw", c, r)), inq[g, c], E4, PART * r, atq[g], E5, 0, start=(g == 0), stop=(g == LAST))
 
         def dw_out(c, r, copy=scopy):
-            if c not in wb:
+            if r == 0:
                 wb[c] = pool.tile([PART, PACK, G], F32, name="wb", tag="wide_0" if c == 1 else "da", bufs=1 if c == 1 else 2, align_bytes=LINE)
             copy(
                 out=wb[c][:, r, :].rearrange("p (m t) -> p m t", t=PACK),
-                in_=filled["dw", c, r][1][:].rearrange("p (t m) -> p m t", t=PACK),
+                in_=bank(("dw", c, r))[:].rearrange("p (t m) -> p m t", t=PACK),
             )
             give_bank(("dw", c, r))
 
         def store_dw(c, lo, hi):
-            rows = out_1[512 * c : 512 * (c + 1), :].rearrange("(r p) w -> p r w", p=PART)
+            rows = out_1[PASS * c : PASS * (c + 1), :].rearrange("(r p) w -> p r w", p=PART)
             nc.sync.dma_start(out=rows[:, lo:hi, :], in_=wb[c][:, lo:hi, :])
 
         vcopy(out=swap[:].rearrange("p (b h) -> p b h", h=2), in_=ident_bf[:].rearrange("p (b h) -> p b h", h=2)[:, :, ::-1])
         w1_raw = stage_tile()
         nc.sync.dma_start(out=w1_raw[:], in_=W1[0:G, :].rearrange("(m t) k -> m (t k)", t=PACK))
-        load_qy(0, 0, 2)
-        load_qy(0, 2, 4)
-        load_qy(1, 0, 2)
-        load_qy(1, 2, 4)
-        load_a(0, 0, 1024 + ROLL)
-        load_a(0, 1024 + ROLL, ROW)
+        load_qy_halves(0)
+        load_qy_halves(1)
+        load_a(0, 0, HALF + ROLL)
+        load_a(0, HALF + ROLL, ROW)
         w0_raw = pool.tile([PART, 2 * ROW], BF16, name="w0_raw", tag="wide_2", align_bytes=LINE)
         nc.sync.dma_start(
             out=w0_raw[:].rearrange("p (n w) -> p n w", n=2), in_=W0[0:P_IN, :].rearrange("(n m t) k -> m n (t k)", n=2, t=PACK)
@@ -364,112 +324,103 @@ def tile_capsuleneuralnetwork_pa_v_kernel(
         w1_staged = stage_tile()
         w0_staged = [stage_tile(), stage_tile()]
 
-        def w0_turn(i):
-            n, s = divmod(i, 2)
-            weight_turn(w0_raw[:, ROW * n : ROW * (n + 1)], w0_staged[n], s, i < PLAIN_W0)
-
-        def dy_half(g, s):
-            dy_mask(g, 2 * s, 2 * s + 2)
-            dy_turn(g, 2 * s, 2 * s + 2)
-            dy_out(g, 2 * s, 2 * s + 2)
-
         for s in range(2):
-            weight_turn(w1_raw[:], w1_staged, s, PLAIN_W1)
+            weight_by_words(w1_raw[:], w1_staged, s)
         q_swap(0)
         dy_half(0, 0)
         quantize(w1q, E4, w1_staged[:])
         dy_half(0, 1)
-        load_qy(2, 0, 2)
-        load_qy(2, 2, 4)
+        load_qy_halves(2)
         load_a(1)
         q_swap(1)
-        dy_mask(1, 0, 2)
-        dy_quantize(0, 0, 4)
+        dy_mask(1, 0)
+        dy_quantize(0)
         dyw_quantize(0)
-        dy_turn(1, 0, 2)
-        dy_out(1, 0, 2)
-        for s in range(3):
-            dh_pass(0, s)
-        dy_mask(1, 2, 4)
+        dy_turn(1, 0)
+        for j in range(3):
+            dh_pass(0, j)
+        dy_mask(1, 1)
         load_qy(3)
 
         for g in range(GROUPS):
+            behind, ahead = g - 1, g + 2
             da_mask(g, 0)
             dh_pass(g, 3)
             da_mask(g, 1)
             dh_pass(g, WRAP)
             if g == 0:
-                dy_turn(1, 2, 4)
-                dy_out(1, 2, 4)
+                dy_turn(1, 1)
             if g == 1:
-                q_swap(3)
-            if g >= 1:
-                da_sums(g - 1, (0, 1))
-                dag_quantize(g - 1)
-                dp_tiles(g - 1, range(2))
-            for s in (2, 3, WRAP):
-                da_mask(g, s)
-            if g >= 1:
-                dp_tiles(g - 1, (2, 3))
-                da_sums(g - 1, (2,))
-                dp_tiles(g - 1, (4, 5))
+                q_swap(ahead)
+            if behind >= 0:
+                da_sums(behind, (0, 1))
+                if g >= 2:
+                    interleave(1, X_CHUNK, scopy, PART * (g - 2), PART * (g - 1))
+                dag_quantize(behind)
+                dp_tiles(behind, (0, 1))
+            for j in (2, 3, WRAP):
+                da_mask(g, j)
+            if behind >= 0:
+                dp_tiles(behind, (2, 3))
+                da_sums(behind, (2,))
+                dp_tiles(behind, (4, 5))
             if g == 0:
                 load_a(2)
                 load_x()
-                for i in range(4):
-                    if i == 1:
-                        q_swap(2)
-                    w0_turn(i)
+                weight_by_matmuls(w0_raw[:, 0:ROW], w0_staged[0], 0)
+                q_swap(ahead)
+                weight_by_matmuls(w0_raw[:, 0:ROW], w0_staged[0], 1)
+                for s in range(2):
+                    weight_by_words(w0_raw[:, ROW : 2 * ROW], w0_staged[1], s)
             if g == 1:
                 load_a(3)
                 nc.sync.dma_start(out=col_b[:], in_=col.partition_broadcast(PACK))
-                load_p(0)
+                load_p_pair(0)
             if 0 < g < LAST:
                 dyw_quantize(g + 1)
-            da_cast(g)
+            da_round(g)
             if g < LAST:
-                dy_quantize(g + 1, 0, 4)
+                dy_quantize(g + 1)
+            else:
+                interleave(2, X_CHUNK, vcopy)
             if g == 0:
                 dyw_quantize(g + 1)
-            for u in range(2):
-                da_turn(g, u)
-                da_out(g, u)
-            if g >= 1:
-                da_sums(g - 1, (3,))
-                dp_tiles(g - 1, (6,))
+            for s in range(2):
+                da_turn(g, s)
+            if behind >= 0:
+                da_sums(behind, (3,))
+                dp_tiles(behind, (6,))
             if g < LAST:
                 dh_pass(g + 1, 0)
                 dh_pass(g + 1, 1)
-            if g < 2:
-                dy_half(g + 2, 0)
-            if g == 2:
+            if ahead <= LAST:
+                dy_half(ahead, 0)
+            elif g < LAST:
                 interleave(0, X_CHUNK, vcopy)
-            if g >= 1:
-                dp_tiles(g - 1, (7,))
+            if behind >= 0:
+                dp_tiles(behind, (7,))
             if g < LAST:
                 dh_pass(g + 1, 2)
-            if g == LAST:
-                da_sums(g, (0, 1, 2, 3))
-            if g < 2:
-                dy_half(g + 2, 1)
-            if g == 1:
-                load_p(2)
-                store_dp(0)
-            if g == 2:
-                store_dp(1)
+            else:
+                da_sums(g, range(PACK))
+            if ahead <= LAST:
+                dy_half(ahead, 1)
+            if ahead == LAST:
+                load_p_pair(2)
+            if 0 <= behind < LAST - 1:
+                store_dp(behind)
             at_quantize(g)
             if g == 0:
-                quantize(w0q, E4, w0_staged[0][:])
-                quantize(w0q, E4, w0_staged[1][:], 512)
-            if g == 2:
-                interleave(1, X_CHUNK, vcopy)
+                for n in range(2):
+                    quantize(w0q, E4, w0_staged[n][:], PASS * n)
+            if g == LAST - 1:
+                interleave(1, X_CHUNK, vcopy, 2 * PART, PASS)
                 inp_quantize(0, X_CHUNK)
 
-        store_dp(2)
+        store_dp(LAST - 1)
         inp_quantize(1, X_CHUNK)
-        interleave(2, X_CHUNK, vcopy)
         for g in range(2):
-            for r in range(4):
+            for r in range(PACK):
                 dw_pass(X_CHUNK, r, g)
         interleave(0, 0, scopy)
         interleave(3, X_CHUNK, vcopy)
@@ -480,48 +431,45 @@ def tile_capsuleneuralnetwork_pa_v_kernel(
         )
         give_bank("sum")
         inp_quantize(3, X_CHUNK)
-        last_bank = take_bank("row")
-        nc.tensor.transpose(last_bank[:, 0:PART], red[:], ident[:])
-        row = pool.tile([PACK, PART], F32, name="row")
+        nc.tensor.transpose(take_bank("row")[:, 0:PART], red[:], ident[:])
+        last_row = pool.tile([PACK, PART], F32, name="row")
         interleave(1, 0, vcopy)
-        nc.vector.tensor_scalar(out=row[:], in0=last_bank[0:PACK, 0:PART], scalar1=col_b[:], scalar2=None, op0=ALU.mult)
+        nc.vector.tensor_scalar(out=last_row[:], in0=bank("row")[0:PACK, 0:PART], scalar1=col_b[:], scalar2=None, op0=ALU.mult)
         give_bank("row")
+        for s in range(2):
+            for r in range(PACK):
+                dp_tiles(LAST, (PACK * s + r,))
+                dw_pass(X_CHUNK, r, 2 + s)
+            store_dp(LAST, 2 * s, 2 * s + 2)
+        interleave(2, 0, vcopy)
         inp_quantize(0, 0)
-        for g in range(2):
-            for r in range(4):
-                dp_tiles(LAST, (4 * g + r,))
-                dw_pass(X_CHUNK, r, 2 + g)
-            store_dp(LAST, 2 * g, 2 * g + 2)
-        for g in range(1, GROUPS):
-            if g < LAST:
-                interleave(g + 1, 0, vcopy)
-            else:
-                interleave(0, 1, vcopy)
-            inp_quantize(g, 0)
-        for r in range(4):
+        inp_quantize(1, 0)
+        interleave(3, 0, vcopy)
+        inp_quantize(2, 0)
+        interleave(0, 1, vcopy)
+        inp_quantize(3, 0)
+        for r in range(PACK):
             dw_pass(0, r, 0)
             dw_out(X_CHUNK, r)
-        store_dw(X_CHUNK, 0, 4)
-        nc.sync.dma_start(out=out_1[C_IN : C_IN + 1, :].rearrange("o (t m) -> (o t) m", t=PACK), in_=row[:])
-        interleave(3, 1, scopy)
-        for r in range(4):
+        store_dw(X_CHUNK, 0, PACK)
+        nc.sync.dma_start(out=out_1[C_IN : C_IN + 1, :].rearrange("o (t m) -> (o t) m", t=PACK), in_=last_row[:])
+        interleave(LAST, 1, scopy)
+        for r in range(PACK):
             dw_pass(0, r, 1)
-        for r in range(4):
+        for r in range(PACK):
             dw_pass(0, r, 2)
             dw_pass(0, r, 3)
             dw_out(0, r)
             if r % 2:
                 store_dw(0, r - 1, r + 1)
-        interleave(1, 1, vcopy)
-        inp_quantize(0, 1)
-        interleave(2, 1, vcopy)
-        inp_quantize(1, 1)
-        inp_quantize(2, 1)
-        inp_quantize(3, 1)
+        for g in range(GROUPS):
+            if g + 1 < LAST:
+                interleave(g + 1, 1, vcopy)
+            inp_quantize(g, 1)
         for g in range(2):
-            for r in range(4):
+            for r in range(PACK):
                 dw_pass(1, r, g)
-        for r in range(4):
+        for r in range(PACK):
             dw_pass(1, r, 2)
             dw_pass(1, r, 3)
             dw_out(1, r, vcopy if r % 2 else scopy)

@@ -100,15 +100,12 @@ def tile_capsuleneuralnetwork_pa_v_kernel(
         y_ring = pool.tile([PART, 2 * ROW], F32, name="y_ring", tag="wide_y", align_bytes=LINE)
         y_t, a_t, p_t, x_t = {}, {}, {}, {}
 
-        def load_qy(g, lo=0, hi=ROW):
-            y_t[g] = y_ring[:, ROW * (g % 2) : ROW * (g % 2 + 1)]
-            q_lo, q_hi = (lo + ROLL if lo else 0), min(hi + ROLL, ROW)
-            nc.sync.dma_start(out=q_all[:, g, q_lo:q_hi], in_=gr_rows[g * PART : (g + 1) * PART, q_lo:q_hi])
-            nc.sync.dma_start(out=y_t[g][:, lo:hi], in_=y_dram[g].rearrange("p j w -> p (j w)")[:, lo:hi])
+        def load_q(g, lo=0, hi=ROW):
+            nc.sync.dma_start(out=q_all[:, g, lo:hi], in_=gr_rows[g * PART : (g + 1) * PART, lo:hi])
 
-        def load_qy_halves(g):
-            load_qy(g, 0, HALF)
-            load_qy(g, HALF, ROW)
+        def load_y(g, lo=0, hi=ROW):
+            y_t[g] = y_ring[:, ROW * (g % 2) : ROW * (g % 2 + 1)]
+            nc.sync.dma_start(out=y_t[g][:, lo:hi], in_=y_dram[g].rearrange("p j w -> p (j w)")[:, lo:hi])
 
         def load_a(g, lo=0, hi=ROW):
             if lo == 0:
@@ -309,8 +306,13 @@ def tile_capsuleneuralnetwork_pa_v_kernel(
         vcopy(out=swap[:].rearrange("p (b h) -> p b h", h=2), in_=ident_bf[:].rearrange("p (b h) -> p b h", h=2)[:, :, ::-1])
         w1_raw = stage_tile()
         nc.sync.dma_start(out=w1_raw[:], in_=W1[0:G, :].rearrange("(m t) k -> m (t k)", t=PACK))
-        load_qy_halves(0)
-        load_qy_halves(1)
+        load_q(0, 0, HALF + ROLL)
+        load_y(0, 0, HALF)
+        load_q(0, HALF + ROLL, ROW)
+        load_y(0, HALF, ROW)
+        load_q(1)
+        load_y(1, 0, HALF)
+        load_y(1, HALF, ROW)
         load_a(0, 0, HALF + ROLL)
         load_a(0, HALF + ROLL, ROW)
         w0_raw = pool.tile([PART, 2 * ROW], BF16, name="w0_raw", tag="wide_2", align_bytes=LINE)
@@ -330,7 +332,9 @@ def tile_capsuleneuralnetwork_pa_v_kernel(
         dy_half(0, 0)
         quantize(w1q, E4, w1_staged[:])
         dy_half(0, 1)
-        load_qy_halves(2)
+        load_q(2)
+        load_y(2, 0, HALF)
+        load_y(2, HALF, ROW)
         load_a(1)
         q_swap(1)
         dy_mask(1, 0)
@@ -340,7 +344,8 @@ def tile_capsuleneuralnetwork_pa_v_kernel(
         for j in range(3):
             dh_pass(0, j)
         dy_mask(1, 1)
-        load_qy(3)
+        load_q(3)
+        load_y(3)
 
         for g in range(GROUPS):
             behind, ahead = g - 1, g + 2
@@ -473,4 +478,5 @@ def tile_capsuleneuralnetwork_pa_v_kernel(
             dw_pass(1, r, 2)
             dw_pass(1, r, 3)
             dw_out(1, r, vcopy if r % 2 else scopy)
-            store_dw(1, r, r + 1)
+            if r > 0:
+                store_dw(1, 0 if r == 1 else r, r + 1)

@@ -26,6 +26,7 @@ ROW = PACK * F
 HALF = ROW // 2
 ROLL = 128
 WRAP = -1
+RUN = 16
 X_CHUNK = 2
 LINE = 256
 
@@ -74,13 +75,13 @@ def tile_capsuleneuralnetwork_pa_v_kernel(
             width = src.shape[1] // PACK
             nc.vector.quantize_mx(out=pair[0][:, lo : lo + width].bitcast(fmt), scales=pair[1][:, lo : lo + width], in_=src)
 
-        def mx_pass(out, lhs, lhs_fmt, m0, rhs, rhs_fmt, n0, start=True, stop=True):
+        def mx_pass(out, lhs, lhs_fmt, m0, rhs, rhs_fmt, n0, start=True, stop=True, width=PASS):
             nc.tensor.matmul_mx(
-                out=out[:],
+                out=out[:, 0:width],
                 lhsT=lhs[0][:, m0 : m0 + PART].bitcast(lhs_fmt),
                 lhsT_scale=lhs[1][:, m0 : m0 + PART],
-                rhs=rhs[0][:, n0 : n0 + PASS].bitcast(rhs_fmt),
-                rhs_scale=rhs[1][:, n0 : n0 + PASS],
+                rhs=rhs[0][:, n0 : n0 + width].bitcast(rhs_fmt),
+                rhs_scale=rhs[1][:, n0 : n0 + width],
                 start=start,
                 stop=stop,
             )
@@ -134,13 +135,20 @@ def tile_capsuleneuralnetwork_pa_v_kernel(
                 for u in range(2):
                     nc.tensor.transpose(tp[:, (2 * i + u) * PART : (2 * i + u + 1) * PART], words[:, lo + u : lo + 2 * PART : 2], ident[:])
 
+        def plane_transposes(key, planes, s):
+            words, tp = planes.bitcast(F32), take_bank(key)
+            for i in range(2):
+                for u in range(2):
+                    lo = PASS * u + PART * (2 * s + i)
+                    nc.tensor.transpose(tp[:, (2 * i + u) * PART : (2 * i + u + 1) * PART], words[:, lo : lo + PART], ident[:])
+
         def identity_matmuls(key, stationaries):
             tp = take_bank(key, BF16)
             for i, lhs in enumerate(stationaries):
                 nc.tensor.matmul(out=tp[:, PART * i : PART * (i + 1)], lhsT=lhs, rhs=ident_bf[:], start=True, stop=True)
 
-        def weight_by_words(raw, staged, s):
-            word_transposes("w", raw, s)
+        def weight_by_words(raw, staged, s, transposes=word_transposes):
+            transposes("w", raw, s)
             scopy(
                 out=staged[:].bitcast(F32).rearrange("p (m half w) -> p m half w", half=2, w=PACK)[:, :, s, :],
                 in_=bank("w")[:].rearrange("p (w m) -> p m w", w=PACK),
@@ -165,15 +173,18 @@ def tile_capsuleneuralnetwork_pa_v_kernel(
 
         def dy_mask(g, s):
             if s == 0:
-                dy[g] = pool.tile([PART, ROW], BF16, name="dy", tag="dy", bufs=2)
+                dy[g] = pool.tile([PART, ROW], BF16, name="dy", tag="dy", bufs=2, align_bytes=LINE)
             lo, hi = HALF * s, HALF * (s + 1)
-            nc.vector.scalar_tensor_tensor(
-                out=dy[g][:, lo:hi], in0=y_t[g][:, lo:hi], scalar=0.0, in1=q_all[:, g, lo + ROLL : hi + ROLL],
-                op0=ALU.is_gt, op1=ALU.mult,
-            )
+            for u in range(2):
+                y_plane = y_t[g][:, lo:hi].rearrange("p (b u e) -> p b u e", u=2, e=RUN)[:, :, u, :]
+                q_plane = q_all[:, g, lo + ROLL : hi + ROLL].rearrange("p (b u e) -> p b u e", u=2, e=RUN)[:, :, u, :]
+                nc.vector.scalar_tensor_tensor(
+                    out=dy[g][:, HALF * u + lo // 2 : HALF * u + hi // 2].rearrange("p (b e) -> p b e", e=RUN),
+                    in0=y_plane, scalar=0.0, in1=q_plane, op0=ALU.is_gt, op1=ALU.mult,
+                )
 
         def dy_turn(g, s):
-            word_transposes("dy", dy[g][:], s)
+            plane_transposes("dy", dy[g][:], s)
             if s == 0:
                 dyg[g] = pool.tile([PART, ROW], BF16, name="dyg", tag="dyg", bufs=1, align_bytes=LINE)
             scopy(
@@ -288,7 +299,7 @@ def tile_capsuleneuralnetwork_pa_v_kernel(
         def dw_pass(c, r, g):
             if g == 0:
                 take_bank(("dw", c, r))
-            mx_pass(bank(("dw", c, r)), inq[g, c], E4, PART * r, atq[g], E5, 0, start=(g == 0), stop=(g == LAST))
+            mx_pass(bank(("dw", c, r)), inq[g, c], E4, PART * r, atq[g], E5, 0, start=(g == 0), stop=(g == (2 if c == 1 else LAST)))
 
         def dw_out(c, r, copy=scopy):
             if r == 0:
@@ -323,11 +334,16 @@ def tile_capsuleneuralnetwork_pa_v_kernel(
         sum_bank = take_bank("sum")
         w1q = mx_pair("w1q", G, 1)
         w0q = mx_pair("w0q", P_IN, 1)
+        w1_planes = stage_tile()
         w1_staged = stage_tile()
-        w0_staged = [stage_tile(), stage_tile()]
 
+        vcopy(
+            out=w1_planes[:].rearrange("p (u b e) -> p u b e", u=2, e=RUN),
+            in_=w1_raw[:].rearrange("p (b u e) -> p u b e", u=2, e=RUN),
+        )
         for s in range(2):
-            weight_by_words(w1_raw[:], w1_staged, s)
+            weight_by_words(w1_planes[:], w1_staged, s, plane_transposes)
+        w0_staged = [stage_tile(), stage_tile()]
         q_swap(0)
         dy_half(0, 0)
         quantize(w1q, E4, w1_staged[:])
@@ -383,11 +399,13 @@ def tile_capsuleneuralnetwork_pa_v_kernel(
                 load_p_pair(0)
             if 0 < g < LAST:
                 dyw_quantize(g + 1)
+            if g == LAST:
+                interleave(2, X_CHUNK, vcopy, 0, PASS // 2)
             da_round(g)
             if g < LAST:
                 dy_quantize(g + 1)
             else:
-                interleave(2, X_CHUNK, vcopy)
+                interleave(2, X_CHUNK, vcopy, PASS // 2, PASS)
             if g == 0:
                 dyw_quantize(g + 1)
             for s in range(2):
@@ -428,8 +446,8 @@ def tile_capsuleneuralnetwork_pa_v_kernel(
             for r in range(PACK):
                 dw_pass(X_CHUNK, r, g)
         interleave(0, 0, scopy)
-        interleave(3, X_CHUNK, vcopy)
         inp_quantize(2, X_CHUNK)
+        interleave(3, X_CHUNK, vcopy)
         dag_quantize(LAST)
         nc.vector.tensor_reduce(
             out=red[:, 0:PACK], in_=sum_bank[:].rearrange("p (t n) -> p t n", t=PACK), axis=mybir.AxisListType.X, op=ALU.add
@@ -467,16 +485,18 @@ def tile_capsuleneuralnetwork_pa_v_kernel(
             dw_out(0, r)
             if r % 2:
                 store_dw(0, r - 1, r + 1)
-        for g in range(GROUPS):
-            if g + 1 < LAST:
-                interleave(g + 1, 1, vcopy)
-            inp_quantize(g, 1)
+        interleave(1, 1, vcopy)
+        inp_quantize(0, 1)
+        inp_quantize(1, 1)
+        interleave(2, 1, vcopy)
+        inp_quantize(3, 1)
+        inp_quantize(2, 1)
         for g in range(2):
             for r in range(PACK):
                 dw_pass(1, r, g)
         for r in range(PACK):
-            dw_pass(1, r, 2)
             dw_pass(1, r, 3)
+            dw_pass(1, r, 2)
             dw_out(1, r, vcopy if r % 2 else scopy)
             if r > 0:
                 store_dw(1, 0 if r == 1 else r, r + 1)

@@ -101,17 +101,17 @@ def tile_capsuleneuralnetwork_pa_v_kernel(
         y_ring = pool.tile([PART, 2 * ROW], F32, name="y_ring", tag="wide_y", align_bytes=LINE)
         y_t, a_t, p_t, x_t = {}, {}, {}, {}
 
-        def load_q(g, lo=0, hi=ROW):
-            nc.sync.dma_start(out=q_all[:, g, lo:hi], in_=gr_rows[g * PART : (g + 1) * PART, lo:hi])
+        def load_q(g, count=1):
+            rows = gr_rows[g * PART : (g + count) * PART, :].rearrange("(g p) w -> p g w", p=PART)
+            nc.sync.dma_start(out=q_all[:, g : g + count, 0:ROW], in_=rows)
 
         def load_y(g, lo=0, hi=ROW):
             y_t[g] = y_ring[:, ROW * (g % 2) : ROW * (g % 2 + 1)]
             nc.sync.dma_start(out=y_t[g][:, lo:hi], in_=y_dram[g].rearrange("p j w -> p (j w)")[:, lo:hi])
 
-        def load_a(g, lo=0, hi=ROW):
-            if lo == 0:
-                a_t[g] = pool.tile([PART, ROW], F32, name="a_sb", tag="ring_a", bufs=2, align_bytes=LINE)
-            nc.sync.dma_start(out=a_t[g][:, lo:hi], in_=a_dram[g].rearrange("p j w -> p (j w)")[:, lo:hi])
+        def load_a(g):
+            a_t[g] = pool.tile([PART, ROW], F32, name="a_sb", tag="ring_a", bufs=2, align_bytes=LINE)
+            nc.sync.dma_start(out=a_t[g][:], in_=a_dram[g].rearrange("p j w -> p (j w)"))
 
         def load_p_pair(g):
             pair = pool.tile([PART, 2, PACK * P_IN], BF16, name="p_sb", tag="wide_p" if g == 0 else "wide_y", align_bytes=LINE)
@@ -288,8 +288,8 @@ def tile_capsuleneuralnetwork_pa_v_kernel(
             if (g, c) not in staged:
                 staged[g, c] = stage_tile()
             copy(
-                out=staged[g, c][:, PACK * lo : PACK * hi].rearrange("p (c i j) -> p c j i", i=PACK, j=PACK),
-                in_=src.rearrange("p j (c i) -> p c j i", i=PACK),
+                out=staged[g, c][:].rearrange("p (r m j) -> p m j r", r=PACK, j=PACK)[:, lo // PACK : hi // PACK],
+                in_=src.rearrange("p j (m r) -> p m j r", r=PACK),
             )
 
         def inp_quantize(g, c):
@@ -311,21 +311,19 @@ def tile_capsuleneuralnetwork_pa_v_kernel(
             give_bank(("dw", c, r))
 
         def store_dw(c, lo, hi):
-            rows = out_1[PASS * c : PASS * (c + 1), :].rearrange("(r p) w -> p r w", p=PART)
+            rows = out_1[PASS * c : PASS * (c + 1), :].rearrange("(p r) w -> p r w", r=PACK)
             nc.sync.dma_start(out=rows[:, lo:hi, :], in_=wb[c][:, lo:hi, :])
 
         vcopy(out=swap[:].rearrange("p (b h) -> p b h", h=2), in_=ident_bf[:].rearrange("p (b h) -> p b h", h=2)[:, :, ::-1])
         w1_raw = stage_tile()
         nc.sync.dma_start(out=w1_raw[:], in_=W1[0:G, :].rearrange("(m t) k -> m (t k)", t=PACK))
-        load_q(0, 0, HALF + ROLL)
+        load_q(0)
         load_y(0, 0, HALF)
-        load_q(0, HALF + ROLL, ROW)
         load_y(0, HALF, ROW)
         load_q(1)
         load_y(1, 0, HALF)
         load_y(1, HALF, ROW)
-        load_a(0, 0, HALF + ROLL)
-        load_a(0, HALF + ROLL, ROW)
+        load_a(0)
         w0_raw = pool.tile([PART, 2 * ROW], BF16, name="w0_raw", tag="wide_2", align_bytes=LINE)
         nc.sync.dma_start(
             out=w0_raw[:].rearrange("p (n w) -> p n w", n=2), in_=W0[0:P_IN, :].rearrange("(n m t) k -> m n (t k)", n=2, t=PACK)
@@ -349,8 +347,7 @@ def tile_capsuleneuralnetwork_pa_v_kernel(
         quantize(w1q, E4, w1_staged[:])
         dy_half(0, 1)
         load_q(2)
-        load_y(2, 0, HALF)
-        load_y(2, HALF, ROW)
+        load_y(2)
         load_a(1)
         q_swap(1)
         dy_mask(1, 0)
@@ -367,6 +364,8 @@ def tile_capsuleneuralnetwork_pa_v_kernel(
             behind, ahead = g - 1, g + 2
             da_mask(g, 0)
             dh_pass(g, 3)
+            if g == 1:
+                dag_quantize(behind)
             da_mask(g, 1)
             dh_pass(g, WRAP)
             if g == 0:
@@ -377,7 +376,7 @@ def tile_capsuleneuralnetwork_pa_v_kernel(
                 da_sums(behind, (0, 1))
                 if g >= 2:
                     interleave(1, X_CHUNK, scopy, PART * (g - 2), PART * (g - 1))
-                dag_quantize(behind)
+                    dag_quantize(behind)
                 dp_tiles(behind, (0, 1))
             for j in (2, 3, WRAP):
                 da_mask(g, j)
@@ -416,6 +415,8 @@ def tile_capsuleneuralnetwork_pa_v_kernel(
             if g < LAST:
                 dh_pass(g + 1, 0)
                 dh_pass(g + 1, 1)
+            if g == 0:
+                at_quantize(g)
             if ahead <= LAST:
                 dy_half(ahead, 0)
             elif g < LAST:
@@ -432,10 +433,11 @@ def tile_capsuleneuralnetwork_pa_v_kernel(
                 load_p_pair(2)
             if 0 <= behind < LAST - 1:
                 store_dp(behind)
-            at_quantize(g)
             if g == 0:
                 for n in range(2):
                     quantize(w0q, E4, w0_staged[n][:], PASS * n)
+            else:
+                at_quantize(g)
             if g == LAST - 1:
                 interleave(1, X_CHUNK, vcopy, 2 * PART, PASS)
                 inp_quantize(0, X_CHUNK)
@@ -498,5 +500,5 @@ def tile_capsuleneuralnetwork_pa_v_kernel(
             dw_pass(1, r, 3)
             dw_pass(1, r, 2)
             dw_out(1, r, vcopy if r % 2 else scopy)
-            if r > 0:
-                store_dw(1, 0 if r == 1 else r, r + 1)
+            if r % 2:
+                store_dw(1, r - 1, r + 1)

@@ -90,6 +90,12 @@ def tile_capsuleneuralnetwork_pa_v_kernel(
         make_identity(nc, ident[:])
         ident_bf = pool.tile([PART, PART], BF16, name="ident_bf")
         make_identity(nc, ident_bf[:])
+        spread = pool.tile([PART, 2, 2 * PART], BF16, name="spread")
+        nc.gpsimd.memset(spread[:], 0.0)
+        nc.gpsimd.affine_select(
+            out=spread[:].rearrange("p e n -> p (e n)"), in_=spread[:].rearrange("p e n -> p (e n)"), compare_op=ALU.not_equal,
+            fill=1.0, base=0, pattern=[[1, 2], [-1, 2 * PART]], channel_multiplier=2,
+        )
         swap = pool.tile([PART, PART], BF16, name="swap")
         col_b = pool.tile([PACK, 1], BF16, name="col_b")
         red = pool.tile([PART, PART], F32, name="red")
@@ -171,10 +177,10 @@ def tile_capsuleneuralnetwork_pa_v_kernel(
             scopy(out=q_all[:, g, ROW : ROW + ROLL], in_=bank("q")[:, 0:ROLL])
             give_bank("q")
 
-        def dy_mask(g, s):
+        def dy_mask(g, s, halves=1):
             if s == 0:
                 dy[g] = pool.tile([PART, ROW], BF16, name="dy", tag="dy", bufs=2, align_bytes=LINE)
-            lo, hi = HALF * s, HALF * (s + 1)
+            lo, hi = HALF * s, HALF * (s + halves)
             for u in range(2):
                 y_plane = y_t[g][:, lo:hi].rearrange("p (b u e) -> p b u e", u=2, e=RUN)[:, :, u, :]
                 q_plane = q_all[:, g, lo + ROLL : hi + ROLL].rearrange("p (b u e) -> p b u e", u=2, e=RUN)[:, :, u, :]
@@ -204,11 +210,11 @@ def tile_capsuleneuralnetwork_pa_v_kernel(
             dy_turn(g, s)
 
         def dy_quantize(g):
-            dyq[g] = mx_pair("dyq", PASS, 2)
+            dyq[g] = mx_pair("dyq", PASS, 1)
             quantize(dyq[g], E5, dyg[g][:])
 
         def dyw_quantize(g):
-            dywq[g] = mx_pair("dywq", PART, 2)
+            dywq[g] = mx_pair("dywq", PART, 1)
             quantize(dywq[g], E5, dyw[g][:])
 
         def dh_pass(g, j):
@@ -256,13 +262,26 @@ def tile_capsuleneuralnetwork_pa_v_kernel(
 
         def da_turn(g, s):
             planes = at[g][:].rearrange("p (t w) -> p t w", t=PACK)
-            identity_matmuls("da", [planes[:, t, j::PACK] for j in (2 * s, 2 * s + 1) for t in range(PACK)])
             if s == 0:
+                identity_matmuls("da", [planes[:, t, j::PACK] for j in (0, 1) for t in range(PACK)])
                 dag[g] = pool.tile([PART, ROW], BF16, name="dag", tag="dag", bufs=1, align_bytes=LINE)
-            scopy(
-                out=dag[g][:, HALF * s : HALF * (s + 1)].rearrange("p (i r t) -> p i r t", i=2, t=PACK),
-                in_=bank("da")[:].rearrange("p (i t r) -> p i r t", i=2, t=PACK),
-            )
+                scopy(
+                    out=dag[g][:, 0:HALF].rearrange("p (i r t) -> p i r t", i=2, t=PACK),
+                    in_=bank("da")[:].rearrange("p (i t r) -> p i r t", i=2, t=PACK),
+                )
+            else:
+                tp = take_bank("da", BF16)
+                for i in range(2):
+                    for t in range(PACK):
+                        lo = 2 * PART * (2 * i + t // 2)
+                        nc.tensor.matmul(
+                            out=tp[:, lo : lo + 2 * PART], lhsT=planes[:, t, 2 + i :: PACK], rhs=spread[:, t % 2, :],
+                            start=(t % 2 == 0), stop=(t % 2 == 1),
+                        )
+                scopy(
+                    out=dag[g][:].bitcast(F32)[:, PASS : 2 * PASS].rearrange("p (i r u) -> p i r u", i=2, u=2),
+                    in_=tp[:].bitcast(F32).rearrange("p (i u r) -> p i r u", i=2, u=2),
+                )
             give_bank("da")
 
         def dag_quantize(g):
@@ -382,7 +401,7 @@ def tile_capsuleneuralnetwork_pa_v_kernel(
                 da_mask(g, j)
             if behind >= 0:
                 dp_tiles(behind, (2, 3))
-                da_sums(behind, (2,))
+                da_sums(behind, (2, 3))
                 dp_tiles(behind, (4, 5))
             if g == 0:
                 load_a(2)
@@ -407,18 +426,18 @@ def tile_capsuleneuralnetwork_pa_v_kernel(
                 interleave(2, X_CHUNK, vcopy, PASS // 2, PASS)
             if g == 0:
                 dyw_quantize(g + 1)
-            for s in range(2):
-                da_turn(g, s)
-            if behind >= 0:
-                da_sums(behind, (3,))
-                dp_tiles(behind, (6,))
+            da_turn(g, 0)
             if g < LAST:
                 dh_pass(g + 1, 0)
+            da_turn(g, 1)
+            if g < LAST:
                 dh_pass(g + 1, 1)
+            if behind >= 0:
+                dp_tiles(behind, (6,))
             if g == 0:
                 at_quantize(g)
             if ahead <= LAST:
-                dy_half(ahead, 0)
+                dy_mask(ahead, 0, 2)
             elif g < LAST:
                 interleave(0, X_CHUNK, vcopy)
             if behind >= 0:
@@ -428,7 +447,8 @@ def tile_capsuleneuralnetwork_pa_v_kernel(
             else:
                 da_sums(g, range(PACK))
             if ahead <= LAST:
-                dy_half(ahead, 1)
+                for s in range(2):
+                    dy_turn(ahead, s)
             if ahead == LAST:
                 load_p_pair(2)
             if 0 <= behind < LAST - 1:

@@ -104,7 +104,7 @@ def tile_capsuleneuralnetwork_pa_v_kernel(
         ctx.enter_context(tc.manual_schedule())
 
         q_all = pool.tile([PART, GROUPS, ROW + ROLL], BF16, name="q_all", tag="wide_q", align_bytes=LINE)
-        y_ring = pool.tile([PART, 2 * ROW], F32, name="y_ring", tag="wide_y", align_bytes=LINE)
+        y_ring = pool.tile([PART, 2 * ROW], F32, name="y_ring", tag="arena", align_bytes=LINE)
         y_t, a_t, p_t, x_t = {}, {}, {}, {}
 
         def load_q(g, count=1):
@@ -119,11 +119,11 @@ def tile_capsuleneuralnetwork_pa_v_kernel(
             a_t[g] = pool.tile([PART, ROW], F32, name="a_sb", tag="ring_a", bufs=2, align_bytes=LINE)
             nc.sync.dma_start(out=a_t[g][:], in_=a_dram[g].rearrange("p j w -> p (j w)"))
 
-        def load_p_pair(g):
-            pair = pool.tile([PART, 2, PACK * P_IN], BF16, name="p_sb", tag="wide_p" if g == 0 else "wide_y", align_bytes=LINE)
-            nc.sync.dma_start(out=pair[:], in_=p_dram[g : g + 2].rearrange("g p j w -> p g (j w)"))
-            for k in range(2):
-                p_t[g + k] = pair[:, k, :].rearrange("p (j w) -> p j w", j=PACK)
+        def load_p():
+            p_all = pool.tile([PART, GROUPS * PACK * P_IN], BF16, name="p_all", tag="arena", align_bytes=LINE)
+            nc.sync.dma_start(out=p_all[:].rearrange("p (g w) -> p g w", g=GROUPS), in_=p_dram.rearrange("g p j w -> p g (j w)"))
+            for g in range(GROUPS):
+                p_t[g] = p_all[:, PACK * P_IN * g : PACK * P_IN * (g + 1)].rearrange("p (j w) -> p j w", j=PACK)
 
         def load_x():
             x_all = pool.tile([PART, GROUPS, ROW], BF16, name="x_all", align_bytes=LINE)
@@ -220,7 +220,8 @@ def tile_capsuleneuralnetwork_pa_v_kernel(
         def dh_pass(g, j):
             out = take_bank(("dh", j))
             if j == WRAP:
-                mx_pass(out, dywq[g], E5, 0, w1q, E4, 0)
+                lo = 0 if g < LAST else G - ROLL
+                mx_pass(out[:, lo:G], dywq[g], E5, 0, w1q, E4, lo, width=G - lo)
             else:
                 mx_pass(out, dyq[g], E5, PART * j, w1q, E4, 0)
 
@@ -292,8 +293,11 @@ def tile_capsuleneuralnetwork_pa_v_kernel(
             for i in tiles:
                 j, n = divmod(i, 2)
                 mx_pass(take_bank("dp"), dagq[g], E5, PART * j, w0q, E4, PASS * n)
-                if i == 0:
-                    ob[g] = pool.tile([PART, PACK, P_IN], F32, name="ob", tag="wide_q" if g == LAST else "wide_%d" % g, align_bytes=LINE)
+                if i == 0 and g == 0:
+                    ob["pair"] = pool.tile([PART, 2 * PACK, P_IN], F32, name="ob_pair", align_bytes=LINE)
+                    ob[0], ob[1] = ob["pair"][:, 0:PACK, :], ob["pair"][:, PACK : 2 * PACK, :]
+                if i == 0 and g >= 2:
+                    ob[g] = pool.tile([PART, PACK, P_IN], F32, name="ob", tag="wide_q" if g == LAST else "wide_2", align_bytes=LINE)
                 scopy(out=ob[g][:, j, PASS * n : PASS * (n + 1)], in_=bank("dp")[:])
                 give_bank("dp")
 
@@ -304,6 +308,8 @@ def tile_capsuleneuralnetwork_pa_v_kernel(
 
         def interleave(g, c, copy, lo=0, hi=PASS):
             src = x_t[g][:, :, lo:hi] if c == X_CHUNK else p_t[g][:, :, PASS * c + lo : PASS * c + hi]
+            if (g, c) not in staged and (g, c) in ((0, 0), (LAST, 1)):
+                staged[g, c] = pool.tile([PART, ROW], BF16, name="late_stage", tag="dy", bufs=2, align_bytes=LINE)
             if (g, c) not in staged:
                 staged[g, c] = stage_tile()
             copy(
@@ -322,7 +328,7 @@ def tile_capsuleneuralnetwork_pa_v_kernel(
 
         def dw_out(c, r, copy=scopy):
             if r == 0:
-                wb[c] = pool.tile([PART, PACK, G], F32, name="wb", tag="wide_0" if c == 1 else "da", bufs=1 if c == 1 else 2, align_bytes=LINE)
+                wb[c] = pool.tile([PART, PACK, G], F32, name="wb", tag="ring_a" if c == 1 else "da", bufs=2, align_bytes=LINE)
             copy(
                 out=wb[c][:, r, :].rearrange("p (m t) -> p m t", t=PACK),
                 in_=bank(("dw", c, r))[:].rearrange("p (t m) -> p m t", t=PACK),
@@ -394,7 +400,7 @@ def tile_capsuleneuralnetwork_pa_v_kernel(
             if behind >= 0:
                 da_sums(behind, (0, 1))
                 if g >= 2:
-                    interleave(1, X_CHUNK, scopy, PART * (g - 2), PART * (g - 1))
+                    interleave(1, X_CHUNK, scopy, PART * (g - 2), PART * (2 * g - 3))
                     dag_quantize(behind)
                 dp_tiles(behind, (0, 1))
             for j in (2, 3, WRAP):
@@ -414,7 +420,6 @@ def tile_capsuleneuralnetwork_pa_v_kernel(
             if g == 1:
                 load_a(3)
                 nc.sync.dma_start(out=col_b[:], in_=col.partition_broadcast(PACK))
-                load_p_pair(0)
             if 0 < g < LAST:
                 dyw_quantize(g + 1)
             if g == LAST:
@@ -450,16 +455,18 @@ def tile_capsuleneuralnetwork_pa_v_kernel(
                 for s in range(2):
                     dy_turn(ahead, s)
             if ahead == LAST:
-                load_p_pair(2)
-            if 0 <= behind < LAST - 1:
-                store_dp(behind)
+                load_p()
+            if behind == 1:
+                nc.sync.dma_start(
+                    out=o_dram[0:2].rearrange("g p j w -> p g (j w)"), in_=ob["pair"][:].rearrange("p (g j) w -> p g (j w)", g=2)
+                )
             if g == 0:
                 for n in range(2):
                     quantize(w0q, E4, w0_staged[n][:], PASS * n)
             else:
                 at_quantize(g)
             if g == LAST - 1:
-                interleave(1, X_CHUNK, vcopy, 2 * PART, PASS)
+                interleave(1, X_CHUNK, vcopy, 3 * PART, PASS)
                 inp_quantize(0, X_CHUNK)
 
         store_dp(LAST - 1)
@@ -476,11 +483,7 @@ def tile_capsuleneuralnetwork_pa_v_kernel(
         )
         give_bank("sum")
         inp_quantize(3, X_CHUNK)
-        nc.tensor.transpose(take_bank("row")[:, 0:PART], red[:], ident[:])
-        last_row = pool.tile([PACK, PART], F32, name="row")
         interleave(1, 0, vcopy)
-        nc.vector.tensor_scalar(out=last_row[:], in0=bank("row")[0:PACK, 0:PART], scalar1=col_b[:], scalar2=None, op0=ALU.mult)
-        give_bank("row")
         for s in range(2):
             for r in range(PACK):
                 dp_tiles(LAST, (PACK * s + r,))
@@ -492,13 +495,13 @@ def tile_capsuleneuralnetwork_pa_v_kernel(
         interleave(3, 0, vcopy)
         inp_quantize(2, 0)
         interleave(0, 1, vcopy)
+        interleave(LAST, 1, vcopy, 3 * PART, PASS)
         inp_quantize(3, 0)
         for r in range(PACK):
             dw_pass(0, r, 0)
             dw_out(X_CHUNK, r)
         store_dw(X_CHUNK, 0, PACK)
-        nc.sync.dma_start(out=out_1[C_IN : C_IN + 1, :].rearrange("o (t m) -> (o t) m", t=PACK), in_=last_row[:])
-        interleave(LAST, 1, scopy)
+        interleave(LAST, 1, scopy, 0, 3 * PART)
         for r in range(PACK):
             dw_pass(0, r, 1)
         for r in range(PACK):
@@ -522,3 +525,8 @@ def tile_capsuleneuralnetwork_pa_v_kernel(
             dw_out(1, r, vcopy if r % 2 else scopy)
             if r % 2:
                 store_dw(1, r - 1, r + 1)
+        nc.tensor.transpose(take_bank("row")[:, 0:PART], red[:], ident[:])
+        last_row = pool.tile([PACK, PART], F32, name="row")
+        nc.vector.tensor_scalar(out=last_row[:], in0=bank("row")[0:PACK, 0:PART], scalar1=col_b[:], scalar2=None, op0=ALU.mult)
+        give_bank("row")
+        nc.sync.dma_start(out=out_1[C_IN : C_IN + 1, :].rearrange("o (t m) -> (o t) m", t=PACK), in_=last_row[:])

@@ -523,8 +523,7 @@ def tile_capsuleneuralnetwork_pa_v_kernel(
             dw_pass(1, r, 3)
             dw_pass(1, r, 2)
             dw_out(1, r, vcopy if r % 2 else scopy)
-            if r % 2:
-                store_dw(1, r - 1, r + 1)
+            store_dw(1, r, r + 1)
         nc.tensor.transpose(take_bank("row")[:, 0:PART], red[:], ident[:])
         last_row = pool.tile([PACK, PART], F32, name="row")
         nc.vector.tensor_scalar(out=last_row[:], in0=bank("row")[0:PACK, 0:PART], scalar1=col_b[:], scalar2=None, op0=ALU.mult)

@@ -121,14 +121,16 @@ def tile_capsuleneuralnetwork_pa_v_kernel(
 
         def load_p():
             p_all = pool.tile([PART, GROUPS * PACK * P_IN], BF16, name="p_all", tag="arena", align_bytes=LINE)
-            nc.sync.dma_start(out=p_all[:].rearrange("p (g w) -> p g w", g=GROUPS), in_=p_dram.rearrange("g p j w -> p g (j w)"))
             for g in range(GROUPS):
+                nc.sync.dma_start(
+                    out=p_all[:, PACK * P_IN * g : PACK * P_IN * (g + 1)], in_=p_dram[g].rearrange("p j w -> p (j w)")
+                )
                 p_t[g] = p_all[:, PACK * P_IN * g : PACK * P_IN * (g + 1)].rearrange("p (j w) -> p j w", j=PACK)
 
         def load_x():
             x_all = pool.tile([PART, GROUPS, ROW], BF16, name="x_all", align_bytes=LINE)
-            nc.sync.dma_start(out=x_all[:], in_=x_dram.rearrange("g p j w -> p g (j w)"))
             for g in range(GROUPS):
+                nc.sync.dma_start(out=x_all[:, g, :], in_=x_dram[g].rearrange("p j w -> p (j w)"))
                 x_t[g] = x_all[:, g, :].rearrange("p (j w) -> p j w", j=PACK)
 
         def stage_tile():
@@ -350,9 +352,10 @@ def tile_capsuleneuralnetwork_pa_v_kernel(
         load_y(1, HALF, ROW)
         load_a(0)
         w0_raw = pool.tile([PART, 2 * ROW], BF16, name="w0_raw", tag="wide_2", align_bytes=LINE)
-        nc.sync.dma_start(
-            out=w0_raw[:].rearrange("p (n w) -> p n w", n=2), in_=W0[0:P_IN, :].rearrange("(n m t) k -> m n (t k)", n=2, t=PACK)
-        )
+        for n in range(2):
+            nc.sync.dma_start(
+                out=w0_raw[:, ROW * n : ROW * (n + 1)], in_=W0[PASS * n : PASS * (n + 1), :].rearrange("(m t) k -> m (t k)", t=PACK)
+            )
 
         sum_bank = take_bank("sum")
         w1q = mx_pair("w1q", G, 1)
@@ -457,9 +460,8 @@ def tile_capsuleneuralnetwork_pa_v_kernel(
             if ahead == LAST:
                 load_p()
             if behind == 1:
-                nc.sync.dma_start(
-                    out=o_dram[0:2].rearrange("g p j w -> p g (j w)"), in_=ob["pair"][:].rearrange("p (g j) w -> p g (j w)", g=2)
-                )
+                store_dp(0)
+                store_dp(1)
             if g == 0:
                 for n in range(2):
                     quantize(w0q, E4, w0_staged[n][:], PASS * n)

@@ -29,6 +29,7 @@ WRAP = -1
 RUN = 16
 X_CHUNK = 2
 LINE = 256
+Q_AT, Y_AT, W_AT = 0, 17 * 1024, 49 * 1024
 
 
 def tile_capsuleneuralnetwork_pa_v_kernel(
@@ -49,6 +50,7 @@ def tile_capsuleneuralnetwork_pa_v_kernel(
 
     with ExitStack() as ctx:
         pool = ctx.enter_context(tc.tile_pool(name="pool", bufs=1))
+        shared = ctx.enter_context(tc.tile_pool(name="shared", bufs=1))
         psum = ctx.enter_context(tc.psum_pool(name="psum", bufs=1))
 
         free_banks = list(range(8))
@@ -103,35 +105,38 @@ def tile_capsuleneuralnetwork_pa_v_kernel(
 
         ctx.enter_context(tc.manual_schedule())
 
-        q_all = pool.tile([PART, GROUPS, ROW + ROLL], BF16, name="q_all", tag="wide_q", align_bytes=LINE)
-        y_ring = pool.tile([PART, 2 * ROW], F32, name="y_ring", tag="arena", align_bytes=LINE)
-        y_t, a_t, p_t, x_t = {}, {}, {}, {}
+        q_t, y_t, a_t, p_t, x_t, w0_raw = ({} for i in range(6))
 
-        def load_q(g, count=1):
-            rows = gr_rows[g * PART : (g + count) * PART, :].rearrange("(g p) w -> p g w", p=PART)
-            nc.sync.dma_start(out=q_all[:, g : g + count, 0:ROW], in_=rows)
+        def placed(name, shape, dtype, offset):
+            return shared.tile(shape, dtype, name=name, tag=name, bufs=1, align_bytes=LINE, offset=offset)
+
+        def load_q(g):
+            q_t[g] = placed("q%d" % g, [PART, ROW + ROLL], BF16, Q_AT + 2 * (ROW + ROLL) * g)
+            nc.sync.dma_start(out=q_t[g][:, 0:ROW], in_=gr_rows[g * PART : (g + 1) * PART, :])
 
         def load_y(g, lo=0, hi=ROW):
-            y_t[g] = y_ring[:, ROW * (g % 2) : ROW * (g % 2 + 1)]
+            if lo == 0:
+                y_t[g] = placed("y%d" % g, [PART, ROW], F32, Y_AT + 4 * ROW * g)
             nc.sync.dma_start(out=y_t[g][:, lo:hi], in_=y_dram[g].rearrange("p j w -> p (j w)")[:, lo:hi])
 
-        def load_a(g):
-            a_t[g] = pool.tile([PART, ROW], F32, name="a_sb", tag="ring_a", bufs=2, align_bytes=LINE)
-            nc.sync.dma_start(out=a_t[g][:], in_=a_dram[g].rearrange("p j w -> p (j w)"))
+        def load_a(g, lo=0, hi=ROW):
+            if lo == 0:
+                a_t[g] = pool.tile([PART, ROW], F32, name="a_sb", tag="ring_a", bufs=2, align_bytes=LINE)
+            nc.sync.dma_start(out=a_t[g][:, lo:hi], in_=a_dram[g].rearrange("p j w -> p (j w)")[:, lo:hi])
 
-        def load_p():
-            p_all = pool.tile([PART, GROUPS * PACK * P_IN], BF16, name="p_all", tag="arena", align_bytes=LINE)
-            for g in range(GROUPS):
-                nc.sync.dma_start(
-                    out=p_all[:, PACK * P_IN * g : PACK * P_IN * (g + 1)], in_=p_dram[g].rearrange("p j w -> p (j w)")
-                )
-                p_t[g] = p_all[:, PACK * P_IN * g : PACK * P_IN * (g + 1)].rearrange("p (j w) -> p j w", j=PACK)
+        def load_p(g):
+            tile = placed("p%d" % g, [PART, PACK, P_IN], BF16, Y_AT + 2 * PACK * P_IN * g)
+            nc.sync.dma_start(out=tile[:], in_=p_dram[g])
+            p_t[g] = tile[:]
 
-        def load_x():
-            x_all = pool.tile([PART, GROUPS, ROW], BF16, name="x_all", align_bytes=LINE)
-            for g in range(GROUPS):
-                nc.sync.dma_start(out=x_all[:, g, :], in_=x_dram[g].rearrange("p j w -> p (j w)"))
-                x_t[g] = x_all[:, g, :].rearrange("p (j w) -> p j w", j=PACK)
+        def load_x(g):
+            tile = pool.tile([PART, PACK, F], BF16, name="x_sb", tag="x_sb", bufs=GROUPS, align_bytes=LINE)
+            nc.sync.dma_start(out=tile[:], in_=x_dram[g])
+            x_t[g] = tile[:]
+
+        def load_w0(n):
+            w0_raw[n] = placed("w0_raw%d" % n, [PART, ROW], BF16, W_AT + 2 * ROW * n)
+            nc.sync.dma_start(out=w0_raw[n][:], in_=W0[PASS * n : PASS * (n + 1), :].rearrange("(m t) k -> m (t k)", t=PACK))
 
         def stage_tile():
             return pool.tile([PART, ROW], BF16, name="stage", tag="stage", bufs=4, align_bytes=LINE)
@@ -175,8 +180,8 @@ def tile_capsuleneuralnetwork_pa_v_kernel(
         dy, dyg, dyw, dyq, dywq = ({} for i in range(5))
 
         def q_swap(g):
-            nc.tensor.matmul(out=take_bank("q", BF16)[:, 0:ROLL], lhsT=swap[:], rhs=q_all[:, g, 0:ROLL], start=True, stop=True)
-            scopy(out=q_all[:, g, ROW : ROW + ROLL], in_=bank("q")[:, 0:ROLL])
+            nc.tensor.matmul(out=take_bank("q", BF16)[:, 0:ROLL], lhsT=swap[:], rhs=q_t[g][:, 0:ROLL], start=True, stop=True)
+            scopy(out=q_t[g][:, ROW : ROW + ROLL], in_=bank("q")[:, 0:ROLL])
             give_bank("q")
 
         def dy_mask(g, s, halves=1):
@@ -185,7 +190,7 @@ def tile_capsuleneuralnetwork_pa_v_kernel(
             lo, hi = HALF * s, HALF * (s + halves)
             for u in range(2):
                 y_plane = y_t[g][:, lo:hi].rearrange("p (b u e) -> p b u e", u=2, e=RUN)[:, :, u, :]
-                q_plane = q_all[:, g, lo + ROLL : hi + ROLL].rearrange("p (b u e) -> p b u e", u=2, e=RUN)[:, :, u, :]
+                q_plane = q_t[g][:, lo + ROLL : hi + ROLL].rearrange("p (b u e) -> p b u e", u=2, e=RUN)[:, :, u, :]
                 nc.vector.scalar_tensor_tensor(
                     out=dy[g][:, HALF * u + lo // 2 : HALF * u + hi // 2].rearrange("p (b e) -> p b e", e=RUN),
                     in0=y_plane, scalar=0.0, in1=q_plane, op0=ALU.is_gt, op1=ALU.mult,
@@ -211,18 +216,19 @@ def tile_capsuleneuralnetwork_pa_v_kernel(
             dy_mask(g, s)
             dy_turn(g, s)
 
-        def dy_quantize(g):
-            dyq[g] = mx_pair("dyq", PASS, 1)
-            quantize(dyq[g], E5, dyg[g][:])
+        def dy_quantize(g, lo=0, hi=ROW):
+            if lo == 0:
+                dyq[g] = mx_pair("dyq", PASS, 1)
+            quantize(dyq[g], E5, dyg[g][:, lo:hi], lo // PACK)
 
         def dyw_quantize(g):
             dywq[g] = mx_pair("dywq", PART, 1)
             quantize(dywq[g], E5, dyw[g][:])
 
-        def dh_pass(g, j):
+        def dh_pass(g, j, wide=False):
             out = take_bank(("dh", j))
             if j == WRAP:
-                lo = 0 if g < LAST else G - ROLL
+                lo = 0 if wide else G - ROLL
                 mx_pass(out[:, lo:G], dywq[g], E5, 0, w1q, E4, lo, width=G - lo)
             else:
                 mx_pass(out, dyq[g], E5, PART * j, w1q, E4, 0)
@@ -240,7 +246,12 @@ def tile_capsuleneuralnetwork_pa_v_kernel(
             )
             give_bank(("dh", j))
 
+        summed, passes = [], {}
+
         def da_sums(g, slots):
+            if not summed:
+                take_bank("sum")
+            sum_bank = bank("sum")
             for j in slots:
                 for t in range(PACK):
                     nc.tensor.matmul(
@@ -248,9 +259,10 @@ def tile_capsuleneuralnetwork_pa_v_kernel(
                         lhsT=da[g][:, G * j + PART * t : G * j + PART * (t + 1)],
                         rhs=ident[:],
                         is_transpose=True,
-                        start=(g == 0 and j == 0 and t == 0),
-                        stop=(g == LAST and j == PACK - 1 and t == PACK - 1),
+                        start=(len(summed) == 0),
+                        stop=(len(summed) == 63),
                     )
+                    summed.append(t)
 
         def da_round(g):
             at[g] = pool.tile([PART, ROW], BF16, name="at", tag="at", bufs=1, align_bytes=LINE)
@@ -287,19 +299,20 @@ def tile_capsuleneuralnetwork_pa_v_kernel(
                 )
             give_bank("da")
 
-        def dag_quantize(g):
-            dagq[g] = mx_pair("dagq", PASS, 2)
-            quantize(dagq[g], E5, dag[g][:])
+        def dag_quantize(g, lo=0, hi=ROW):
+            if lo == 0:
+                dagq[g] = mx_pair("dagq", PASS, 2)
+            quantize(dagq[g], E5, dag[g][:, lo:hi], lo // PACK)
 
         def dp_tiles(g, tiles):
             for i in tiles:
                 j, n = divmod(i, 2)
                 mx_pass(take_bank("dp"), dagq[g], E5, PART * j, w0q, E4, PASS * n)
-                if i == 0 and g == 0:
+                if g not in ob and g < 2:
                     ob["pair"] = pool.tile([PART, 2 * PACK, P_IN], F32, name="ob_pair", align_bytes=LINE)
                     ob[0], ob[1] = ob["pair"][:, 0:PACK, :], ob["pair"][:, PACK : 2 * PACK, :]
-                if i == 0 and g >= 2:
-                    ob[g] = pool.tile([PART, PACK, P_IN], F32, name="ob", tag="wide_q" if g == LAST else "wide_2", align_bytes=LINE)
+                if g not in ob:
+                    ob[g] = placed("ob%d" % g, [PART, PACK, P_IN], F32, Q_AT if g == LAST else W_AT)
                 scopy(out=ob[g][:, j, PASS * n : PASS * (n + 1)], in_=bank("dp")[:])
                 give_bank("dp")
 
@@ -324,12 +337,22 @@ def tile_capsuleneuralnetwork_pa_v_kernel(
             quantize(inq[g, c], E4, staged[g, c][:])
 
         def dw_pass(c, r, g):
-            if g == 0:
+            done = passes.get((c, r), 0)
+            if done == 0:
                 take_bank(("dw", c, r))
-            mx_pass(bank(("dw", c, r)), inq[g, c], E4, PART * r, atq[g], E5, 0, start=(g == 0), stop=(g == (2 if c == 1 else LAST)))
+            passes[c, r] = done + 1
+            mx_pass(bank(("dw", c, r)), inq[g, c], E4, PART * r, atq[g], E5, 0, start=(done == 0), stop=(done == LAST))
+
+        def sum_reduce():
+            assert len(summed) == 64
+            nc.vector.tensor_reduce(
+                out=red[:, 0:PACK], in_=bank("sum")[:].rearrange("p (t n) -> p t n", t=PACK), axis=mybir.AxisListType.X, op=ALU.add
+            )
+            give_bank("sum")
 
         def dw_out(c, r, copy=scopy):
-            if r == 0:
+            assert passes[c, r] == GROUPS
+            if c not in wb:
                 wb[c] = pool.tile([PART, PACK, G], F32, name="wb", tag="ring_a" if c == 1 else "da", bufs=2, align_bytes=LINE)
             copy(
                 out=wb[c][:, r, :].rearrange("p (m t) -> p m t", t=PACK),
@@ -342,155 +365,215 @@ def tile_capsuleneuralnetwork_pa_v_kernel(
             nc.sync.dma_start(out=rows[:, lo:hi, :], in_=wb[c][:, lo:hi, :])
 
         vcopy(out=swap[:].rearrange("p (b h) -> p b h", h=2), in_=ident_bf[:].rearrange("p (b h) -> p b h", h=2)[:, :, ::-1])
-        w1_raw = stage_tile()
-        nc.sync.dma_start(out=w1_raw[:], in_=W1[0:G, :].rearrange("(m t) k -> m (t k)", t=PACK))
+        w1_raw = stage_tile(); nc.sync.dma_start(out=w1_raw[:], in_=W1[0:G, :].rearrange("(m t) k -> m (t k)", t=PACK))
         load_q(0)
         load_y(0, 0, HALF)
         load_y(0, HALF, ROW)
         load_q(1)
         load_y(1, 0, HALF)
         load_y(1, HALF, ROW)
-        load_a(0)
-        w0_raw = pool.tile([PART, 2 * ROW], BF16, name="w0_raw", tag="wide_2", align_bytes=LINE)
-        for n in range(2):
-            nc.sync.dma_start(
-                out=w0_raw[:, ROW * n : ROW * (n + 1)], in_=W0[PASS * n : PASS * (n + 1), :].rearrange("(m t) k -> m (t k)", t=PACK)
-            )
-
-        sum_bank = take_bank("sum")
-        w1q = mx_pair("w1q", G, 1)
-        w0q = mx_pair("w0q", P_IN, 1)
-        w1_planes = stage_tile()
-        w1_staged = stage_tile()
-
-        vcopy(
-            out=w1_planes[:].rearrange("p (u b e) -> p u b e", u=2, e=RUN),
-            in_=w1_raw[:].rearrange("p (b u e) -> p u b e", u=2, e=RUN),
-        )
-        for s in range(2):
-            weight_by_words(w1_planes[:], w1_staged, s, plane_transposes)
-        w0_staged = [stage_tile(), stage_tile()]
+        load_a(0, 0, HALF + ROLL)
+        load_a(0, HALF + ROLL, ROW)
+        load_w0(0)
+        w1q = mx_pair("w1q", G, 1); w0q = mx_pair("w0q", P_IN, 1); w1_planes = stage_tile(); w1_staged = stage_tile()
+        vcopy(out=w1_planes[:].rearrange("p (u b e) -> p u b e", u=2, e=RUN), in_=w1_raw[:].rearrange("p (b u e) -> p u b e", u=2, e=RUN))
         q_swap(0)
-        dy_half(0, 0)
+        weight_by_words(w1_planes[:], w1_staged, 0, plane_transposes)
+        weight_by_words(w1_planes[:], w1_staged, 1, plane_transposes)
+        w0_staged = [stage_tile(), stage_tile()]
+        dy_mask(0, 0)
+        dy_turn(0, 0)
+        dy_mask(0, 1)
         quantize(w1q, E4, w1_staged[:])
-        dy_half(0, 1)
+        dy_turn(0, 1)
+        dy_quantize(0, 0, HALF)
         load_q(2)
         load_y(2)
+        load_w0(1)
         load_a(1)
         q_swap(1)
+        dh_pass(0, 0)
+        dh_pass(0, 1)
         dy_mask(1, 0)
-        dy_quantize(0)
+        dy_quantize(0, HALF, ROW)
         dyw_quantize(0)
+        dh_pass(0, 2)
         dy_turn(1, 0)
-        for j in range(3):
-            dh_pass(0, j)
+        dh_pass(0, 3)
         dy_mask(1, 1)
+        dy_turn(1, 1)
+        dh_pass(0, WRAP, True)
         load_q(3)
         load_y(3)
-
-        for g in range(GROUPS):
-            behind, ahead = g - 1, g + 2
-            da_mask(g, 0)
-            dh_pass(g, 3)
-            if g == 1:
-                dag_quantize(behind)
-            da_mask(g, 1)
-            dh_pass(g, WRAP)
-            if g == 0:
-                dy_turn(1, 1)
-            if g == 1:
-                q_swap(ahead)
-            if behind >= 0:
-                da_sums(behind, (0, 1))
-                if g >= 2:
-                    interleave(1, X_CHUNK, scopy, PART * (g - 2), PART * (2 * g - 3))
-                    dag_quantize(behind)
-                dp_tiles(behind, (0, 1))
-            for j in (2, 3, WRAP):
-                da_mask(g, j)
-            if behind >= 0:
-                dp_tiles(behind, (2, 3))
-                da_sums(behind, (2, 3))
-                dp_tiles(behind, (4, 5))
-            if g == 0:
-                load_a(2)
-                load_x()
-                weight_by_matmuls(w0_raw[:, 0:ROW], w0_staged[0], 0)
-                q_swap(ahead)
-                weight_by_matmuls(w0_raw[:, 0:ROW], w0_staged[0], 1)
-                for s in range(2):
-                    weight_by_words(w0_raw[:, ROW : 2 * ROW], w0_staged[1], s)
-            if g == 1:
-                load_a(3)
-                nc.sync.dma_start(out=col_b[:], in_=col.partition_broadcast(PACK))
-            if 0 < g < LAST:
-                dyw_quantize(g + 1)
-            if g == LAST:
-                interleave(2, X_CHUNK, vcopy, 0, PASS // 2)
-            da_round(g)
-            if g < LAST:
-                dy_quantize(g + 1)
-            else:
-                interleave(2, X_CHUNK, vcopy, PASS // 2, PASS)
-            if g == 0:
-                dyw_quantize(g + 1)
-            da_turn(g, 0)
-            if g < LAST:
-                dh_pass(g + 1, 0)
-            da_turn(g, 1)
-            if g < LAST:
-                dh_pass(g + 1, 1)
-            if behind >= 0:
-                dp_tiles(behind, (6,))
-            if g == 0:
-                at_quantize(g)
-            if ahead <= LAST:
-                dy_mask(ahead, 0, 2)
-            elif g < LAST:
-                interleave(0, X_CHUNK, vcopy)
-            if behind >= 0:
-                dp_tiles(behind, (7,))
-            if g < LAST:
-                dh_pass(g + 1, 2)
-            else:
-                da_sums(g, range(PACK))
-            if ahead <= LAST:
-                for s in range(2):
-                    dy_turn(ahead, s)
-            if ahead == LAST:
-                load_p()
-            if behind == 1:
-                store_dp(0)
-                store_dp(1)
-            if g == 0:
-                for n in range(2):
-                    quantize(w0q, E4, w0_staged[n][:], PASS * n)
-            else:
-                at_quantize(g)
-            if g == LAST - 1:
-                interleave(1, X_CHUNK, vcopy, 3 * PART, PASS)
-                inp_quantize(0, X_CHUNK)
-
-        store_dp(LAST - 1)
+        da_mask(0, 0)
+        da_mask(0, 1)
+        da_mask(0, 2)
+        da_mask(0, 3)
+        da_mask(0, WRAP)
+        load_a(2)
+        load_x(0)
+        load_x(1)
+        load_x(2)
+        load_x(3)
+        weight_by_matmuls(w0_raw[0][:], w0_staged[0], 0)
+        weight_by_matmuls(w0_raw[0][:], w0_staged[0], 1)
+        q_swap(2)
+        dy_quantize(1)
+        dh_pass(1, 0)
+        dh_pass(1, 1)
+        da_sums(0, (1,))
+        da_sums(0, (0,))
+        da_round(0)
+        dyw_quantize(1)
+        da_turn(0, 0)
+        dh_pass(1, 2)
+        da_turn(0, 1)
+        weight_by_matmuls(w0_raw[1][:], w0_staged[1], 0)
+        weight_by_words(w0_raw[1][:], w0_staged[1], 1)
+        at_quantize(0)
+        quantize(w0q, E4, w0_staged[0][:], 0)
+        dy_mask(2, 0, 2)
+        dag_quantize(0)
+        da_mask(1, 0)
+        dy_turn(2, 0)
+        dh_pass(1, 3)
+        dp_tiles(0, (0,))
+        da_mask(1, 1)
+        dy_turn(2, 1)
+        dh_pass(1, WRAP, True)
+        dp_tiles(0, (2,))
+        quantize(w0q, E4, w0_staged[1][:], PASS)
+        q_swap(3)
+        dp_tiles(0, (4,))
+        da_sums(0, (2,))
+        da_sums(0, (3,))
+        dp_tiles(0, (1,))
+        da_mask(1, 2)
+        da_mask(1, 3)
+        da_mask(1, WRAP)
+        dp_tiles(0, (3,))
+        dp_tiles(0, (5,))
+        load_a(3)
+        nc.sync.dma_start(out=col_b[:], in_=col.partition_broadcast(PACK))
+        dyw_quantize(2)
+        dy_quantize(2)
+        dh_pass(2, 0)
+        dp_tiles(0, (6,))
+        da_round(1)
+        da_turn(1, 0)
+        da_turn(1, 1)
+        dh_pass(2, 1)
+        dy_mask(3, 0, 2)
+        dp_tiles(0, (7,))
+        dh_pass(2, 2)
+        dy_turn(3, 0)
+        dy_turn(3, 1)
+        load_p(0)
+        load_p(1)
+        load_p(2)
+        load_p(3)
+        at_quantize(1)
+        da_mask(2, 0)
+        dh_pass(2, 3)
+        da_mask(2, 1)
+        dh_pass(2, WRAP, True)
+        da_sums(1, (0,))
+        da_sums(1, (1,))
+        interleave(1, X_CHUNK, scopy, 0, PART)
+        dag_quantize(1)
+        dp_tiles(1, (0,))
+        dp_tiles(1, (1,))
+        da_mask(2, 2)
+        da_mask(2, 3)
+        da_mask(2, WRAP)
+        dp_tiles(1, (2,))
+        dp_tiles(1, (3,))
+        da_sums(1, (2,))
+        da_sums(1, (3,))
+        dp_tiles(1, (4,))
+        dp_tiles(1, (5,))
+        dy_quantize(3)
+        da_round(2)
+        da_turn(2, 0)
+        dh_pass(3, 0)
+        da_turn(2, 1)
+        dh_pass(3, 1)
+        dp_tiles(1, (6,))
+        interleave(0, X_CHUNK, vcopy)
+        dp_tiles(1, (7,))
+        dh_pass(3, 2)
+        store_dp(0)
+        store_dp(1)
+        dyw_quantize(3)
+        at_quantize(2)
+        interleave(1, X_CHUNK, vcopy, 3 * PART, PASS)
+        inp_quantize(0, X_CHUNK)
+        da_mask(3, 0)
+        dh_pass(3, 3)
+        da_mask(3, 1)
+        dh_pass(3, WRAP, False)
+        da_sums(2, (0,))
+        da_sums(2, (1,))
+        interleave(1, X_CHUNK, scopy, PART, 3 * PART)
+        dag_quantize(2)
+        dp_tiles(2, (0,))
+        dp_tiles(2, (1,))
+        da_mask(3, 2)
+        da_mask(3, 3)
+        da_mask(3, WRAP)
+        dp_tiles(2, (2,))
+        dp_tiles(2, (3,))
+        da_sums(2, (2,))
+        da_sums(2, (3,))
+        dp_tiles(2, (4,))
+        dp_tiles(2, (5,))
+        interleave(2, X_CHUNK, vcopy, 0, PASS // 2)
+        da_round(3)
+        interleave(2, X_CHUNK, vcopy, PASS // 2, PASS)
+        da_turn(3, 0)
+        da_turn(3, 1)
+        dp_tiles(2, (6,))
+        dp_tiles(2, (7,))
+        da_sums(3, (0,))
+        da_sums(3, (1,))
+        da_sums(3, (2,))
+        da_sums(3, (3,))
+        at_quantize(3)
+        store_dp(2)
         inp_quantize(1, X_CHUNK)
-        for g in range(2):
-            for r in range(PACK):
-                dw_pass(X_CHUNK, r, g)
+        dw_pass(X_CHUNK, 0, 0)
+        dw_pass(X_CHUNK, 1, 0)
+        dw_pass(X_CHUNK, 2, 0)
+        dw_pass(X_CHUNK, 3, 0)
+        dw_pass(X_CHUNK, 0, 1)
+        dw_pass(X_CHUNK, 1, 1)
+        dw_pass(X_CHUNK, 2, 1)
+        dw_pass(X_CHUNK, 3, 1)
         interleave(0, 0, scopy)
         inp_quantize(2, X_CHUNK)
         interleave(3, X_CHUNK, vcopy)
         dag_quantize(LAST)
-        nc.vector.tensor_reduce(
-            out=red[:, 0:PACK], in_=sum_bank[:].rearrange("p (t n) -> p t n", t=PACK), axis=mybir.AxisListType.X, op=ALU.add
-        )
-        give_bank("sum")
+        sum_reduce()
         inp_quantize(3, X_CHUNK)
         interleave(1, 0, vcopy)
-        for s in range(2):
-            for r in range(PACK):
-                dp_tiles(LAST, (PACK * s + r,))
-                dw_pass(X_CHUNK, r, 2 + s)
-            store_dp(LAST, 2 * s, 2 * s + 2)
+        dp_tiles(LAST, (0,))
+        dw_pass(X_CHUNK, 0, 2)
+        dp_tiles(LAST, (1,))
+        dw_pass(X_CHUNK, 1, 2)
+        dp_tiles(LAST, (2,))
+        dw_pass(X_CHUNK, 2, 2)
+        dp_tiles(LAST, (3,))
+        dw_pass(X_CHUNK, 3, 2)
+        store_dp(LAST, 0, 2)
+        dp_tiles(LAST, (4,))
+        dw_pass(X_CHUNK, 0, 3)
+        dp_tiles(LAST, (5,))
+        dw_pass(X_CHUNK, 1, 3)
+        dp_tiles(LAST, (6,))
+        dw_pass(X_CHUNK, 2, 3)
+        dp_tiles(LAST, (7,))
+        dw_pass(X_CHUNK, 3, 3)
+        store_dp(LAST, 2, 4)
         interleave(2, 0, vcopy)
         inp_quantize(0, 0)
         inp_quantize(1, 0)
@@ -499,33 +582,64 @@ def tile_capsuleneuralnetwork_pa_v_kernel(
         interleave(0, 1, vcopy)
         interleave(LAST, 1, vcopy, 3 * PART, PASS)
         inp_quantize(3, 0)
-        for r in range(PACK):
-            dw_pass(0, r, 0)
-            dw_out(X_CHUNK, r)
+        dw_pass(0, 0, 0)
+        dw_out(X_CHUNK, 0)
+        dw_pass(0, 1, 0)
+        dw_out(X_CHUNK, 1)
+        dw_pass(0, 2, 0)
+        dw_out(X_CHUNK, 2)
+        dw_pass(0, 3, 0)
+        dw_out(X_CHUNK, 3)
         store_dw(X_CHUNK, 0, PACK)
         interleave(LAST, 1, scopy, 0, 3 * PART)
-        for r in range(PACK):
-            dw_pass(0, r, 1)
-        for r in range(PACK):
-            dw_pass(0, r, 2)
-            dw_pass(0, r, 3)
-            dw_out(0, r)
-            if r % 2:
-                store_dw(0, r - 1, r + 1)
+        dw_pass(0, 0, 1)
+        dw_pass(0, 1, 1)
+        dw_pass(0, 2, 1)
+        dw_pass(0, 3, 1)
+        dw_pass(0, 0, 2)
+        dw_pass(0, 0, 3)
+        dw_out(0, 0)
+        dw_pass(0, 1, 2)
+        dw_pass(0, 1, 3)
+        dw_out(0, 1)
+        store_dw(0, 0, 2)
+        dw_pass(0, 2, 2)
+        dw_pass(0, 2, 3)
+        dw_out(0, 2)
+        dw_pass(0, 3, 2)
+        dw_pass(0, 3, 3)
+        dw_out(0, 3)
+        store_dw(0, 2, 4)
         interleave(1, 1, vcopy)
         inp_quantize(0, 1)
         inp_quantize(1, 1)
         interleave(2, 1, vcopy)
         inp_quantize(3, 1)
         inp_quantize(2, 1)
-        for g in range(2):
-            for r in range(PACK):
-                dw_pass(1, r, g)
-        for r in range(PACK):
-            dw_pass(1, r, 3)
-            dw_pass(1, r, 2)
-            dw_out(1, r, vcopy if r % 2 else scopy)
-            store_dw(1, r, r + 1)
+        dw_pass(1, 0, 0)
+        dw_pass(1, 1, 0)
+        dw_pass(1, 2, 0)
+        dw_pass(1, 3, 0)
+        dw_pass(1, 0, 1)
+        dw_pass(1, 1, 1)
+        dw_pass(1, 2, 1)
+        dw_pass(1, 3, 1)
+        dw_pass(1, 0, 3)
+        dw_pass(1, 1, 3)
+        dw_pass(1, 0, 2)
+        dw_out(1, 0, scopy)
+        store_dw(1, 0, 1)
+        dw_pass(1, 1, 2)
+        dw_out(1, 1, vcopy)
+        store_dw(1, 1, 2)
+        dw_pass(1, 2, 3)
+        dw_pass(1, 2, 2)
+        dw_out(1, 2, scopy)
+        store_dw(1, 2, 3)
+        dw_pass(1, 3, 3)
+        dw_pass(1, 3, 2)
+        dw_out(1, 3, vcopy)
+        store_dw(1, 3, 4)
         nc.tensor.transpose(take_bank("row")[:, 0:PART], red[:], ident[:])
         last_row = pool.tile([PACK, PART], F32, name="row")
         nc.vector.tensor_scalar(out=last_row[:], in0=bank("row")[0:PACK, 0:PART], scalar1=col_b[:], scalar2=None, op0=ALU.mult)

@@ -275,13 +275,14 @@ def tile_capsuleneuralnetwork_pa_v_kernel(
             atq[g] = mx_pair("atq", G, GROUPS)
             quantize(atq[g], E5, at[g][:])
 
-        def da_turn(g, s):
+        def da_turn(g, s, pairs=True):
             planes = at[g][:].rearrange("p (t w) -> p t w", t=PACK)
             if s == 0:
-                identity_matmuls("da", [planes[:, t, j::PACK] for j in (0, 1) for t in range(PACK)])
                 dag[g] = pool.tile([PART, ROW], BF16, name="dag", tag="dag", bufs=1, align_bytes=LINE)
+            if s == 0 or not pairs:
+                identity_matmuls("da", [planes[:, t, j::PACK] for j in (2 * s, 2 * s + 1) for t in range(PACK)])
                 scopy(
-                    out=dag[g][:, 0:HALF].rearrange("p (i r t) -> p i r t", i=2, t=PACK),
+                    out=dag[g][:, HALF * s : HALF * (s + 1)].rearrange("p (i r t) -> p i r t", i=2, t=PACK),
                     in_=bank("da")[:].rearrange("p (i t r) -> p i r t", i=2, t=PACK),
                 )
             else:
@@ -396,15 +397,15 @@ def tile_capsuleneuralnetwork_pa_v_kernel(
         dh_pass(0, 1)
         dy_mask(1, 0)
         dy_quantize(0, HALF, ROW)
-        dyw_quantize(0)
         dh_pass(0, 2)
         dy_turn(1, 0)
-        dh_pass(0, 3)
         dy_mask(1, 1)
         dy_turn(1, 1)
-        dh_pass(0, WRAP, True)
+        dh_pass(0, 3)
         load_q(3)
         load_y(3)
+        dyw_quantize(0)
+        dh_pass(0, WRAP, True)
         da_mask(0, 0)
         da_mask(0, 1)
         da_mask(0, 2)
@@ -426,16 +427,16 @@ def tile_capsuleneuralnetwork_pa_v_kernel(
         da_round(0)
         dyw_quantize(1)
         da_turn(0, 0)
-        dh_pass(1, 2)
         da_turn(0, 1)
         weight_by_matmuls(w0_raw[1][:], w0_staged[1], 0)
         weight_by_words(w0_raw[1][:], w0_staged[1], 1)
         at_quantize(0)
-        quantize(w0q, E4, w0_staged[0][:], 0)
         dy_mask(2, 0, 2)
+        quantize(w0q, E4, w0_staged[0][:], 0)
         dag_quantize(0)
         da_mask(1, 0)
         dy_turn(2, 0)
+        dh_pass(1, 2)
         dh_pass(1, 3)
         dp_tiles(0, (0,))
         da_mask(1, 1)
@@ -455,7 +456,6 @@ def tile_capsuleneuralnetwork_pa_v_kernel(
         dp_tiles(0, (5,))
         load_a(3)
         nc.sync.dma_start(out=col_b[:], in_=col.partition_broadcast(PACK))
-        dyw_quantize(2)
         dy_quantize(2)
         dh_pass(2, 0)
         dp_tiles(0, (6,))
@@ -472,6 +472,7 @@ def tile_capsuleneuralnetwork_pa_v_kernel(
         load_p(1)
         load_p(2)
         load_p(3)
+        dyw_quantize(2)
         at_quantize(1)
         da_mask(2, 0)
         dh_pass(2, 3)
@@ -549,12 +550,13 @@ def tile_capsuleneuralnetwork_pa_v_kernel(
         dw_pass(X_CHUNK, 1, 1)
         dw_pass(X_CHUNK, 2, 1)
         dw_pass(X_CHUNK, 3, 1)
-        interleave(0, 0, scopy)
+        interleave(0, 0, scopy, 0, 3 * PART)
         inp_quantize(2, X_CHUNK)
         interleave(3, X_CHUNK, vcopy)
         dag_quantize(LAST)
         sum_reduce()
         inp_quantize(3, X_CHUNK)
+        interleave(0, 0, vcopy, 3 * PART, PASS)
         interleave(1, 0, vcopy)
         dp_tiles(LAST, (0,))
         dw_pass(X_CHUNK, 0, 2)

@@ -29,6 +29,7 @@ WRAP = -1
 RUN = 16
 X_CHUNK = 2
 LINE = 256
+STORES = {0: 2, 1: 4, X_CHUNK: 1}
 Q_AT, Y_AT, W_AT = 0, 17 * 1024, 49 * 1024
 
 
@@ -328,10 +329,15 @@ def tile_capsuleneuralnetwork_pa_v_kernel(
                 staged[g, c] = pool.tile([PART, ROW], BF16, name="late_stage", tag="dy", bufs=2, align_bytes=LINE)
             if (g, c) not in staged:
                 staged[g, c] = stage_tile()
-            copy(
-                out=staged[g, c][:].rearrange("p (r m j) -> p m j r", r=PACK, j=PACK)[:, lo // PACK : hi // PACK],
-                in_=src.rearrange("p j (m r) -> p m j r", r=PACK),
-            )
+            runs = PACK // STORES[c]
+            width = 2 * PART if runs == 2 else PASS
+            for base in range(lo // width * width, hi, width):
+                first, last = max(lo, base), min(hi, base + width)
+                tiles = staged[g, c][:, PACK * base : PACK * (base + width)]
+                copy(
+                    out=tiles.rearrange("p (r m e j) -> p m j e r", r=runs, e=PACK // runs, j=PACK)[:, (first - base) // PACK : (last - base) // PACK],
+                    in_=src[:, :, first - lo : last - lo].rearrange("p j (m e r) -> p m j e r", e=PACK // runs, r=runs),
+                )
 
         def inp_quantize(g, c):
             inq[g, c] = mx_pair("inq", PASS, 2 * GROUPS)
@@ -362,8 +368,8 @@ def tile_capsuleneuralnetwork_pa_v_kernel(
             give_bank(("dw", c, r))
 
         def store_dw(c, lo, hi):
-            rows = out_1[PASS * c : PASS * (c + 1), :].rearrange("(p r) w -> p r w", r=PACK)
-            nc.sync.dma_start(out=rows[:, lo:hi, :], in_=wb[c][:, lo:hi, :])
+            rows = out_1[PASS * c + PART * lo : PASS * c + PART * hi, :].rearrange("(p r) w -> p r w", p=PART)
+            nc.sync.dma_start(out=rows, in_=wb[c][:, lo:hi, :])
 
         vcopy(out=swap[:].rearrange("p (b h) -> p b h", h=2), in_=ident_bf[:].rearrange("p (b h) -> p b h", h=2)[:, :, ::-1])
         w1_raw = stage_tile(); nc.sync.dma_start(out=w1_raw[:], in_=W1[0:G, :].rearrange("(m t) k -> m (t k)", t=PACK))

from contextlib import ExitStack

import concourse.mybir as mybir
from concourse.masks import make_identity

B, T, P_IN, F, G = 256, 8, 1024, 512, 512
N = B * T
C_IN = P_IN + F
FLOPS = 2 * N * F * G + 2 * N * G * P_IN + 2 * N * C_IN * G
BYTES = 2 * (N * P_IN + N * F + 1 + P_IN * G + G * F + N * F) + 4 * (N * G + N * F) + 4 * (N * P_IN + (C_IN + 1) * G)

F32 = mybir.dt.float32
BF16 = mybir.dt.bfloat16
U32 = mybir.dt.uint32
U8 = mybir.dt.uint8
E4 = mybir.dt.float8_e4m3fn_x4
E5 = mybir.dt.float8_e5m2_x4
ALU = mybir.AluOpType

PART = 128
PACK = 4
PASS = PART * PACK
GROUPS = N // PASS
LAST = GROUPS - 1
ROW = PACK * F
HALF = ROW // 2
ROLL = 128
WRAP = -1
RUN = 16
X_CHUNK = 2
LINE = 256
STORES = {0: 2, 1: 4, X_CHUNK: 1}
Q_AT, Y_AT, W_AT = 0, 17 * 1024, 49 * 1024


def tile_capsuleneuralnetwork_pa_v_kernel(
    tc, primary_input, prev, col, W0, b0, W1, b1, a, y, grad_out, out_0, out_1
):
    nc = tc.nc
    vcopy, scopy = nc.vector.tensor_copy, nc.scalar.copy

    def by_group(rows):
        return rows.rearrange("(g p j) w -> g p j w", p=PART, j=PACK)

    p_dram = by_group(primary_input.rearrange("b (t w) -> (b t) w", t=T))
    x_dram = by_group(prev.rearrange("b (t w) -> (b t) w", t=T))
    a_dram = by_group(a.rearrange("b t w -> (b t) w"))
    y_dram = by_group(y.rearrange("b t w -> (b t) w"))
    o_dram = by_group(out_0.rearrange("b (t w) -> (b t) w", t=T))
    gr_rows = grad_out.rearrange("b (h w) -> (b h) w", h=2)

    with ExitStack() as ctx:
        pool = ctx.enter_context(tc.tile_pool(name="pool", bufs=1))
        shared = ctx.enter_context(tc.tile_pool(name="shared", bufs=1))
        psum = ctx.enter_context(tc.psum_pool(name="psum", bufs=1))

        free_banks = list(range(8))
        filled = {}

        def take_bank(key, dtype=F32):
            k = free_banks.pop(0)
            tile = psum.tile([PART, PASS if dtype == F32 else 2 * PASS], dtype, name="bank%d" % k, tag="bank%d" % k, bufs=1)
            filled[key] = (k, tile)
            return tile

        def bank(key):
            return filled[key][1]

        def give_bank(key):
            free_banks.append(filled.pop(key)[0])

        def mx_pair(name, width, bufs):
            codes = pool.tile([PART, width], U32, name=name + "_c", tag=name + "_c", bufs=bufs, align_bytes=LINE)
            scales = pool.tile([PART, width], U8, name=name + "_s", tag=name + "_s", bufs=bufs, align_bytes=LINE)
            return codes, scales

        def quantize(pair, fmt, src, lo=0):
            width = src.shape[1] // PACK
            nc.vector.quantize_mx(out=pair[0][:, lo : lo + width].bitcast(fmt), scales=pair[1][:, lo : lo + width], in_=src)

        def mx_pass(out, lhs, lhs_fmt, m0, rhs, rhs_fmt, n0, start=True, stop=True, width=PASS):
            nc.tensor.matmul_mx(
                out=out[:, 0:width],
                lhsT=lhs[0][:, m0 : m0 + PART].bitcast(lhs_fmt),
                lhsT_scale=lhs[1][:, m0 : m0 + PART],
                rhs=rhs[0][:, n0 : n0 + width].bitcast(rhs_fmt),
                rhs_scale=rhs[1][:, n0 : n0 + width],
                start=start,
                stop=stop,
            )

        ident = pool.tile([PART, PART], F32, name="ident")
        make_identity(nc, ident[:])
        ident_bf = pool.tile([PART, PART], BF16, name="ident_bf")
        make_identity(nc, ident_bf[:])
        spread = pool.tile([PART, 2, 2 * PART], BF16, name="spread")
        nc.gpsimd.memset(spread[:], 0.0)
        nc.gpsimd.affine_select(
            out=spread[:].rearrange("p e n -> p (e n)"), in_=spread[:].rearrange("p e n -> p (e n)"), compare_op=ALU.not_equal,
            fill=1.0, base=0, pattern=[[1, 2], [-1, 2 * PART]], channel_multiplier=2,
        )
        swap = pool.tile([PART, PART], BF16, name="swap")
        col_b = pool.tile([PACK, 1], BF16, name="col_b")
        red = pool.tile([PART, PART], F32, name="red")
        nc.gpsimd.memset(red[:], 0.0)

        ctx.enter_context(tc.manual_schedule())

        q_t, y_t, a_t, p_t, x_t, w0_raw = ({} for i in range(6))

        def placed(name, shape, dtype, offset):
            return shared.tile(shape, dtype, name=name, tag=name, bufs=1, align_bytes=LINE, offset=offset)

        def load_q(g):
            q_t[g] = placed("q%d" % g, [PART, ROW + ROLL], BF16, Q_AT + 2 * (ROW + ROLL) * g)
            nc.sync.dma_start(out=q_t[g][:, 0:ROW], in_=gr_rows[g * PART : (g + 1) * PART, :])

        def load_y(g, lo=0, hi=ROW):
            if lo == 0:
                y_t[g] = placed("y%d" % g, [PART, ROW], F32, Y_AT + 4 * ROW * g)
            nc.sync.dma_start(out=y_t[g][:, lo:hi], in_=y_dram[g].rearrange("p j w -> p (j w)")[:, lo:hi])

        def load_a(g, lo=0, hi=ROW):
            if lo == 0:
                a_t[g] = pool.tile([PART, ROW], F32, name="a_sb", tag="ring_a", bufs=2, align_bytes=LINE)
            nc.sync.dma_start(out=a_t[g][:, lo:hi], in_=a_dram[g].rearrange("p j w -> p (j w)")[:, lo:hi])

        def load_p(g):
            tile = placed("p%d" % g, [PART, PACK, P_IN], BF16, Y_AT + 2 * PACK * P_IN * g)
            nc.sync.dma_start(out=tile[:], in_=p_dram[g])
            p_t[g] = tile[:]

        def load_x(g):
            tile = pool.tile([PART, PACK, F], BF16, name="x_sb", tag="x_sb", bufs=GROUPS, align_bytes=LINE)
            nc.sync.dma_start(out=tile[:], in_=x_dram[g])
            x_t[g] = tile[:]

        def load_w0(n):
            w0_raw[n] = placed("w0_raw%d" % n, [PART, ROW], BF16, W_AT + 2 * ROW * n)
            nc.sync.dma_start(out=w0_raw[n][:], in_=W0[PASS * n : PASS * (n + 1), :].rearrange("(m t) k -> m (t k)", t=PACK))

        def stage_tile():
            return pool.tile([PART, ROW], BF16, name="stage", tag="stage", bufs=4, align_bytes=LINE)

        def word_transposes(key, row, s):
            words, tp = row.bitcast(F32), take_bank(key)
            for i in range(2):
                lo = 2 * PART * (2 * s + i)
                for u in range(2):
                    nc.tensor.transpose(tp[:, (2 * i + u) * PART : (2 * i + u + 1) * PART], words[:, lo + u : lo + 2 * PART : 2], ident[:])

        def plane_transposes(key, planes, s):
            words, tp = planes.bitcast(F32), take_bank(key)
            for i in range(2):
                for u in range(2):
                    lo = PASS * u + PART * (2 * s + i)
                    nc.tensor.transpose(tp[:, (2 * i + u) * PART : (2 * i + u + 1) * PART], words[:, lo : lo + PART], ident[:])

        def identity_matmuls(key, stationaries):
            tp = take_bank(key, BF16)
            for i, lhs in enumerate(stationaries):
                nc.tensor.matmul(out=tp[:, PART * i : PART * (i + 1)], lhsT=lhs, rhs=ident_bf[:], start=True, stop=True)

        def weight_by_words(raw, staged, s, transposes=word_transposes):
            transposes("w", raw, s)
            scopy(
                out=staged[:].bitcast(F32).rearrange("p (m half w) -> p m half w", half=2, w=PACK)[:, :, s, :],
                in_=bank("w")[:].rearrange("p (w m) -> p m w", w=PACK),
            )
            give_bank("w")

        def weight_by_matmuls(raw, staged, s):
            slots = raw.rearrange("p (i k) -> p i k", i=PACK)
            identity_matmuls("w", [slots[:, i, t::PACK] for i in (2 * s, 2 * s + 1) for t in range(PACK)])
            scopy(
                out=staged[:].rearrange("p (m half w) -> p m half w", half=2, w=2 * PACK)[:, :, s, :],
                in_=bank("w")[:].rearrange("p (w m) -> p m w", w=2 * PACK),
            )
            give_bank("w")

        dy, dyg, dyw, dyq, dywq = ({} for i in range(5))

        def q_swap(g):
            nc.tensor.matmul(out=take_bank("q", BF16)[:, 0:ROLL], lhsT=swap[:], rhs=q_t[g][:, 0:ROLL], start=True, stop=True)
            scopy(out=q_t[g][:, ROW : ROW + ROLL], in_=bank("q")[:, 0:ROLL])
            give_bank("q")

        def dy_mask(g, s, halves=1):
            if s == 0:
                dy[g] = pool.tile([PART, ROW], BF16, name="dy", tag="dy", bufs=2, align_bytes=LINE)
            lo, hi = HALF * s, HALF * (s + halves)
            for u in range(2):
                y_plane = y_t[g][:, lo:hi].rearrange("p (b u e) -> p b u e", u=2, e=RUN)[:, :, u, :]
                q_plane = q_t[g][:, lo + ROLL : hi + ROLL].rearrange("p (b u e) -> p b u e", u=2, e=RUN)[:, :, u, :]
                nc.vector.scalar_tensor_tensor(
                    out=dy[g][:, HALF * u + lo // 2 : HALF * u + hi // 2].rearrange("p (b e) -> p b e", e=RUN),
                    in0=y_plane, scalar=0.0, in1=q_plane, op0=ALU.is_gt, op1=ALU.mult,
                )

        def dy_turn(g, s):
            plane_transposes("dy", dy[g][:], s)
            if s == 0:
                dyg[g] = pool.tile([PART, ROW], BF16, name="dyg", tag="dyg", bufs=1, align_bytes=LINE)
            scopy(
                out=dyg[g][:].bitcast(F32)[:, PASS * s : PASS * (s + 1)].rearrange("p (i r u) -> p i r u", i=2, u=2),
                in_=bank("dy")[:].rearrange("p (i u r) -> p i r u", i=2, u=2),
            )
            if s == 1:
                dyw[g] = pool.tile([PART, PASS], BF16, name="dyw", tag="dyw", bufs=1, align_bytes=LINE)
                scopy(
                    out=dyw[g][:].bitcast(F32).rearrange("p (b h u) -> p b h u", h=2, u=2),
                    in_=bank("dy")[:, 2 * PART : PASS].rearrange("p (u b h) -> p b h u", u=2, h=2)[:, :, ::-1, :],
                )
            give_bank("dy")

        def dy_half(g, s):
            dy_mask(g, s)
            dy_turn(g, s)

        def dy_quantize(g, lo=0, hi=ROW):
            if lo == 0:
                dyq[g] = mx_pair("dyq", PASS, 1)
            quantize(dyq[g], E5, dyg[g][:, lo:hi], lo // PACK)

        def dyw_quantize(g):
            dywq[g] = mx_pair("dywq", PART, 1)
            quantize(dywq[g], E5, dyw[g][:])

        def dh_pass(g, j, wide=False):
            out = take_bank(("dh", j))
            if j == WRAP:
                lo = 0 if wide else G - ROLL
                mx_pass(out[:, lo:G], dywq[g], E5, 0, w1q, E4, lo, width=G - lo)
            else:
                mx_pass(out, dyq[g], E5, PART * j, w1q, E4, 0)

        da, at, atq, dag, dagq, ob = ({} for i in range(6))

        def da_mask(g, j):
            if j == 0:
                da[g] = pool.tile([PART, ROW], F32, name="da", tag="da", bufs=2, align_bytes=LINE)
            lo, hi = max(0, G * j + ROLL), min(ROW, G * (j + 1) + ROLL)
            src = lo - (G * j + ROLL)
            nc.vector.scalar_tensor_tensor(
                out=da[g][:, lo:hi], in0=a_t[g][:, lo:hi], scalar=0.0, in1=bank(("dh", j))[:, src : src + hi - lo],
                op0=ALU.is_gt, op1=ALU.mult,
            )
            give_bank(("dh", j))

        summed, passes = [], {}

        def da_sums(g, slots):
            if not summed:
                take_bank("sum")
            sum_bank = bank("sum")
            for j in slots:
                for t in range(PACK):
                    nc.tensor.matmul(
                        out=sum_bank[:, PART * t : PART * (t + 1)],
                        lhsT=da[g][:, G * j + PART * t : G * j + PART * (t + 1)],
                        rhs=ident[:],
                        is_transpose=True,
                        start=(len(summed) == 0),
                        stop=(len(summed) == 63),
                    )
                    summed.append(t)

        def da_round(g):
            at[g] = pool.tile([PART, ROW], BF16, name="at", tag="at", bufs=1, align_bytes=LINE)
            vcopy(
                out=at[g][:].rearrange("p (t m j) -> p m j t", t=PACK, j=PACK),
                in_=da[g][:].rearrange("p (j m t) -> p m j t", j=PACK, t=PACK),
            )

        def at_quantize(g):
            atq[g] = mx_pair("atq", G, GROUPS)
            quantize(atq[g], E5, at[g][:])

        def da_turn(g, s, pairs=True):
            planes = at[g][:].rearrange("p (t w) -> p t w", t=PACK)
            if s == 0:
                dag[g] = pool.tile([PART, ROW], BF16, name="dag", tag="dag", bufs=1, align_bytes=LINE)
            if s == 0 or not pairs:
                identity_matmuls("da", [planes[:, t, j::PACK] for j in (2 * s, 2 * s + 1) for t in range(PACK)])
                scopy(
                    out=dag[g][:, HALF * s : HALF * (s + 1)].rearrange("p (i r t) -> p i r t", i=2, t=PACK),
                    in_=bank("da")[:].rearrange("p (i t r) -> p i r t", i=2, t=PACK),
                )
            else:
                tp = take_bank("da", BF16)
                for i in range(2):
                    for t in range(PACK):
                        lo = 2 * PART * (2 * i + t // 2)
                        nc.tensor.matmul(
                            out=tp[:, lo : lo + 2 * PART], lhsT=planes[:, t, 2 + i :: PACK], rhs=spread[:, t % 2, :],
                            start=(t % 2 == 0), stop=(t % 2 == 1),
                        )
                scopy(
                    out=dag[g][:].bitcast(F32)[:, PASS : 2 * PASS].rearrange("p (i r u) -> p i r u", i=2, u=2),
                    in_=tp[:].bitcast(F32).rearrange("p (i u r) -> p i r u", i=2, u=2),
                )
            give_bank("da")

        def dag_quantize(g, lo=0, hi=ROW):
            if lo == 0:
                dagq[g] = mx_pair("dagq", PASS, 2)
            quantize(dagq[g], E5, dag[g][:, lo:hi], lo // PACK)

        def dp_tiles(g, tiles):
            for i in tiles:
                j, n = divmod(i, 2)
                mx_pass(take_bank("dp"), dagq[g], E5, PART * j, w0q, E4, PASS * n)
                if g not in ob and g < 2:
                    ob["pair"] = pool.tile([PART, 2 * PACK, P_IN], F32, name="ob_pair", align_bytes=LINE)
                    ob[0], ob[1] = ob["pair"][:, 0:PACK, :], ob["pair"][:, PACK : 2 * PACK, :]
                if g not in ob:
                    ob[g] = placed("ob%d" % g, [PART, PACK, P_IN], F32, Q_AT if g == LAST else W_AT)
                scopy(out=ob[g][:, j, PASS * n : PASS * (n + 1)], in_=bank("dp")[:])
                give_bank("dp")

        def store_dp(g, lo=0, hi=PACK):
            nc.sync.dma_start(out=o_dram[g][:, lo:hi, :], in_=ob[g][:, lo:hi, :])

        staged, inq, wb = {}, {}, {}

        def interleave(g, c, copy, lo=0, hi=PASS):
            src = x_t[g][:, :, lo:hi] if c == X_CHUNK else p_t[g][:, :, PASS * c + lo : PASS * c + hi]
            if (g, c) not in staged and (g, c) in ((0, 0), (LAST, 1)):
                staged[g, c] = pool.tile([PART, ROW], BF16, name="late_stage", tag="dy", bufs=2, align_bytes=LINE)
            if (g, c) not in staged:
                staged[g, c] = stage_tile()
            runs = PACK // STORES[c]
            width = 2 * PART if runs == 2 else PASS
            for base in range(lo // width * width, hi, width):
                first, last = max(lo, base), min(hi, base + width)
                tiles = staged[g, c][:, PACK * base : PACK * (base + width)]
                copy(
                    out=tiles.rearrange("p (r m e j) -> p m j e r", r=runs, e=PACK // runs, j=PACK)[:, (first - base) // PACK : (last - base) // PACK],
                    in_=src[:, :, first - lo : last - lo].rearrange("p j (m e r) -> p m j e r", e=PACK // runs, r=runs),
                )

        def inp_quantize(g, c):
            inq[g, c] = mx_pair("inq", PASS, 2 * GROUPS)
            quantize(inq[g, c], E4, staged[g, c][:])

        def dw_pass(c, r, g):
            done = passes.get((c, r), 0)
            if done == 0:
                take_bank(("dw", c, r))
            passes[c, r] = done + 1
            mx_pass(bank(("dw", c, r)), inq[g, c], E4, PART * r, atq[g], E5, 0, start=(done == 0), stop=(done == LAST))

        def sum_reduce():
            assert len(summed) == 64
            nc.vector.tensor_reduce(
                out=red[:, 0:PACK], in_=bank("sum")[:].rearrange("p (t n) -> p t n", t=PACK), axis=mybir.AxisListType.X, op=ALU.add
            )
            give_bank("sum")

        def dw_out(c, r, copy=scopy):
            assert passes[c, r] == GROUPS
            if c not in wb:
                wb[c] = pool.tile([PART, PACK, G], F32, name="wb", tag="ring_a" if c == 1 else "da", bufs=2, align_bytes=LINE)
            copy(
                out=wb[c][:, r, :].rearrange("p (m t) -> p m t", t=PACK),
                in_=bank(("dw", c, r))[:].rearrange("p (t m) -> p m t", t=PACK),
            )
            give_bank(("dw", c, r))

        def store_dw(c, lo, hi):
            rows = out_1[PASS * c + PART * lo : PASS * c + PART * hi, :].rearrange("(p r) w -> p r w", p=PART)
            nc.sync.dma_start(out=rows, in_=wb[c][:, lo:hi, :])

        vcopy(out=swap[:].rearrange("p (b h) -> p b h", h=2), in_=ident_bf[:].rearrange("p (b h) -> p b h", h=2)[:, :, ::-1])
        w1_raw = stage_tile(); nc.sync.dma_start(out=w1_raw[:], in_=W1[0:G, :].rearrange("(m t) k -> m (t k)", t=PACK))
        load_q(0)
        load_y(0, 0, HALF)
        load_y(0, HALF, ROW)
        load_q(1)
        load_y(1, 0, HALF)
        load_y(1, HALF, ROW)
        load_a(0, 0, HALF + ROLL)
        load_a(0, HALF + ROLL, ROW)
        load_w0(0)
        w1q = mx_pair("w1q", G, 1); w0q = mx_pair("w0q", P_IN, 1); w1_planes = stage_tile(); w1_staged = stage_tile()
        vcopy(out=w1_planes[:].rearrange("p (u b e) -> p u b e", u=2, e=RUN), in_=w1_raw[:].rearrange("p (b u e) -> p u b e", u=2, e=RUN))
        q_swap(0)
        weight_by_words(w1_planes[:], w1_staged, 0, plane_transposes)
        weight_by_words(w1_planes[:], w1_staged, 1, plane_transposes)
        w0_staged = [stage_tile(), stage_tile()]
        dy_mask(0, 0)
        dy_turn(0, 0)
        dy_mask(0, 1)
        quantize(w1q, E4, w1_staged[:])
        dy_turn(0, 1)
        dy_quantize(0, 0, HALF)
        load_q(2)
        load_y(2)
        load_w0(1)
        load_a(1)
        q_swap(1)
        dh_pass(0, 0)
        dh_pass(0, 1)
        dy_mask(1, 0)
        dy_quantize(0, HALF, ROW)
        dh_pass(0, 2)
        dy_turn(1, 0)
        dy_mask(1, 1)
        dy_turn(1, 1)
        dh_pass(0, 3)
        load_q(3)
        load_y(3)
        dyw_quantize(0)
        dh_pass(0, WRAP, True)
        da_mask(0, 0)
        da_mask(0, 1)
        da_mask(0, 2)
        da_mask(0, 3)
        da_mask(0, WRAP)
        load_a(2)
        load_x(0)
        load_x(1)
        load_x(2)
        load_x(3)
        weight_by_matmuls(w0_raw[0][:], w0_staged[0], 0)
        weight_by_matmuls(w0_raw[0][:], w0_staged[0], 1)
        q_swap(2)
        dy_quantize(1)
        dh_pass(1, 0)
        dh_pass(1, 1)
        da_sums(0, (1,))
        da_sums(0, (0,))
        da_round(0)
        dyw_quantize(1)
        da_turn(0, 0)
        da_turn(0, 1)
        weight_by_matmuls(w0_raw[1][:], w0_staged[1], 0)
        weight_by_words(w0_raw[1][:], w0_staged[1], 1)
        at_quantize(0)
        dy_mask(2, 0, 2)
        quantize(w0q, E4, w0_staged[0][:], 0)
        dag_quantize(0)
        da_mask(1, 0)
        dy_turn(2, 0)
        dh_pass(1, 2)
        dh_pass(1, 3)
        dp_tiles(0, (0,))
        da_mask(1, 1)
        dy_turn(2, 1)
        dh_pass(1, WRAP, True)
        dp_tiles(0, (2,))
        quantize(w0q, E4, w0_staged[1][:], PASS)
        q_swap(3)
        dp_tiles(0, (4,))
        da_sums(0, (2,))
        da_sums(0, (3,))
        dp_tiles(0, (1,))
        da_mask(1, 2)
        da_mask(1, 3)
        da_mask(1, WRAP)
        dp_tiles(0, (3,))
        dp_tiles(0, (5,))
        load_a(3)
        nc.sync.dma_start(out=col_b[:], in_=col.partition_broadcast(PACK))
        dy_quantize(2)
        dh_pass(2, 0)
        dp_tiles(0, (6,))
        da_round(1)
        da_turn(1, 0)
        da_turn(1, 1)
        dh_pass(2, 1)
        dy_mask(3, 0, 2)
        dp_tiles(0, (7,))
        dh_pass(2, 2)
        dy_turn(3, 0)
        dy_turn(3, 1)
        load_p(0)
        load_p(1)
        load_p(2)
        load_p(3)
        dyw_quantize(2)
        at_quantize(1)
        da_mask(2, 0)
        dh_pass(2, 3)
        da_mask(2, 1)
        dh_pass(2, WRAP, True)
        da_sums(1, (0,))
        da_sums(1, (1,))
        interleave(1, X_CHUNK, scopy, 0, PART)
        dag_quantize(1)
        dp_tiles(1, (0,))
        dp_tiles(1, (1,))
        da_mask(2, 2)
        da_mask(2, 3)
        da_mask(2, WRAP)
        dp_tiles(1, (2,))
        dp_tiles(1, (3,))
        da_sums(1, (2,))
        da_sums(1, (3,))
        dp_tiles(1, (4,))
        dp_tiles(1, (5,))
        dy_quantize(3)
        da_round(2)
        da_turn(2, 0)
        dh_pass(3, 0)
        da_turn(2, 1)
        dh_pass(3, 1)
        dp_tiles(1, (6,))
        interleave(0, X_CHUNK, vcopy)
        dp_tiles(1, (7,))
        dh_pass(3, 2)
        store_dp(0)
        store_dp(1)
        dyw_quantize(3)
        at_quantize(2)
        interleave(1, X_CHUNK, vcopy, 3 * PART, PASS)
        inp_quantize(0, X_CHUNK)
        da_mask(3, 0)
        dh_pass(3, 3)
        da_mask(3, 1)
        dh_pass(3, WRAP, False)
        da_sums(2, (0,))
        da_sums(2, (1,))
        interleave(1, X_CHUNK, scopy, PART, 3 * PART)
        dag_quantize(2)
        dp_tiles(2, (0,))
        dp_tiles(2, (1,))
        da_mask(3, 2)
        da_mask(3, 3)
        da_mask(3, WRAP)
        dp_tiles(2, (2,))
        dp_tiles(2, (3,))
        da_sums(2, (2,))
        da_sums(2, (3,))
        dp_tiles(2, (4,))
        dp_tiles(2, (5,))
        interleave(2, X_CHUNK, vcopy, 0, PASS // 2)
        da_round(3)
        interleave(2, X_CHUNK, vcopy, PASS // 2, PASS)
        da_turn(3, 0)
        da_turn(3, 1)
        dp_tiles(2, (6,))
        dp_tiles(2, (7,))
        da_sums(3, (0,))
        da_sums(3, (1,))
        da_sums(3, (2,))
        da_sums(3, (3,))
        at_quantize(3)
        store_dp(2)
        inp_quantize(1, X_CHUNK)
        dw_pass(X_CHUNK, 0, 0)
        dw_pass(X_CHUNK, 1, 0)
        dw_pass(X_CHUNK, 2, 0)
        dw_pass(X_CHUNK, 3, 0)
        dw_pass(X_CHUNK, 0, 1)
        dw_pass(X_CHUNK, 1, 1)
        dw_pass(X_CHUNK, 2, 1)
        dw_pass(X_CHUNK, 3, 1)
        interleave(0, 0, scopy, 0, 3 * PART)
        inp_quantize(2, X_CHUNK)
        interleave(3, X_CHUNK, vcopy)
        dag_quantize(LAST)
        sum_reduce()
        inp_quantize(3, X_CHUNK)
        interleave(0, 0, vcopy, 3 * PART, PASS)
        interleave(1, 0, vcopy)
        dp_tiles(LAST, (0,))
        dw_pass(X_CHUNK, 0, 2)
        dp_tiles(LAST, (1,))
        dw_pass(X_CHUNK, 1, 2)
        dp_tiles(LAST, (2,))
        dw_pass(X_CHUNK, 2, 2)
        dp_tiles(LAST, (3,))
        dw_pass(X_CHUNK, 3, 2)
        store_dp(LAST, 0, 2)
        dp_tiles(LAST, (4,))
        dw_pass(X_CHUNK, 0, 3)
        dp_tiles(LAST, (5,))
        dw_pass(X_CHUNK, 1, 3)
        dp_tiles(LAST, (6,))
        dw_pass(X_CHUNK, 2, 3)
        dp_tiles(LAST, (7,))
        dw_pass(X_CHUNK, 3, 3)
        store_dp(LAST, 2, 4)
        interleave(2, 0, vcopy)
        inp_quantize(0, 0)
        inp_quantize(1, 0)
        interleave(3, 0, vcopy)
        inp_quantize(2, 0)
        interleave(0, 1, vcopy)
        interleave(LAST, 1, vcopy, 3 * PART, PASS)
        inp_quantize(3, 0)
        dw_pass(0, 0, 0)
        dw_out(X_CHUNK, 0)
        dw_pass(0, 1, 0)
        dw_out(X_CHUNK, 1)
        dw_pass(0, 2, 0)
        dw_out(X_CHUNK, 2)
        dw_pass(0, 3, 0)
        dw_out(X_CHUNK, 3)
        store_dw(X_CHUNK, 0, PACK)
        interleave(LAST, 1, scopy, 0, 3 * PART)
        dw_pass(0, 0, 1)
        dw_pass(0, 1, 1)
        dw_pass(0, 2, 1)
        dw_pass(0, 3, 1)
        dw_pass(0, 0, 2)
        dw_pass(0, 0, 3)
        dw_out(0, 0)
        dw_pass(0, 1, 2)
        dw_pass(0, 1, 3)
        dw_out(0, 1)
        store_dw(0, 0, 2)
        dw_pass(0, 2, 2)
        dw_pass(0, 2, 3)
        dw_out(0, 2)
        dw_pass(0, 3, 2)
        dw_pass(0, 3, 3)
        dw_out(0, 3)
        store_dw(0, 2, 4)
        interleave(1, 1, vcopy)
        inp_quantize(0, 1)
        inp_quantize(1, 1)
        interleave(2, 1, vcopy)
        inp_quantize(3, 1)
        inp_quantize(2, 1)
        dw_pass(1, 0, 0)
        dw_pass(1, 1, 0)
        dw_pass(1, 2, 0)
        dw_pass(1, 3, 0)
        dw_pass(1, 0, 1)
        dw_pass(1, 1, 1)
        dw_pass(1, 2, 1)
        dw_pass(1, 3, 1)
        dw_pass(1, 0, 3)
        dw_pass(1, 1, 3)
        dw_pass(1, 0, 2)
        dw_out(1, 0, scopy)
        store_dw(1, 0, 1)
        dw_pass(1, 1, 2)
        dw_out(1, 1, vcopy)
        store_dw(1, 1, 2)
        dw_pass(1, 2, 3)
        dw_pass(1, 2, 2)
        dw_out(1, 2, scopy)
        store_dw(1, 2, 3)
        dw_pass(1, 3, 3)
        dw_pass(1, 3, 2)
        dw_out(1, 3, vcopy)
        store_dw(1, 3, 4)
        nc.tensor.transpose(take_bank("row")[:, 0:PART], red[:], ident[:])
        last_row = pool.tile([PACK, PART], F32, name="row")
        nc.vector.tensor_scalar(out=last_row[:], in0=bank("row")[0:PACK, 0:PART], scalar1=col_b[:], scalar2=None, op0=ALU.mult)
        give_bank("row")
        nc.sync.dma_start(out=out_1[C_IN : C_IN + 1, :].rearrange("o (t m) -> (o t) m", t=PACK), in_=last_row[:])
